import numpy as np
import ml_dtypes


def mxq(x, axis, fmt="e4m3"):
    dtype, down = {"e4m3": (ml_dtypes.float8_e4m3fn, 7), "e5m2": (ml_dtypes.float8_e5m2, 14)}[fmt]
    v = np.moveaxis(np.asarray(x, np.float32).astype(ml_dtypes.bfloat16).astype(np.float64), axis, -1)
    blocks = v.reshape(v.shape[:-1] + (-1, 32))
    amax = np.abs(blocks).max(-1, keepdims=True)
    byte = np.maximum(np.where(amax > 0, np.frexp(amax)[1] - 1 + 127, 0) - down, 1)
    scale = np.exp2(byte - 127.0)
    codes = (blocks / scale).astype(np.float32).astype(dtype).astype(np.float64)
    return np.moveaxis((codes * scale).reshape(v.shape), -1, axis)


WIDE = False


def mx_kscale(k):
    if not WIDE:
        return np.ones(k)
    levels = np.array([10, -10, 5, -5, 0])
    a = np.random.permutation(np.resize(levels, k // 512 * 4)).reshape(k // 512, 4)
    idx = np.arange(k)
    return np.exp2(a[idx // 512, idx % 128 // 32])


BF16 = ml_dtypes.bfloat16


def bf(x):
    return np.asarray(x, np.float32).astype(BF16)


def f64(x):
    return np.asarray(x).astype(np.float64)


E2M1 = np.array([0.0, 0.5, 1.0, 1.5, 2.0, 3.0, 4.0, 6.0, -0.0, -0.5, -1.0, -1.5, -2.0, -3.0, -4.0, -6.0])


def pack_weight(w, fmt):
    k, n = w.shape
    w = f64(bf(w)).reshape(k // 32, 32, n)
    amax = np.abs(w).max(1)
    if fmt == "e4m3":
        byte = np.frexp(amax)[1] - 1 + 127 - 7
    else:
        mant, ex = np.frexp(amax / 6.0)
        byte = np.where(mant > 0.5, ex, ex - 1) + 127
    byte = np.clip(np.where(amax > 0, byte, 1), 1, 254)
    scaled = (w * np.exp2(127.0 - byte)[:, None, :]).reshape(k, n).astype(np.float32)
    by_word = np.ascontiguousarray(scaled.reshape(k // 512, 128, 4, n).transpose(0, 1, 3, 2))
    if fmt == "e4m3":
        words = by_word.astype(ml_dtypes.float8_e4m3fn).view(np.uint8)
    else:
        c = by_word.astype(ml_dtypes.float4_e2m1fn).view(np.uint8) & 0xF
        words = c[..., 0::2] | (c[..., 1::2] << 4)
    return np.ascontiguousarray(words), np.ascontiguousarray(byte.astype(np.uint8).reshape(k // 512, 16, n))


def unpack_weight(words, scales, fmt):
    g, p, n, _ = words.shape
    if fmt == "e4m3":
        vals = np.ascontiguousarray(words).view(ml_dtypes.float8_e4m3fn).astype(np.float64)
    else:
        nib = np.empty((g, p, n, 4), np.uint8)
        nib[..., 0::2] = words & 0xF
        nib[..., 1::2] = words >> 4
        vals = E2M1[nib]
    vals = vals * np.repeat(np.exp2(scales.astype(np.float64) - 127.0), 8, axis=1)[..., None]
    return vals.transpose(0, 1, 3, 2).reshape(g * 512, n)


N, C, D, H, W, NHEADS, KSIZE = 2, 512, 256, 32, 32, 8, 5
PAD = KSIZE // 2
HD = D // NHEADS
WIN = KSIZE * KSIZE
FMT = "e4m3"


def _patches(t):
    tp = np.pad(t, ((0, 0), (0, 0), (PAD, PAD), (PAD, PAD)))
    return np.stack([tp[:, :, i:i + H, j:j + W] for i in range(KSIZE) for j in range(KSIZE)], axis=2)


def setup_inputs():
    s = mx_kscale(C)
    a = np.sqrt(1.5) / HD ** 0.25
    g = np.concatenate([np.full(2 * D, a), np.ones(D)])
    x = bf(np.random.standard_normal((N, C, H, W)) * s[None, :, None, None])
    w = np.random.standard_normal((3 * D, C)) * g[:, None] / np.sqrt(C) / s[None, :]
    words, scales = pack_weight(np.ascontiguousarray(w.T), FMT)
    return {"x": x, "w_qkv_words": words, "w_qkv_scales": scales}


def reference(x, w_qkv_words, w_qkv_scales):
    xq = mxq(f64(x).reshape(N, C, H * W), 1, "e4m3")
    wq = unpack_weight(w_qkv_words, w_qkv_scales, FMT).T
    qkv = (wq @ xq).reshape(N, 3 * D, H, W)
    Q, K, V = np.split(qkv, 3, axis=1)
    Qh = Q.reshape(N, NHEADS, HD, 1, H, W)
    scores = np.sum(_patches(K).reshape(N, NHEADS, HD, WIN, H, W) * Qh, axis=2, keepdims=True)
    e = np.exp(scores - scores.max(axis=3, keepdims=True))
    att = e / e.sum(axis=3, keepdims=True)
    out = np.sum(_patches(V).reshape(N, NHEADS, HD, WIN, H, W) * att, axis=3).reshape(N, D, H, W)
    return out

@@ -1,0 +1,281 @@
+from contextlib import ExitStack
+
+import concourse.mybir as mybir
+from concourse.masks import make_identity
+
+F32 = mybir.dt.float32
+BF16 = mybir.dt.bfloat16
+I32 = mybir.dt.int32
+U32 = mybir.dt.uint32
+U8 = mybir.dt.uint8
+FP8X4 = mybir.dt.float8_e4m3fn_x4
+ALU = mybir.AluOpType
+ACT = mybir.ActivationFunctionType
+AX = mybir.AxisListType
+
+P = 128
+PACK = 4
+IMAGES, CHANNELS_IN, SIDE = 2, 512, 32
+PIXELS = IMAGES * SIDE * SIDE
+HEADS, HEAD_DIM = 8, 32
+DEPTH = HEADS * HEAD_DIM
+HALVES = DEPTH // P
+HEADS_HALF = HEADS // HALVES
+WINDOW = 5
+OFFSETS = WINDOW * WINDOW
+PATCH = 4
+SPOTS = PATCH * PATCH
+GRID = SIDE // PATCH
+HALO = PATCH + WINDOW - 1
+MARGIN = 16
+ROW = P + 2 * MARGIN
+QUERIES = SPOTS * HEADS
+
+FLOPS = 2 * 3 * DEPTH * CHANNELS_IN * PIXELS + 2 * 2 * PIXELS * HEADS * OFFSETS * HEAD_DIM
+
+
+def halo_place(u):
+    step = (u - 2) // PATCH
+    border = 0 if u < 2 else (2 if u >= HALO - 2 else 1)
+    return step, (u - 2) - PATCH * step, border
+
+
+def tile_relation_kernel(tc, x, w_qkv_words, w_qkv_scales, out):
+    nc = tc.nc
+    with ExitStack() as whole:
+        const = whole.enter_context(tc.tile_pool(name="const", bufs=1))
+        keep = whole.enter_context(tc.tile_pool(name="keep", bufs=1))
+        stage_ps = whole.enter_context(tc.psum_pool(name="stage_ps", bufs=3))
+
+        ident = const.tile([P, P], F32)
+        make_identity(nc, ident[:])
+
+        by_patch = ident[:].rearrange("p (n y x) -> p n y x", n=IMAGES, y=GRID, x=GRID)
+        at_border = const.tile([P, 2, 2], F32)
+        nc.vector.tensor_reduce(out=at_border[:, 0, 0:1], in_=by_patch[:, :, 0, :], axis=AX.XY, op=ALU.add)
+        nc.vector.tensor_reduce(out=at_border[:, 0, 1:2], in_=by_patch[:, :, GRID - 1, :], axis=AX.XY, op=ALU.add)
+        nc.vector.tensor_reduce(out=at_border[:, 1, 0:1], in_=by_patch[:, :, :, 0], axis=AX.XY, op=ALU.add)
+        nc.vector.tensor_reduce(out=at_border[:, 1, 1:2], in_=by_patch[:, :, :, GRID - 1], axis=AX.XY, op=ALU.add)
+        one_way = const.tile([P, 2, 3], F32)
+        nc.vector.memset(one_way[:], 1.0)
+        nc.vector.tensor_scalar(
+            out=one_way[:, :, 0:3:2], in0=at_border[:], scalar1=-1.0, scalar2=1.0, op0=ALU.mult, op1=ALU.add
+        )
+        inside = const.tile([P, 3, 3], F32)
+        nc.vector.tensor_tensor(
+            out=inside[:],
+            in0=one_way[:, 0, :].unsqueeze(2).to_broadcast([P, 3, 3]),
+            in1=one_way[:, 1, :].unsqueeze(1).to_broadcast([P, 3, 3]),
+            op=ALU.mult,
+        )
+
+        by_channel = [None] * 6
+        for m in (4, 5):
+            by_channel[m] = keep.tile([P, SPOTS, ROW], F32, name="by_channel%d" % m)
+        k_halo = keep.tile([P, HEAD_DIM, HALO, HALO, HEADS], F32, tag="halo")
+        q_patch = keep.tile([P, HEAD_DIM, PATCH, PATCH, HEADS], F32)
+        scores = keep.tile([P, OFFSETS, P], F32)
+
+        def to_patches(source, u, v, bank_part):
+            step_y, ry = halo_place(u)[0:2]
+            step_x, rx = halo_place(v)[0:2]
+            first = MARGIN + GRID * step_y + step_x
+            nc.tensor.transpose(out=bank_part, in_=source[:, ry * PATCH + rx, first : first + P], identity=ident[:])
+
+        def leave_psum(turn, out_ap, in_ap, factor):
+            if turn % 2 == 0:
+                nc.scalar.activation(out=out_ap, in_=in_ap, func=ACT.Copy, scale=factor)
+            else:
+                nc.vector.tensor_scalar(out=out_ap, in0=in_ap, scalar1=factor, scalar2=None, op0=ALU.mult)
+
+        with tc.tile_pool(name="chan_qk", bufs=1) as chan_qk:
+            for m in range(4):
+                by_channel[m] = chan_qk.tile([P, SPOTS, ROW], F32, name="by_channel%d" % m)
+            for m in range(2, 6):
+                nc.gpsimd.memset(by_channel[m][:, :, 0:MARGIN], 0.0)
+                nc.gpsimd.memset(by_channel[m][:, :, MARGIN + P : ROW], 0.0)
+
+            with tc.tile_pool(name="front", bufs=1) as front, tc.tile_pool(name="group", bufs=2) as group, tc.psum_pool(
+                name="acc_ps", bufs=2
+            ) as acc_ps:
+                w_words = front.tile([P, 3 * DEPTH], U32, align_bytes=64)
+                w_scales = front.tile([P, 3 * DEPTH], U8, align_bytes=64)
+                nc.vector.memset(w_scales[:].bitcast(I32), 0)
+                nc.sync.dma_start(
+                    out=w_words[:].bitcast(I32), in_=w_qkv_words[0].rearrange("p n t -> p (n t)").bitcast(I32)
+                )
+                for quad in range(4):
+                    nc.sync.dma_start(
+                        out=w_scales[32 * quad : 32 * quad + 4, :].bitcast(I32),
+                        in_=w_qkv_scales[0, 4 * quad : 4 * quad + 4, :].bitcast(I32),
+                    )
+                x_sb = front.tile([P, PACK, PIXELS], BF16)
+                per_image = SIDE * SIDE
+                for n in range(IMAGES):
+                    nc.scalar.dma_start(
+                        out=x_sb[:, :, n * per_image : (n + 1) * per_image],
+                        in_=x[n].rearrange("(p t) h w -> p t (h w)", t=PACK),
+                    )
+                x_words = front.tile([P, PIXELS], U32, align_bytes=64)
+                x_scales = front.tile([P, PIXELS], U8, align_bytes=64)
+                x_by_spot = x_sb[:].rearrange(
+                    "p t (g ry qx rx) -> p ry rx g qx t", g=IMAGES * GRID, ry=PATCH, qx=GRID, rx=PATCH
+                )
+                for ry in range(PATCH):
+                    cols = slice(ry * PATCH * P, (ry + 1) * PATCH * P)
+                    grouped = group.tile([P, PATCH, P, PACK], BF16, align_bytes=64)
+                    nc.vector.tensor_copy(
+                        out=grouped[:].rearrange("p rx (g qx) t -> p rx g qx t", qx=GRID), in_=x_by_spot[:, ry]
+                    )
+                    nc.vector.quantize_mx(
+                        out=x_words[:, cols].bitcast(FP8X4),
+                        scales=x_scales[:, cols],
+                        in_=grouped[:].rearrange("p rx q t -> p (rx q t)"),
+                    )
+                    for m in (2, 3, 0, 1, 4, 5):
+                        outs = slice(m * P, (m + 1) * P)
+                        acc = acc_ps.tile([P, PATCH, P], F32)
+                        nc.tensor.matmul_mx(
+                            out=acc[:].rearrange("p r q -> p (r q)"),
+                            lhsT=w_words[:, outs].bitcast(FP8X4),
+                            lhsT_scale=w_scales[:, outs],
+                            rhs=x_words[:, cols].bitcast(FP8X4),
+                            rhs_scale=x_scales[:, cols],
+                            start=True,
+                            stop=True,
+                        )
+                        target = by_channel[m][:, ry * PATCH : (ry + 1) * PATCH, MARGIN : MARGIN + P]
+                        if m % 2 == 0:
+                            nc.scalar.copy(out=target, in_=acc[:])
+                        else:
+                            nc.vector.tensor_copy(out=target, in_=acc[:])
+
+            for u in range(HALO):
+                for pair in range(HALO // 2):
+                    bank = stage_ps.tile([P, 2, HALVES, P], F32, tag="bank")
+                    for side in range(2):
+                        for half in range(HALVES):
+                            to_patches(by_channel[2 + half], u, 2 * pair + side, bank[:, side, half, :])
+                    leave_psum(
+                        pair,
+                        k_halo[:, :, u, 2 * pair : 2 * pair + 2, :].rearrange("p c v h -> p c (v h)"),
+                        bank[:].rearrange("p v f (h c) -> p c (v f h)", c=HEAD_DIM),
+                        inside[:, halo_place(u)[2], halo_place(2 * pair)[2] : halo_place(2 * pair)[2] + 1],
+                    )
+            for a in range(PATCH):
+                for pair in range(PATCH // 2):
+                    bank = stage_ps.tile([P, 2, HALVES, P], F32, tag="bank")
+                    for side in range(2):
+                        for half in range(HALVES):
+                            to_patches(by_channel[half], a + 2, 2 * pair + side + 2, bank[:, side, half, :])
+                    leave_psum(
+                        pair,
+                        q_patch[:, :, a, 2 * pair : 2 * pair + 2, :].rearrange("p c b h -> p c (b h)"),
+                        bank[:].rearrange("p b f (h c) -> p c (b f h)", c=HEAD_DIM),
+                        inside[:, 1, 1:2],
+                    )
+
+        with tc.tile_pool(name="prod", bufs=3) as prod_pool, tc.psum_pool(name="score_ps", bufs=2) as score_ps:
+            for di in range(WINDOW):
+                for dj in range(WINDOW):
+                    prod = prod_pool.tile([P, HEAD_DIM, PATCH, PATCH * HEADS], F32)
+                    nc.vector.tensor_tensor(
+                        out=prod[:],
+                        in0=q_patch[:].rearrange("p c a b h -> p c a (b h)"),
+                        in1=k_halo[:, :, di : di + PATCH, dj : dj + PATCH, :].rearrange("p c a b h -> p c a (b h)"),
+                        op=ALU.mult,
+                    )
+                    score = score_ps.tile([P, P], F32)
+                    for c in range(HEAD_DIM):
+                        nc.tensor.matmul(
+                            out=score[:],
+                            lhsT=prod[:, c, :, :].rearrange("p a g -> p (a g)"),
+                            rhs=ident[:],
+                            is_transpose=True,
+                            start=(c == 0),
+                            stop=(c == HEAD_DIM - 1),
+                        )
+                    nc.scalar.copy(out=scores[:, di * WINDOW + dj, :], in_=score[:])
+
+        v_halo = keep.tile([P, HALO, HALO, DEPTH], F32, tag="halo")
+        for u in range(HALO):
+            for pair in range(HALO // 2):
+                bank = stage_ps.tile([P, 2, HALVES, P], F32, tag="bank")
+                for side in range(2):
+                    for half in range(HALVES):
+                        to_patches(by_channel[4 + half], u, 2 * pair + side, bank[:, side, half, :])
+                leave_psum(
+                    0,
+                    v_halo[:, u, 2 * pair : 2 * pair + 2, :].rearrange("p v d -> p (v d)"),
+                    bank[:].rearrange("p v f d -> p (v f d)"),
+                    inside[:, halo_place(u)[2], halo_place(2 * pair)[2] : halo_place(2 * pair)[2] + 1],
+                )
+
+        over_offsets = scores[:].rearrange("j o p -> j p o")
+        top = keep.tile([P, P], F32)
+        nc.vector.tensor_reduce(out=top[:], in_=over_offsets, axis=AX.X, op=ALU.max)
+        nc.vector.tensor_tensor(
+            out=scores[:], in0=scores[:], in1=top[:].unsqueeze(1).to_broadcast([P, OFFSETS, P]), op=ALU.subtract
+        )
+        nc.scalar.activation(out=scores[:], in_=scores[:], func=ACT.Exp)
+        total = keep.tile([P, P], F32)
+        nc.vector.tensor_reduce(out=total[:], in_=over_offsets, axis=AX.X, op=ALU.add)
+        nc.vector.reciprocal(out=total[:], in_=total[:])
+        nc.vector.tensor_tensor(
+            out=scores[:], in0=scores[:], in1=total[:].unsqueeze(1).to_broadcast([P, OFFSETS, P]), op=ALU.mult
+        )
+
+        with tc.tile_pool(name="late", bufs=1) as late, tc.tile_pool(name="weighted", bufs=3) as weighted_pool, tc.psum_pool(
+            name="out_ps", bufs=2
+        ) as out_ps:
+            att = late.tile([P, SPOTS, OFFSETS, HEADS], F32)
+            for first in range(0, OFFSETS, 4):
+                count = min(4, OFFSETS - first)
+                bank = stage_ps.tile([P, 4, SPOTS, HEADS], F32, tag="bank")
+                for k in range(count):
+                    nc.tensor.transpose(
+                        out=bank[:, k, :, :].rearrange("p s h -> p (s h)"), in_=scores[:, first + k, :], identity=ident[:]
+                    )
+                nc.scalar.copy(
+                    out=att[:, :, first : first + count, :], in_=bank[:, 0:count, :, :].rearrange("p o s h -> p s o h")
+                )
+
+            result = [late.tile([P, PIXELS], F32, name="result%d" % half) for half in range(HALVES)]
+            for a in range(PATCH):
+                sums = [out_ps.tile([P, PATCH, P], F32, name="sums%d" % half) for half in range(HALVES)]
+                for b in range(PATCH):
+                    weighted = weighted_pool.tile([P, WINDOW, WINDOW * HEADS, HEAD_DIM], F32)
+                    nc.vector.tensor_tensor(
+                        out=weighted[:],
+                        in0=v_halo[:, a : a + WINDOW, b : b + WINDOW, :].rearrange(
+                            "p u v (h c) -> p u (v h) c", c=HEAD_DIM
+                        ),
+                        in1=att[:, a * PATCH + b, :, :]
+                        .rearrange("p (di dj) h -> p di (dj h)", di=WINDOW)
+                        .unsqueeze(3)
+                        .to_broadcast([P, WINDOW, WINDOW * HEADS, HEAD_DIM]),
+                        op=ALU.mult,
+                    )
+                    by_offset = weighted[:].rearrange("p di (dj h) c -> p (di dj) (h c)", h=HEADS)
+                    for half in range(HALVES):
+                        for off in range(OFFSETS):
+                            nc.tensor.matmul(
+                                out=sums[half][:, b, :],
+                                lhsT=by_offset[:, off, half * P : (half + 1) * P],
+                                rhs=ident[:],
+                                is_transpose=True,
+                                start=(off == 0),
+                                stop=(off == OFFSETS - 1),
+                            )
+                for half in range(HALVES):
+                    nc.scalar.copy(
+                        out=result[half][:].rearrange(
+                            "c (g a qx b) -> c a g qx b", g=IMAGES * GRID, a=PATCH, qx=GRID, b=PATCH
+                        )[:, a],
+                        in_=sums[half][:].rearrange("c b (g qx) -> c g qx b", qx=GRID),
+                    )
+            for half in range(HALVES):
+                nc.sync.dma_start(
+                    out=out.rearrange("n (f c) h w -> f c n (h w)", f=HALVES)[half],
+                    in_=result[half][:].rearrange("c (n s) -> c n s", n=IMAGES),
+                )

@@ -6,12 +6,10 @@ from concourse.masks import make_identity
 F32 = mybir.dt.float32
 BF16 = mybir.dt.bfloat16
 I32 = mybir.dt.int32
-U32 = mybir.dt.uint32
 U8 = mybir.dt.uint8
 FP8X4 = mybir.dt.float8_e4m3fn_x4
 ALU = mybir.AluOpType
 ACT = mybir.ActivationFunctionType
-AX = mybir.AxisListType
 
 P = 128
 PACK = 4
@@ -19,263 +17,433 @@ IMAGES, CHANNELS_IN, SIDE = 2, 512, 32
 PIXELS = IMAGES * SIDE * SIDE
 HEADS, HEAD_DIM = 8, 32
 DEPTH = HEADS * HEAD_DIM
-HALVES = DEPTH // P
-HEADS_HALF = HEADS // HALVES
+HALVES = 2
+HH = HEADS // HALVES
 WINDOW = 5
 OFFSETS = WINDOW * WINDOW
 PATCH = 4
 SPOTS = PATCH * PATCH
 GRID = SIDE // PATCH
+REACH = WINDOW // 2
 HALO = PATCH + WINDOW - 1
-MARGIN = 16
-ROW = P + 2 * MARGIN
-QUERIES = SPOTS * HEADS
+PAIRS = OFFSETS // 2
+GROUP = SPOTS * HH
+S_ITEMS = (8, 6)
 
 FLOPS = 2 * 3 * DEPTH * CHANNELS_IN * PIXELS + 2 * 2 * PIXELS * HEADS * OFFSETS * HEAD_DIM
-
-
-def halo_place(u):
-    step = (u - 2) // PATCH
-    border = 0 if u < 2 else (2 if u >= HALO - 2 else 1)
-    return step, (u - 2) - PATCH * step, border
 
 
 def tile_relation_kernel(tc, x, w_qkv_words, w_qkv_scales, out):
     nc = tc.nc
     with ExitStack() as whole:
-        const = whole.enter_context(tc.tile_pool(name="const", bufs=1))
         keep = whole.enter_context(tc.tile_pool(name="keep", bufs=1))
+        work = whole.enter_context(tc.tile_pool(name="work", bufs=2))
+        small = whole.enter_context(tc.tile_pool(name="small", bufs=1))
         stage_ps = whole.enter_context(tc.psum_pool(name="stage_ps", bufs=3))
+        score_ps = whole.enter_context(tc.psum_pool(name="score_ps", bufs=2))
+        out_ps = whole.enter_context(tc.psum_pool(name="out_ps", bufs=3))
 
-        ident = const.tile([P, P], F32)
+        ident = keep.tile([P, P], F32)
         make_identity(nc, ident[:])
+        w_words = keep.tile([P, 3 * DEPTH], I32, align_bytes=64)
+        w_scales = keep.tile([P, 3 * DEPTH], U8, align_bytes=64)
+        x_words = keep.tile([P, HALO, HALO, P], I32, align_bytes=64, tag="words")
+        x_scales = keep.tile([P, HALO, HALO, P], U8, align_bytes=64, tag="scales")
+        front = keep.tile([P, 2, PACK * PIXELS], BF16, align_bytes=64, tag="v")
+        x_sb = front[:, 0].rearrange("p (t s) -> p t s", t=PACK)
+        grouped = front[:, 1].rearrange("p (ry rx q t) -> p ry rx q t", ry=PATCH, rx=PATCH, t=PACK)
 
-        by_patch = ident[:].rearrange("p (n y x) -> p n y x", n=IMAGES, y=GRID, x=GRID)
-        at_border = const.tile([P, 2, 2], F32)
-        nc.vector.tensor_reduce(out=at_border[:, 0, 0:1], in_=by_patch[:, :, 0, :], axis=AX.XY, op=ALU.add)
-        nc.vector.tensor_reduce(out=at_border[:, 0, 1:2], in_=by_patch[:, :, GRID - 1, :], axis=AX.XY, op=ALU.add)
-        nc.vector.tensor_reduce(out=at_border[:, 1, 0:1], in_=by_patch[:, :, :, 0], axis=AX.XY, op=ALU.add)
-        nc.vector.tensor_reduce(out=at_border[:, 1, 1:2], in_=by_patch[:, :, :, GRID - 1], axis=AX.XY, op=ALU.add)
-        one_way = const.tile([P, 2, 3], F32)
-        nc.vector.memset(one_way[:], 1.0)
-        nc.vector.tensor_scalar(
-            out=one_way[:, :, 0:3:2], in0=at_border[:], scalar1=-1.0, scalar2=1.0, op0=ALU.mult, op1=ALU.add
+        per_image = SIDE * SIDE
+        for n in range(IMAGES):
+            nc.scalar.dma_start(
+                out=x_sb[:, :, n * per_image : (n + 1) * per_image],
+                in_=x[n].rearrange("(p t) h w -> p t (h w)", t=PACK),
+            )
+        nc.vector.memset(w_scales[:].bitcast(I32), 0)
+        nc.sync.dma_start(out=w_words[:], in_=w_qkv_words[0].rearrange("p n t -> p (n t)").bitcast(I32))
+        for quad in range(4):
+            nc.sync.dma_start(
+                out=w_scales[32 * quad : 32 * quad + 4, :].bitcast(I32),
+                in_=w_qkv_scales[0, 4 * quad : 4 * quad + 4, :].bitcast(I32),
+            )
+        nc.gpsimd.memset(x_scales[:].rearrange("p u v q -> p (u v q)").bitcast(I32), 0)
+        nc.gpsimd.memset(x_words[:, PATCH // 2 : PATCH // 2 + PATCH, 0:REACH, :], 0)
+        nc.gpsimd.memset(x_words[:, PATCH // 2 : PATCH // 2 + PATCH, REACH + PATCH : HALO, :], 0)
+        nc.gpsimd.memset(x_words[:, 0:REACH, :, :], 0)
+        nc.gpsimd.memset(x_words[:, REACH + PATCH : HALO, :, :], 0)
+        spark = small.tile([P, 1], F32)
+        nc.vector.memset(spark[:], 0.0)
+        nc.scalar.activation(out=spark[:], in_=spark[:], func=ACT.Exp)
+
+        by_spot = x_sb.rearrange(
+            "p t (g ry qx rx) -> p ry rx g qx t", g=IMAGES * GRID, ry=PATCH, qx=GRID, rx=PATCH
         )
-        inside = const.tile([P, 3, 3], F32)
-        nc.vector.tensor_tensor(
-            out=inside[:],
-            in0=one_way[:, 0, :].unsqueeze(2).to_broadcast([P, 3, 3]),
-            in1=one_way[:, 1, :].unsqueeze(1).to_broadcast([P, 3, 3]),
-            op=ALU.mult,
+        for ry in range(PATCH):
+            nc.vector.tensor_copy(
+                out=grouped[:, ry].rearrange("p rx (g qx) t -> p rx g qx t", qx=GRID), in_=by_spot[:, ry]
+            )
+        for ry in range(PATCH):
+            mid = slice(REACH, REACH + PATCH)
+            nc.vector.quantize_mx(
+                out=x_words[:, REACH + ry, mid, :].rearrange("p v q -> p (v q)").bitcast(FP8X4),
+                scales=x_scales[:, REACH + ry, mid, :].rearrange("p v q -> p (v q)"),
+                in_=grouped[:, ry].rearrange("p rx q t -> p (rx q t)"),
+            )
+
+        def columns(tile, v0, v1, x0, x1):
+            return tile[:, REACH : REACH + PATCH, v0:v1, :].rearrange("p u v (r x) -> p u (v r) x", x=GRID)[
+                :, :, :, x0:x1
+            ]
+
+        def rows(tile, u0, u1, q0, q1):
+            return tile[:, u0:u1, :, :].rearrange("p u v (n q) -> p u (v n) q", n=IMAGES)[:, :, :, q0:q1]
+
+        scale_words = x_scales[:].rearrange("p u v q -> p (u v q)").bitcast(I32).rearrange(
+            "p (u v q) -> p u v q", u=HALO, v=HALO
         )
+        per_grid = GRID * GRID
+        for tile in (x_words, x_scales):
+            nc.vector.tensor_copy(out=columns(tile, 0, 2, 1, GRID), in_=columns(tile, 4, 6, 0, GRID - 1))
+            nc.vector.tensor_copy(out=columns(tile, 6, 8, 0, GRID - 1), in_=columns(tile, 2, 4, 1, GRID))
+        for tile, row, size in ((x_words, GRID, per_grid), (scale_words, GRID // 4, per_grid // 4)):
+            nc.vector.tensor_copy(out=rows(tile, 0, 2, row, size), in_=rows(tile, 4, 6, 0, size - row))
+            nc.vector.tensor_copy(out=rows(tile, 6, 8, 0, size - row), in_=rows(tile, 2, 4, row, size))
 
-        by_channel = [None] * 6
-        for m in (4, 5):
-            by_channel[m] = keep.tile([P, SPOTS, ROW], F32, name="by_channel%d" % m)
-        k_halo = keep.tile([P, HEAD_DIM, HALO, HALO, HEADS], F32, tag="halo")
-        q_patch = keep.tile([P, HEAD_DIM, PATCH, PATCH, HEADS], F32)
-        scores = keep.tile([P, OFFSETS, P], F32)
+        def convolve(first, wide, u, v0):
+            bank = stage_ps.tile([P, PATCH * P // wide, wide], F32, tag="stage", name="bank")
+            cols = slice(first, first + wide)
+            for j in range(PATCH * P // wide):
+                nc.tensor.matmul_mx(
+                    out=bank[:, j, :],
+                    lhsT=x_words[:, u, v0 + j, :].bitcast(FP8X4),
+                    lhsT_scale=x_scales[:, u, v0 + j, :],
+                    rhs=w_words[:, cols].bitcast(FP8X4),
+                    rhs_scale=w_scales[:, cols],
+                    start=True,
+                    stop=True,
+                )
+            return bank
 
-        def to_patches(source, u, v, bank_part):
-            step_y, ry = halo_place(u)[0:2]
-            step_x, rx = halo_place(v)[0:2]
-            first = MARGIN + GRID * step_y + step_x
-            nc.tensor.transpose(out=bank_part, in_=source[:, ry * PATCH + rx, first : first + P], identity=ident[:])
-
-        def leave_psum(turn, out_ap, in_ap, factor):
-            if turn % 2 == 0:
-                nc.scalar.activation(out=out_ap, in_=in_ap, func=ACT.Copy, scale=factor)
+        def leave(on_vector, out_ap, in_ap):
+            if on_vector:
+                nc.vector.tensor_copy(out=out_ap, in_=in_ap)
             else:
-                nc.vector.tensor_scalar(out=out_ap, in0=in_ap, scalar1=factor, scalar2=None, op0=ALU.mult)
+                nc.scalar.copy(out=out_ap, in_=in_ap)
 
-        with tc.tile_pool(name="chan_qk", bufs=1) as chan_qk:
-            for m in range(4):
-                by_channel[m] = chan_qk.tile([P, SPOTS, ROW], F32, name="by_channel%d" % m)
-            for m in range(2, 6):
-                nc.gpsimd.memset(by_channel[m][:, :, 0:MARGIN], 0.0)
-                nc.gpsimd.memset(by_channel[m][:, :, MARGIN + P : ROW], 0.0)
+        q_own = [None, None]
+        k_halo = [None, None]
 
-            with tc.tile_pool(name="front", bufs=1) as front, tc.tile_pool(name="group", bufs=2) as group, tc.psum_pool(
-                name="acc_ps", bufs=2
-            ) as acc_ps:
-                w_words = front.tile([P, 3 * DEPTH], U32, align_bytes=64)
-                w_scales = front.tile([P, 3 * DEPTH], U8, align_bytes=64)
-                nc.vector.memset(w_scales[:].bitcast(I32), 0)
-                nc.sync.dma_start(
-                    out=w_words[:].bitcast(I32), in_=w_qkv_words[0].rearrange("p n t -> p (n t)").bitcast(I32)
+        def load_q(half, ry, on_vector=False):
+            if q_own[half] is None:
+                q_own[half] = keep.tile([P, HEAD_DIM, SPOTS, HH], F32, name="q%d" % half)
+            bank = convolve(half * P, P, REACH + ry, REACH)
+            leave(
+                on_vector,
+                q_own[half][:, :, ry * PATCH : (ry + 1) * PATCH, :],
+                bank[:].rearrange("p r (h c) -> p c r h", c=HEAD_DIM),
+            )
+
+        def load_k(half, u, v0, on_vector=False):
+            if k_halo[half] is None:
+                k_halo[half] = keep.tile([P, HEAD_DIM, HALO, HALO, HH], F32, tag="k%d" % half, align_bytes=64, name="k%d" % half)
+            bank = convolve(DEPTH + half * P, P, u, v0)
+            leave(
+                on_vector,
+                k_halo[half][:, :, u, v0 : v0 + PATCH, :],
+                bank[:].rearrange("p r (h c) -> p c r h", c=HEAD_DIM),
+            )
+
+        v_halo = keep.tile([P, HALVES, HALO, HALO, P], F32, tag="v", align_bytes=64, name="v_halo")
+
+        def load_v(half, u, v0):
+            bank = convolve(2 * DEPTH, DEPTH, u, v0)
+            nc.scalar.copy(
+                out=v_halo[:, :, u, v0 : v0 + 2, :], in_=bank[:].rearrange("p r (f d) -> p f r d", f=HALVES)
+            )
+
+        scores = [keep.tile([P, PAIRS, P], F32, name="scores0"), None]
+        lone = keep.tile([P, P], F32, name="lone")
+
+        def products(prod, slot, half, offset):
+            di, dj = divmod(offset, WINDOW)
+            nc.vector.tensor_tensor(
+                out=prod[:, :, slot, :].rearrange("p c (a g) -> p c a g", a=PATCH),
+                in0=q_own[half][:].rearrange("p c (a b) h -> p c a (b h)", a=PATCH),
+                in1=k_halo[half][:, :, di : di + PATCH, dj : dj + PATCH, :].rearrange("p c a b h -> p c a (b h)"),
+                op=ALU.mult,
+            )
+
+        def sum_over_channels(prod, target):
+            score = score_ps.tile([P, P], F32, name="score")
+            for c in range(HEAD_DIM):
+                nc.tensor.matmul(
+                    out=score[:],
+                    lhsT=prod[:, c, :, :].rearrange("p o g -> p (o g)"),
+                    rhs=ident[:],
+                    is_transpose=True,
+                    start=(c == 0),
+                    stop=(c == HEAD_DIM - 1),
                 )
-                for quad in range(4):
-                    nc.sync.dma_start(
-                        out=w_scales[32 * quad : 32 * quad + 4, :].bitcast(I32),
-                        in_=w_qkv_scales[0, 4 * quad : 4 * quad + 4, :].bitcast(I32),
-                    )
-                x_sb = front.tile([P, PACK, PIXELS], BF16)
-                per_image = SIDE * SIDE
-                for n in range(IMAGES):
-                    nc.scalar.dma_start(
-                        out=x_sb[:, :, n * per_image : (n + 1) * per_image],
-                        in_=x[n].rearrange("(p t) h w -> p t (h w)", t=PACK),
-                    )
-                x_words = front.tile([P, PIXELS], U32, align_bytes=64)
-                x_scales = front.tile([P, PIXELS], U8, align_bytes=64)
-                x_by_spot = x_sb[:].rearrange(
-                    "p t (g ry qx rx) -> p ry rx g qx t", g=IMAGES * GRID, ry=PATCH, qx=GRID, rx=PATCH
+            nc.scalar.copy(out=target, in_=score[:])
+
+        late_sums = []
+
+        def start_tile(first, second, target):
+            prod = work.tile([P, HEAD_DIM, 2, GROUP], F32, tag="work", name="prod")
+            products(prod, 0, first[0], first[1])
+            products(prod, 1, second[0], second[1])
+            late_sums.append((prod, target))
+
+        def finish_tile():
+            prod, target = late_sums[0]
+            late_sums.remove(late_sums[0])
+            sum_over_channels(prod, target)
+
+        def start_pair(half, t):
+            start_tile((half, 2 * t), (half, 2 * t + 1), scores[half][:, t, :])
+
+        late = [None]
+
+        def att_of(half):
+            if late[0] is None:
+                late[0] = keep.tile(
+                    [P, 2 * OFFSETS * GROUP + 2 * PIXELS], F32, tag="words", align_bytes=64, name="late"
                 )
-                for ry in range(PATCH):
-                    cols = slice(ry * PATCH * P, (ry + 1) * PATCH * P)
-                    grouped = group.tile([P, PATCH, P, PACK], BF16, align_bytes=64)
-                    nc.vector.tensor_copy(
-                        out=grouped[:].rearrange("p rx (g qx) t -> p rx g qx t", qx=GRID), in_=x_by_spot[:, ry]
-                    )
-                    nc.vector.quantize_mx(
-                        out=x_words[:, cols].bitcast(FP8X4),
-                        scales=x_scales[:, cols],
-                        in_=grouped[:].rearrange("p rx q t -> p (rx q t)"),
-                    )
-                    for m in (2, 3, 0, 1, 4, 5):
-                        outs = slice(m * P, (m + 1) * P)
-                        acc = acc_ps.tile([P, PATCH, P], F32)
-                        nc.tensor.matmul_mx(
-                            out=acc[:].rearrange("p r q -> p (r q)"),
-                            lhsT=w_words[:, outs].bitcast(FP8X4),
-                            lhsT_scale=w_scales[:, outs],
-                            rhs=x_words[:, cols].bitcast(FP8X4),
-                            rhs_scale=x_scales[:, cols],
-                            start=True,
-                            stop=True,
-                        )
-                        target = by_channel[m][:, ry * PATCH : (ry + 1) * PATCH, MARGIN : MARGIN + P]
-                        if m % 2 == 0:
-                            nc.scalar.copy(out=target, in_=acc[:])
-                        else:
-                            nc.vector.tensor_copy(out=target, in_=acc[:])
+            return late[0][:, half * OFFSETS * GROUP : (half + 1) * OFFSETS * GROUP].rearrange(
+                "p (s o h) -> p s o h", s=SPOTS, o=OFFSETS
+            )
 
-            for u in range(HALO):
-                for pair in range(HALO // 2):
-                    bank = stage_ps.tile([P, 2, HALVES, P], F32, tag="bank")
-                    for side in range(2):
-                        for half in range(HALVES):
-                            to_patches(by_channel[2 + half], u, 2 * pair + side, bank[:, side, half, :])
-                    leave_psum(
-                        pair,
-                        k_halo[:, :, u, 2 * pair : 2 * pair + 2, :].rearrange("p c v h -> p c (v h)"),
-                        bank[:].rearrange("p v f (h c) -> p c (v f h)", c=HEAD_DIM),
-                        inside[:, halo_place(u)[2], halo_place(2 * pair)[2] : halo_place(2 * pair)[2] + 1],
-                    )
-            for a in range(PATCH):
-                for pair in range(PATCH // 2):
-                    bank = stage_ps.tile([P, 2, HALVES, P], F32, tag="bank")
-                    for side in range(2):
-                        for half in range(HALVES):
-                            to_patches(by_channel[half], a + 2, 2 * pair + side + 2, bank[:, side, half, :])
-                    leave_psum(
-                        pair,
-                        q_patch[:, :, a, 2 * pair : 2 * pair + 2, :].rearrange("p c b h -> p c (b h)"),
-                        bank[:].rearrange("p b f (h c) -> p c (b f h)", c=HEAD_DIM),
-                        inside[:, 1, 1:2],
-                    )
+        def result_of(half):
+            base = 2 * OFFSETS * GROUP + half * PIXELS
+            return late[0][:, base : base + PIXELS]
 
-        with tc.tile_pool(name="prod", bufs=3) as prod_pool, tc.psum_pool(name="score_ps", bufs=2) as score_ps:
-            for di in range(WINDOW):
-                for dj in range(WINDOW):
-                    prod = prod_pool.tile([P, HEAD_DIM, PATCH, PATCH * HEADS], F32)
-                    nc.vector.tensor_tensor(
-                        out=prod[:],
-                        in0=q_patch[:].rearrange("p c a b h -> p c a (b h)"),
-                        in1=k_halo[:, :, di : di + PATCH, dj : dj + PATCH, :].rearrange("p c a b h -> p c a (b h)"),
-                        op=ALU.mult,
-                    )
-                    score = score_ps.tile([P, P], F32)
-                    for c in range(HEAD_DIM):
-                        nc.tensor.matmul(
-                            out=score[:],
-                            lhsT=prod[:, c, :, :].rearrange("p a g -> p (a g)"),
-                            rhs=ident[:],
-                            is_transpose=True,
-                            start=(c == 0),
-                            stop=(c == HEAD_DIM - 1),
-                        )
-                    nc.scalar.copy(out=scores[:, di * WINDOW + dj, :], in_=score[:])
+        lone_patch = keep.tile([P, HALVES, GROUP], F32, name="lone_patch")
+        tops = [small.tile([P, SPOTS, HH], F32, name="top%d" % half) for half in range(HALVES)]
+        trees = [None, None]
+        raw = {}
 
-        v_halo = keep.tile([P, HALO, HALO, DEPTH], F32, tag="halo")
-        for u in range(HALO):
-            for pair in range(HALO // 2):
-                bank = stage_ps.tile([P, 2, HALVES, P], F32, tag="bank")
-                for side in range(2):
-                    for half in range(HALVES):
-                        to_patches(by_channel[4 + half], u, 2 * pair + side, bank[:, side, half, :])
-                leave_psum(
-                    0,
-                    v_halo[:, u, 2 * pair : 2 * pair + 2, :].rearrange("p v d -> p (v d)"),
-                    bank[:].rearrange("p v f d -> p (v f d)"),
-                    inside[:, halo_place(u)[2], halo_place(2 * pair)[2] : halo_place(2 * pair)[2] + 1],
+        def softmax_max(half):
+            tree = small.tile([P, PAIRS // 2, P], F32, tag="tree", name="tree")
+            trees[half] = tree
+            nc.vector.tensor_max(out=tree[:], in0=scores[half][:, 0:6, :], in1=scores[half][:, 6:12, :])
+            nc.vector.tensor_max(out=tree[:, 0:3, :], in0=tree[:, 0:3, :], in1=tree[:, 3:6, :])
+            nc.vector.tensor_max(out=tree[:, 0, :], in0=tree[:, 0, :], in1=tree[:, 1, :])
+            nc.vector.tensor_max(out=tree[:, 0, :], in0=tree[:, 0, :], in1=tree[:, 2, :])
+
+        def softmax_turn(half):
+            bank = stage_ps.tile([P, PATCH, P], F32, tag="stage", name="bank")
+            if half == 0:
+                nc.tensor.transpose(out=bank[:, 0, :], in_=lone[:], identity=ident[:])
+            nc.tensor.transpose(out=bank[:, 1, :], in_=trees[half][:, 0, :], identity=ident[:])
+            both = small.tile([P, 2, SPOTS, HH], F32, tag="both", name="both")
+            raw[half, "both"] = both
+            if half == 0:
+                nc.scalar.copy(out=lone_patch[:].rearrange("p f g -> p (f g)"), in_=bank[:, 0, :])
+            nc.scalar.copy(out=both[:].rearrange("p f s h -> p (f s h)"), in_=bank[:, 1, :])
+            for k in range(PAIRS // 4):
+                bank = stage_ps.tile([P, PATCH, P], F32, tag="stage", name="bank")
+                raw[half, k] = bank
+                for j in range(4):
+                    nc.tensor.transpose(out=bank[:, j, :], in_=scores[half][:, 4 * k + j, :], identity=ident[:])
+
+        def softmax_exp(half):
+            top = tops[half]
+            both = raw[half, "both"]
+            own = lone_patch[:, half, :].rearrange("p (s h) -> p s h", h=HH)
+            by_offset = att_of(half).rearrange("p s o h -> p o s h")
+            nc.vector.tensor_max(out=top[:], in0=both[:, 0], in1=both[:, 1])
+            nc.vector.tensor_max(out=top[:], in0=top[:], in1=own)
+            nc.vector.tensor_sub(out=by_offset[:, OFFSETS - 1], in0=own, in1=top[:])
+            for k in range(PAIRS // 4):
+                nc.vector.tensor_sub(
+                    out=by_offset[:, 8 * k : 8 * k + 8],
+                    in0=raw[half, k][:].rearrange("p t (o s h) -> p (t o) s h", o=2, h=HH),
+                    in1=top[:].unsqueeze(1).to_broadcast([P, 8, SPOTS, HH]),
                 )
+            flat = att_of(half).rearrange("p s o h -> p (s o h)")
+            nc.scalar.activation(out=flat, in_=flat, func=ACT.Exp)
 
-        over_offsets = scores[:].rearrange("j o p -> j p o")
-        top = keep.tile([P, P], F32)
-        nc.vector.tensor_reduce(out=top[:], in_=over_offsets, axis=AX.X, op=ALU.max)
-        nc.vector.tensor_tensor(
-            out=scores[:], in0=scores[:], in1=top[:].unsqueeze(1).to_broadcast([P, OFFSETS, P]), op=ALU.subtract
-        )
-        nc.scalar.activation(out=scores[:], in_=scores[:], func=ACT.Exp)
-        total = keep.tile([P, P], F32)
-        nc.vector.tensor_reduce(out=total[:], in_=over_offsets, axis=AX.X, op=ALU.add)
-        nc.vector.reciprocal(out=total[:], in_=total[:])
-        nc.vector.tensor_tensor(
-            out=scores[:], in0=scores[:], in1=total[:].unsqueeze(1).to_broadcast([P, OFFSETS, P]), op=ALU.mult
-        )
+        def softmax_norm(half):
+            att = att_of(half)
+            rows_of = att.rearrange("p s o h -> p s (o h)")
+            total = small.tile([P, SPOTS, 12 * HH], F32, tag="total", name="total")
+            nc.vector.tensor_add(out=total[:], in0=rows_of[:, :, 0 : 12 * HH], in1=rows_of[:, :, 12 * HH : 24 * HH])
+            for n in (6, 3):
+                nc.vector.tensor_add(
+                    out=total[:, :, 0 : n * HH], in0=total[:, :, 0 : n * HH], in1=total[:, :, n * HH : 2 * n * HH]
+                )
+            sums = total[:, :, 0:HH]
+            nc.vector.tensor_add(out=sums, in0=sums, in1=total[:, :, HH : 2 * HH])
+            nc.vector.tensor_add(out=sums, in0=sums, in1=total[:, :, 2 * HH : 3 * HH])
+            nc.vector.tensor_add(out=sums, in0=sums, in1=att[:, :, OFFSETS - 1, :])
+            nc.vector.reciprocal(out=tops[half][:], in_=sums)
+            nc.vector.tensor_tensor(
+                out=att, in0=att, in1=tops[half][:].unsqueeze(2).to_broadcast([P, SPOTS, OFFSETS, HH]), op=ALU.mult
+            )
 
-        with tc.tile_pool(name="late", bufs=1) as late, tc.tile_pool(name="weighted", bufs=3) as weighted_pool, tc.psum_pool(
-            name="out_ps", bufs=2
-        ) as out_ps:
-            att = late.tile([P, SPOTS, OFFSETS, HEADS], F32)
-            for first in range(0, OFFSETS, 4):
-                count = min(4, OFFSETS - first)
-                bank = stage_ps.tile([P, 4, SPOTS, HEADS], F32, tag="bank")
-                for k in range(count):
-                    nc.tensor.transpose(
-                        out=bank[:, k, :, :].rearrange("p s h -> p (s h)"), in_=scores[:, first + k, :], identity=ident[:]
-                    )
+        banks = {}
+        filled = {}
+
+        def sum_over_offsets(half, s, weighted):
+            a, b = divmod(s, PATCH)
+            if (half, a) not in filled:
+                banks[half, a] = out_ps.tile([P, PATCH, P], F32, tag="sums", name="sums")
+                filled[half, a] = 0
+            bank = banks[half, a]
+            for off in range(OFFSETS):
+                nc.tensor.matmul(
+                    out=bank[:, b, :],
+                    lhsT=weighted[:, off, :],
+                    rhs=ident[:],
+                    is_transpose=True,
+                    start=(off == 0),
+                    stop=(off == OFFSETS - 1),
+                )
+            filled[half, a] += 1
+            if filled[half, a] == PATCH:
                 nc.scalar.copy(
-                    out=att[:, :, first : first + count, :], in_=bank[:, 0:count, :, :].rearrange("p o s h -> p s o h")
+                    out=result_of(half).rearrange(
+                        "c (g a qx b) -> c a g qx b", g=IMAGES * GRID, a=PATCH, qx=GRID, b=PATCH
+                    )[:, a],
+                    in_=bank[:].rearrange("c b (g qx) -> c g qx b", qx=GRID),
                 )
 
-            result = [late.tile([P, PIXELS], F32, name="result%d" % half) for half in range(HALVES)]
-            for a in range(PATCH):
-                sums = [out_ps.tile([P, PATCH, P], F32, name="sums%d" % half) for half in range(HALVES)]
-                for b in range(PATCH):
-                    weighted = weighted_pool.tile([P, WINDOW, WINDOW * HEADS, HEAD_DIM], F32)
-                    nc.vector.tensor_tensor(
-                        out=weighted[:],
-                        in0=v_halo[:, a : a + WINDOW, b : b + WINDOW, :].rearrange(
-                            "p u v (h c) -> p u (v h) c", c=HEAD_DIM
-                        ),
-                        in1=att[:, a * PATCH + b, :, :]
-                        .rearrange("p (di dj) h -> p di (dj h)", di=WINDOW)
-                        .unsqueeze(3)
-                        .to_broadcast([P, WINDOW, WINDOW * HEADS, HEAD_DIM]),
-                        op=ALU.mult,
-                    )
-                    by_offset = weighted[:].rearrange("p di (dj h) c -> p (di dj) (h c)", h=HEADS)
-                    for half in range(HALVES):
-                        for off in range(OFFSETS):
-                            nc.tensor.matmul(
-                                out=sums[half][:, b, :],
-                                lhsT=by_offset[:, off, half * P : (half + 1) * P],
-                                rhs=ident[:],
-                                is_transpose=True,
-                                start=(off == 0),
-                                stop=(off == OFFSETS - 1),
-                            )
-                for half in range(HALVES):
-                    nc.scalar.copy(
-                        out=result[half][:].rearrange(
-                            "c (g a qx b) -> c a g qx b", g=IMAGES * GRID, a=PATCH, qx=GRID, b=PATCH
-                        )[:, a],
-                        in_=sums[half][:].rearrange("c b (g qx) -> c g qx b", qx=GRID),
-                    )
-            for half in range(HALVES):
-                nc.sync.dma_start(
-                    out=out.rearrange("n (f c) h w -> f c n (h w)", f=HALVES)[half],
-                    in_=result[half][:].rearrange("c (n s) -> c n s", n=IMAGES),
-                )
+        late_items = []
+
+        def vector_item(half, s):
+            a, b = divmod(s, PATCH)
+            block = work.tile([P, OFFSETS, P], F32, tag="work", name="block")
+            nc.vector.tensor_tensor(
+                out=block[:].rearrange("p (di dj) (h c) -> p di (dj h) c", di=WINDOW, c=HEAD_DIM),
+                in0=v_halo[:, half, a : a + WINDOW, b : b + WINDOW, :].rearrange(
+                    "p u v (h c) -> p u (v h) c", c=HEAD_DIM
+                ),
+                in1=att_of(half)[:, s]
+                .rearrange("p (di dj) h -> p di (dj h)", di=WINDOW)
+                .unsqueeze(3)
+                .to_broadcast([P, WINDOW, WINDOW * HH, HEAD_DIM]),
+                op=ALU.mult,
+            )
+            late_items.append((half, s, block))
+
+        scalar_rows = [(half, s, di) for half in range(HALVES) for s in range(S_ITEMS[half]) for di in range(WINDOW)]
+        blocks_s = {}
+
+        def scalar_work(count):
+            for _ in range(min(count, len(scalar_rows))):
+                half, s, di = scalar_rows[0]
+                scalar_rows.remove(scalar_rows[0])
+                a, b = divmod(s, PATCH)
+                if di == 0:
+                    if "pair" not in blocks_s:
+                        blocks_s["pair"] = keep.tile([P, 2, OFFSETS, P], F32, tag="k0", align_bytes=64, name="pair_s")
+                        blocks_s["next"] = 0
+                    blocks_s["now"] = blocks_s["pair"][:, blocks_s["next"] % 2]
+                    blocks_s["next"] += 1
+                block = blocks_s["now"]
+                for dj in range(WINDOW):
+                    off = di * WINDOW + dj
+                    for h in range(HH):
+                        ch = slice(h * HEAD_DIM, (h + 1) * HEAD_DIM)
+                        nc.scalar.activation(
+                            out=block[:, off, ch],
+                            in_=v_halo[:, half, a + di, b + dj, ch],
+                            func=ACT.Copy,
+                            scale=att_of(half)[:, s, off, h : h + 1],
+                        )
+                if di == WINDOW - 1:
+                    late_items.append((half, s, block))
+
+        def finish_items(count):
+            for _ in range(count):
+                half, s, block = late_items[0]
+                late_items.remove(late_items[0])
+                sum_over_offsets(half, s, block)
+
+        def store(half):
+            nc.sync.dma_start(
+                out=out.rearrange("n (f c) h w -> f c n (h w)", f=HALVES)[half],
+                in_=result_of(half).rearrange("c (n s) -> c n s", n=IMAGES),
+            )
+
+        pinned = {mybir.EngineType.PE, mybir.EngineType.Activation, mybir.EngineType.DVE}
+        with tc.manual_schedule(engines=pinned):
+            for ry in range(PATCH):
+                load_q(0, ry, ry % 2 == 1)
+            for v0 in (0, PATCH):
+                for u in range(PATCH):
+                    load_k(0, u, v0, v0 == 0 and u % 2 == 1)
+            pending = [(load_k, 0, u, v0) for u in range(PATCH, HALO) for v0 in (0, PATCH)]
+            pending += [(load_q, 1, ry, None) for ry in range(PATCH)]
+            pending += [(load_k, 1, u, v0) for u in range(HALO) for v0 in (0, PATCH)]
+            pending += [(load_v, 0, u, v0) for u in range(HALO) for v0 in range(0, HALO, 2)]
+
+            def some_loads(count):
+                for _ in range(min(count, len(pending))):
+                    load, half, u, v0 = pending[0]
+                    pending.remove(pending[0])
+                    if v0 is None:
+                        load(half, u)
+                    else:
+                        load(half, u, v0)
+
+            start_pair(0, 0)
+            some_loads(6)
+            for t in range(1, PAIRS):
+                start_pair(0, t)
+                finish_tile()
+                some_loads(5)
+            start_tile((0, OFFSETS - 1), (1, OFFSETS - 1), lone[:])
+            finish_tile()
+            some_loads(len(pending))
+            scores[1] = keep.tile([P, PAIRS, P], F32, tag="scales", align_bytes=64, name="scores1")
+            start_pair(1, 0)
+            finish_tile()
+            softmax_max(0)
+            start_pair(1, 1)
+            finish_tile()
+            softmax_turn(0)
+            softmax_exp(0)
+            start_pair(1, 2)
+            finish_tile()
+            softmax_norm(0)
+            for t in range(3, PAIRS):
+                start_pair(1, t)
+                finish_tile()
+                ready = len(late_items)
+                scalar_work(3)
+                finish_items(ready)
+            vector_rest = [(half, s) for half in range(HALVES) for s in reversed(range(S_ITEMS[half], SPOTS))]
+
+            def vector_work():
+                half, s = vector_rest[0]
+                vector_rest.remove(vector_rest[0])
+                vector_item(half, s)
+
+            def step(count):
+                ready = len(late_items)
+                if vector_rest:
+                    vector_work()
+                scalar_work(count)
+                finish_items(ready)
+
+            ready = len(late_items)
+            vector_work()
+            finish_tile()
+            finish_items(ready)
+            softmax_max(1)
+            scalar_work(2)
+            step(2)
+            softmax_turn(1)
+            softmax_exp(1)
+            step(2)
+            softmax_norm(1)
+            stored = 0
+            turn = 0
+            while vector_rest or late_items or scalar_rows:
+                step(2 + turn % 2)
+                turn += 1
+                if stored == 0 and all((0, a) in filled and filled[0, a] == PATCH for a in range(PATCH)):
+                    store(0)
+                    stored = 1
+            store(1)

@@ -28,7 +28,10 @@ REACH = WINDOW // 2
 HALO = PATCH + WINDOW - 1
 PAIRS = OFFSETS // 2
 GROUP = SPOTS * HH
-S_ITEMS = (8, 6)
+S_ITEMS = (8, 7)
+
+FOLD_QK = (0, 8)
+FOLD_AV = 5
 
 FLOPS = 2 * 3 * DEPTH * CHANNELS_IN * PIXELS + 2 * 2 * PIXELS * HEADS * OFFSETS * HEAD_DIM
 
@@ -173,18 +176,32 @@ def tile_relation_kernel(tc, x, w_qkv_words, w_qkv_scales, out):
                 op=ALU.mult,
             )
 
-        def sum_over_channels(prod, target):
+        pending = []
+
+        def some_loads(count):
+            for _ in range(min(count, len(pending))):
+                load, half, u, v0 = pending[0]
+                pending.remove(pending[0])
+                if v0 is None:
+                    load(half, u)
+                else:
+                    load(half, u, v0)
+
+        def sum_over_channels(prod, count, target, loads):
             score = score_ps.tile([P, P], F32, name="score")
-            for c in range(HEAD_DIM):
+            for c in range(count):
+                if c == count // 2:
+                    some_loads(loads)
                 nc.tensor.matmul(
                     out=score[:],
                     lhsT=prod[:, c, :, :].rearrange("p o g -> p (o g)"),
                     rhs=ident[:],
                     is_transpose=True,
                     start=(c == 0),
-                    stop=(c == HEAD_DIM - 1),
+                    stop=(c == count - 1),
                 )
             nc.scalar.copy(out=target, in_=score[:])
+            some_loads(loads)
 
         late_sums = []
 
@@ -192,12 +209,17 @@ def tile_relation_kernel(tc, x, w_qkv_words, w_qkv_scales, out):
             prod = work.tile([P, HEAD_DIM, 2, GROUP], F32, tag="work", name="prod")
             products(prod, 0, first[0], first[1])
             products(prod, 1, second[0], second[1])
-            late_sums.append((prod, target))
+            fold = FOLD_QK[second[0]]
+            for slot in range(2 if fold else 0):
+                nc.vector.tensor_add(
+                    out=prod[:, 0:fold, slot, :], in0=prod[:, 0:fold, slot, :], in1=prod[:, HEAD_DIM - fold :, slot, :]
+                )
+            late_sums.append((prod, HEAD_DIM - fold, target))
 
-        def finish_tile():
-            prod, target = late_sums[0]
+        def finish_tile(loads=0):
+            prod, count, target = late_sums[0]
             late_sums.remove(late_sums[0])
-            sum_over_channels(prod, target)
+            sum_over_channels(prod, count, target, loads)
 
         def start_pair(half, t):
             start_tile((half, 2 * t), (half, 2 * t + 1), scores[half][:, t, :])
@@ -264,6 +286,7 @@ def tile_relation_kernel(tc, x, w_qkv_words, w_qkv_scales, out):
             nc.scalar.activation(out=flat, in_=flat, func=ACT.Exp)
 
         def softmax_norm(half):
+            weights_ready.add(half)
             att = att_of(half)
             rows_of = att.rearrange("p s o h -> p s (o h)")
             total = small.tile([P, SPOTS, 12 * HH], F32, tag="total", name="total")
@@ -284,20 +307,20 @@ def tile_relation_kernel(tc, x, w_qkv_words, w_qkv_scales, out):
         banks = {}
         filled = {}
 
-        def sum_over_offsets(half, s, weighted):
+        def sum_over_offsets(half, s, weighted, count):
             a, b = divmod(s, PATCH)
             if (half, a) not in filled:
                 banks[half, a] = out_ps.tile([P, PATCH, P], F32, tag="sums", name="sums")
                 filled[half, a] = 0
             bank = banks[half, a]
-            for off in range(OFFSETS):
+            for off in range(count):
                 nc.tensor.matmul(
                     out=bank[:, b, :],
                     lhsT=weighted[:, off, :],
                     rhs=ident[:],
                     is_transpose=True,
                     start=(off == 0),
-                    stop=(off == OFFSETS - 1),
+                    stop=(off == count - 1),
                 )
             filled[half, a] += 1
             if filled[half, a] == PATCH:
@@ -309,32 +332,43 @@ def tile_relation_kernel(tc, x, w_qkv_words, w_qkv_scales, out):
                 )
 
         late_items = []
+        clock = [0]
 
         def vector_item(half, s):
             a, b = divmod(s, PATCH)
             block = work.tile([P, OFFSETS, P], F32, tag="work", name="block")
-            nc.vector.tensor_tensor(
-                out=block[:].rearrange("p (di dj) (h c) -> p di (dj h) c", di=WINDOW, c=HEAD_DIM),
-                in0=v_halo[:, half, a : a + WINDOW, b : b + WINDOW, :].rearrange(
-                    "p u v (h c) -> p u (v h) c", c=HEAD_DIM
-                ),
-                in1=att_of(half)[:, s]
-                .rearrange("p (di dj) h -> p di (dj h)", di=WINDOW)
-                .unsqueeze(3)
-                .to_broadcast([P, WINDOW, WINDOW * HH, HEAD_DIM]),
-                op=ALU.mult,
+            for d0, d1 in ((3, WINDOW), (0, 3)):
+                nc.vector.tensor_tensor(
+                    out=block[:].rearrange("p (di dj) (h c) -> p di (dj h) c", di=WINDOW, c=HEAD_DIM)[:, d0:d1],
+                    in0=v_halo[:, half, a + d0 : a + d1, b : b + WINDOW, :].rearrange(
+                        "p u v (h c) -> p u (v h) c", c=HEAD_DIM
+                    ),
+                    in1=att_of(half)[:, s]
+                    .rearrange("p (di dj) h -> p di (dj h)", di=WINDOW)[:, d0:d1]
+                    .unsqueeze(3)
+                    .to_broadcast([P, d1 - d0, WINDOW * HH, HEAD_DIM]),
+                    op=ALU.mult,
+                )
+            left = OFFSETS - FOLD_AV
+            nc.vector.tensor_add(
+                out=block[:, left - FOLD_AV : left, :], in0=block[:, left - FOLD_AV : left, :], in1=block[:, left:, :]
             )
-            late_items.append((half, s, block))
+            late_items.append((half, s, block, left, -1, clock[0]))
 
         scalar_rows = [(half, s, di) for half in range(HALVES) for s in range(S_ITEMS[half]) for di in range(WINDOW)]
         blocks_s = {}
+        weights_ready = set()
 
         def scalar_work(count):
             for _ in range(min(count, len(scalar_rows))):
                 half, s, di = scalar_rows[0]
+                if half not in weights_ready:
+                    return
                 scalar_rows.remove(scalar_rows[0])
                 a, b = divmod(s, PATCH)
                 if di == 0:
+                    while any(0 <= item[4] < blocks_s.get("next", 0) - 1 for item in late_items):
+                        finish_item()
                     if "pair" not in blocks_s:
                         blocks_s["pair"] = keep.tile([P, 2, OFFSETS, P], F32, tag="k0", align_bytes=64, name="pair_s")
                         blocks_s["next"] = 0
@@ -352,13 +386,17 @@ def tile_relation_kernel(tc, x, w_qkv_words, w_qkv_scales, out):
                             scale=att_of(half)[:, s, off, h : h + 1],
                         )
                 if di == WINDOW - 1:
-                    late_items.append((half, s, block))
+                    late_items.append((half, s, block, OFFSETS, blocks_s["next"] - 1, clock[0]))
 
-        def finish_items(count):
-            for _ in range(count):
-                half, s, block = late_items[0]
-                late_items.remove(late_items[0])
-                sum_over_offsets(half, s, block)
+        def finish_item():
+            half, s, block, count = late_items[0][0:4]
+            late_items.remove(late_items[0])
+            sum_over_offsets(half, s, block, count)
+
+        def finish_earlier():
+            while late_items and late_items[0][5] < clock[0]:
+                finish_item()
+            clock[0] += 1
 
         def store(half):
             nc.sync.dma_start(
@@ -373,26 +411,16 @@ def tile_relation_kernel(tc, x, w_qkv_words, w_qkv_scales, out):
             for v0 in (0, PATCH):
                 for u in range(PATCH):
                     load_k(0, u, v0, v0 == 0 and u % 2 == 1)
-            pending = [(load_k, 0, u, v0) for u in range(PATCH, HALO) for v0 in (0, PATCH)]
+            pending += [(load_k, 0, u, v0) for u in range(PATCH, HALO) for v0 in (0, PATCH)]
             pending += [(load_q, 1, ry, None) for ry in range(PATCH)]
             pending += [(load_k, 1, u, v0) for u in range(HALO) for v0 in (0, PATCH)]
             pending += [(load_v, 0, u, v0) for u in range(HALO) for v0 in range(0, HALO, 2)]
-
-            def some_loads(count):
-                for _ in range(min(count, len(pending))):
-                    load, half, u, v0 = pending[0]
-                    pending.remove(pending[0])
-                    if v0 is None:
-                        load(half, u)
-                    else:
-                        load(half, u, v0)
 
             start_pair(0, 0)
             some_loads(6)
             for t in range(1, PAIRS):
                 start_pair(0, t)
-                finish_tile()
-                some_loads(5)
+                finish_tile(3)
             start_tile((0, OFFSETS - 1), (1, OFFSETS - 1), lone[:])
             finish_tile()
             some_loads(len(pending))
@@ -410,9 +438,8 @@ def tile_relation_kernel(tc, x, w_qkv_words, w_qkv_scales, out):
             for t in range(3, PAIRS):
                 start_pair(1, t)
                 finish_tile()
-                ready = len(late_items)
-                scalar_work(3)
-                finish_items(ready)
+                scalar_work(4)
+                finish_earlier()
             vector_rest = [(half, s) for half in range(HALVES) for s in reversed(range(S_ITEMS[half], SPOTS))]
 
             def vector_work():
@@ -421,28 +448,24 @@ def tile_relation_kernel(tc, x, w_qkv_words, w_qkv_scales, out):
                 vector_item(half, s)
 
             def step(count):
-                ready = len(late_items)
                 if vector_rest:
                     vector_work()
                 scalar_work(count)
-                finish_items(ready)
+                finish_earlier()
 
-            ready = len(late_items)
             vector_work()
             finish_tile()
-            finish_items(ready)
+            finish_earlier()
             softmax_max(1)
-            scalar_work(2)
-            step(2)
+            scalar_work(3)
+            step(3)
             softmax_turn(1)
             softmax_exp(1)
-            step(2)
+            step(3)
             softmax_norm(1)
             stored = 0
-            turn = 0
             while vector_rest or late_items or scalar_rows:
-                step(2 + turn % 2)
-                turn += 1
+                step(3)
                 if stored == 0 and all((0, a) in filled and filled[0, a] == PATCH for a in range(PATCH)):
                     store(0)
                     stored = 1

@@ -28,10 +28,7 @@ REACH = WINDOW // 2
 HALO = PATCH + WINDOW - 1
 PAIRS = OFFSETS // 2
 GROUP = SPOTS * HH
-S_ITEMS = (8, 7)
-
-FOLD_QK = (0, 8)
-FOLD_AV = 5
+S_ITEMS = (8, 6)
 
 FLOPS = 2 * 3 * DEPTH * CHANNELS_IN * PIXELS + 2 * 2 * PIXELS * HEADS * OFFSETS * HEAD_DIM
 
@@ -69,11 +66,11 @@ def tile_relation_kernel(tc, x, w_qkv_words, w_qkv_scales, out):
                 out=w_scales[32 * quad : 32 * quad + 4, :].bitcast(I32),
                 in_=w_qkv_scales[0, 4 * quad : 4 * quad + 4, :].bitcast(I32),
             )
-        nc.gpsimd.memset(x_scales[:].rearrange("p u v q -> p (u v q)").bitcast(I32), 0)
-        nc.gpsimd.memset(x_words[:, PATCH // 2 : PATCH // 2 + PATCH, 0:REACH, :], 0)
-        nc.gpsimd.memset(x_words[:, PATCH // 2 : PATCH // 2 + PATCH, REACH + PATCH : HALO, :], 0)
-        nc.gpsimd.memset(x_words[:, 0:REACH, :, :], 0)
-        nc.gpsimd.memset(x_words[:, REACH + PATCH : HALO, :, :], 0)
+        nc.vector.memset(x_scales[:].rearrange("p u v q -> p (u v q)").bitcast(I32), 0)
+        nc.vector.memset(x_words[:, PATCH // 2 : PATCH // 2 + PATCH, 0:REACH, :], 0)
+        nc.vector.memset(x_words[:, PATCH // 2 : PATCH // 2 + PATCH, REACH + PATCH : HALO, :], 0)
+        nc.vector.memset(x_words[:, 0:REACH, :, :], 0)
+        nc.vector.memset(x_words[:, REACH + PATCH : HALO, :, :], 0)
         spark = small.tile([P, 1], F32)
         nc.vector.memset(spark[:], 0.0)
         nc.scalar.activation(out=spark[:], in_=spark[:], func=ACT.Exp)
@@ -187,10 +184,10 @@ def tile_relation_kernel(tc, x, w_qkv_words, w_qkv_scales, out):
                 else:
                     load(half, u, v0)
 
-        def sum_over_channels(prod, count, target, loads):
+        def sum_over_channels(prod, target, loads):
             score = score_ps.tile([P, P], F32, name="score")
-            for c in range(count):
-                if c == count // 2:
+            for c in range(HEAD_DIM):
+                if c == HEAD_DIM // 2:
                     some_loads(loads)
                 nc.tensor.matmul(
                     out=score[:],
@@ -198,7 +195,7 @@ def tile_relation_kernel(tc, x, w_qkv_words, w_qkv_scales, out):
                     rhs=ident[:],
                     is_transpose=True,
                     start=(c == 0),
-                    stop=(c == count - 1),
+                    stop=(c == HEAD_DIM - 1),
                 )
             nc.scalar.copy(out=target, in_=score[:])
             some_loads(loads)
@@ -209,17 +206,12 @@ def tile_relation_kernel(tc, x, w_qkv_words, w_qkv_scales, out):
             prod = work.tile([P, HEAD_DIM, 2, GROUP], F32, tag="work", name="prod")
             products(prod, 0, first[0], first[1])
             products(prod, 1, second[0], second[1])
-            fold = FOLD_QK[second[0]]
-            for slot in range(2 if fold else 0):
-                nc.vector.tensor_add(
-                    out=prod[:, 0:fold, slot, :], in0=prod[:, 0:fold, slot, :], in1=prod[:, HEAD_DIM - fold :, slot, :]
-                )
-            late_sums.append((prod, HEAD_DIM - fold, target))
+            late_sums.append((prod, target))
 
         def finish_tile(loads=0):
-            prod, count, target = late_sums[0]
+            prod, target = late_sums[0]
             late_sums.remove(late_sums[0])
-            sum_over_channels(prod, count, target, loads)
+            sum_over_channels(prod, target, loads)
 
         def start_pair(half, t):
             start_tile((half, 2 * t), (half, 2 * t + 1), scores[half][:, t, :])
@@ -307,20 +299,20 @@ def tile_relation_kernel(tc, x, w_qkv_words, w_qkv_scales, out):
         banks = {}
         filled = {}
 
-        def sum_over_offsets(half, s, weighted, count):
+        def sum_over_offsets(half, s, weighted):
             a, b = divmod(s, PATCH)
             if (half, a) not in filled:
                 banks[half, a] = out_ps.tile([P, PATCH, P], F32, tag="sums", name="sums")
                 filled[half, a] = 0
             bank = banks[half, a]
-            for off in range(count):
+            for off in range(OFFSETS):
                 nc.tensor.matmul(
                     out=bank[:, b, :],
                     lhsT=weighted[:, off, :],
                     rhs=ident[:],
                     is_transpose=True,
                     start=(off == 0),
-                    stop=(off == count - 1),
+                    stop=(off == OFFSETS - 1),
                 )
             filled[half, a] += 1
             if filled[half, a] == PATCH:
@@ -337,23 +329,18 @@ def tile_relation_kernel(tc, x, w_qkv_words, w_qkv_scales, out):
         def vector_item(half, s):
             a, b = divmod(s, PATCH)
             block = work.tile([P, OFFSETS, P], F32, tag="work", name="block")
-            for d0, d1 in ((3, WINDOW), (0, 3)):
-                nc.vector.tensor_tensor(
-                    out=block[:].rearrange("p (di dj) (h c) -> p di (dj h) c", di=WINDOW, c=HEAD_DIM)[:, d0:d1],
-                    in0=v_halo[:, half, a + d0 : a + d1, b : b + WINDOW, :].rearrange(
-                        "p u v (h c) -> p u (v h) c", c=HEAD_DIM
-                    ),
-                    in1=att_of(half)[:, s]
-                    .rearrange("p (di dj) h -> p di (dj h)", di=WINDOW)[:, d0:d1]
-                    .unsqueeze(3)
-                    .to_broadcast([P, d1 - d0, WINDOW * HH, HEAD_DIM]),
-                    op=ALU.mult,
-                )
-            left = OFFSETS - FOLD_AV
-            nc.vector.tensor_add(
-                out=block[:, left - FOLD_AV : left, :], in0=block[:, left - FOLD_AV : left, :], in1=block[:, left:, :]
+            nc.vector.tensor_tensor(
+                out=block[:].rearrange("p (di dj) (h c) -> p di (dj h) c", di=WINDOW, c=HEAD_DIM),
+                in0=v_halo[:, half, a : a + WINDOW, b : b + WINDOW, :].rearrange(
+                    "p u v (h c) -> p u (v h) c", c=HEAD_DIM
+                ),
+                in1=att_of(half)[:, s]
+                .rearrange("p (di dj) h -> p di (dj h)", di=WINDOW)
+                .unsqueeze(3)
+                .to_broadcast([P, WINDOW, WINDOW * HH, HEAD_DIM]),
+                op=ALU.mult,
             )
-            late_items.append((half, s, block, left, -1, clock[0]))
+            late_items.append((half, s, block, -1, clock[0]))
 
         scalar_rows = [(half, s, di) for half in range(HALVES) for s in range(S_ITEMS[half]) for di in range(WINDOW)]
         blocks_s = {}
@@ -367,7 +354,7 @@ def tile_relation_kernel(tc, x, w_qkv_words, w_qkv_scales, out):
                 scalar_rows.remove(scalar_rows[0])
                 a, b = divmod(s, PATCH)
                 if di == 0:
-                    while any(0 <= item[4] < blocks_s.get("next", 0) - 1 for item in late_items):
+                    while any(0 <= item[3] < blocks_s.get("next", 0) - 1 for item in late_items):
                         finish_item()
                     if "pair" not in blocks_s:
                         blocks_s["pair"] = keep.tile([P, 2, OFFSETS, P], F32, tag="k0", align_bytes=64, name="pair_s")
@@ -386,15 +373,15 @@ def tile_relation_kernel(tc, x, w_qkv_words, w_qkv_scales, out):
                             scale=att_of(half)[:, s, off, h : h + 1],
                         )
                 if di == WINDOW - 1:
-                    late_items.append((half, s, block, OFFSETS, blocks_s["next"] - 1, clock[0]))
+                    late_items.append((half, s, block, blocks_s["next"] - 1, clock[0]))
 
         def finish_item():
-            half, s, block, count = late_items[0][0:4]
+            half, s, block = late_items[0][0:3]
             late_items.remove(late_items[0])
-            sum_over_offsets(half, s, block, count)
+            sum_over_offsets(half, s, block)
 
         def finish_earlier():
-            while late_items and late_items[0][5] < clock[0]:
+            while late_items and late_items[0][4] < clock[0]:
                 finish_item()
             clock[0] += 1
 
@@ -438,7 +425,7 @@ def tile_relation_kernel(tc, x, w_qkv_words, w_qkv_scales, out):
             for t in range(3, PAIRS):
                 start_pair(1, t)
                 finish_tile()
-                scalar_work(4)
+                scalar_work(3)
                 finish_earlier()
             vector_rest = [(half, s) for half in range(HALVES) for s in reversed(range(S_ITEMS[half], SPOTS))]
 
@@ -464,8 +451,10 @@ def tile_relation_kernel(tc, x, w_qkv_words, w_qkv_scales, out):
             step(3)
             softmax_norm(1)
             stored = 0
+            turn = 0
             while vector_rest or late_items or scalar_rows:
-                step(3)
+                step(2 + turn % 2)
+                turn += 1
                 if stored == 0 and all((0, a) in filled and filled[0, a] == PATCH for a in range(PATCH)):
                     store(0)
                     stored = 1

@@ -10,6 +10,7 @@ U8 = mybir.dt.uint8
 FP8X4 = mybir.dt.float8_e4m3fn_x4
 ALU = mybir.AluOpType
 ACT = mybir.ActivationFunctionType
+AX = mybir.AxisListType
 
 P = 128
 PACK = 4
@@ -27,6 +28,7 @@ GRID = SIDE // PATCH
 REACH = WINDOW // 2
 HALO = PATCH + WINDOW - 1
 PAIRS = OFFSETS // 2
+ORDER = (12, 13, 14, 10, 11) + tuple(range(10)) + tuple(range(15, OFFSETS))
 GROUP = SPOTS * HH
 S_ITEMS = (8, 6)
 
@@ -53,7 +55,16 @@ def tile_relation_kernel(tc, x, w_qkv_words, w_qkv_scales, out):
         x_sb = front[:, 0].rearrange("p (t s) -> p t s", t=PACK)
         grouped = front[:, 1].rearrange("p (ry rx q t) -> p ry rx q t", ry=PATCH, rx=PATCH, t=PACK)
 
+        def columns(tile, v0, v1, x0, x1):
+            return tile[:, REACH : REACH + PATCH, v0:v1, :].rearrange("p u v (r x) -> p u (v r) x", x=GRID)[
+                :, :, :, x0:x1
+            ]
+
+        def rows(tile, u0, u1, q0, q1):
+            return tile[:, u0:u1, :, :].rearrange("p u v (n q) -> p u (v n) q", n=IMAGES)[:, :, :, q0:q1]
+
         per_image = SIDE * SIDE
+        per_grid = GRID * GRID
         for n in range(IMAGES):
             nc.scalar.dma_start(
                 out=x_sb[:, :, n * per_image : (n + 1) * per_image],
@@ -67,10 +78,10 @@ def tile_relation_kernel(tc, x, w_qkv_words, w_qkv_scales, out):
                 in_=w_qkv_scales[0, 4 * quad : 4 * quad + 4, :].bitcast(I32),
             )
         nc.vector.memset(x_scales[:].rearrange("p u v q -> p (u v q)").bitcast(I32), 0)
-        nc.vector.memset(x_words[:, PATCH // 2 : PATCH // 2 + PATCH, 0:REACH, :], 0)
-        nc.vector.memset(x_words[:, PATCH // 2 : PATCH // 2 + PATCH, REACH + PATCH : HALO, :], 0)
-        nc.vector.memset(x_words[:, 0:REACH, :, :], 0)
-        nc.vector.memset(x_words[:, REACH + PATCH : HALO, :, :], 0)
+        nc.vector.memset(columns(x_words, 0, 2, 0, PATCH), 0)
+        nc.vector.memset(columns(x_words, 6, 8, GRID - PATCH, GRID), 0)
+        nc.vector.memset(rows(x_words, 0, 2, 0, GRID), 0)
+        nc.vector.memset(rows(x_words, 6, 8, per_grid - GRID, per_grid), 0)
         spark = small.tile([P, 1], F32)
         nc.vector.memset(spark[:], 0.0)
         nc.scalar.activation(out=spark[:], in_=spark[:], func=ACT.Exp)
@@ -79,7 +90,8 @@ def tile_relation_kernel(tc, x, w_qkv_words, w_qkv_scales, out):
             "p t (g ry qx rx) -> p ry rx g qx t", g=IMAGES * GRID, ry=PATCH, qx=GRID, rx=PATCH
         )
         for ry in range(PATCH):
-            nc.vector.tensor_copy(
+            copy = nc.scalar.copy if ry == PATCH - 1 else nc.vector.tensor_copy
+            copy(
                 out=grouped[:, ry].rearrange("p rx (g qx) t -> p rx g qx t", qx=GRID), in_=by_spot[:, ry]
             )
         for ry in range(PATCH):
@@ -90,18 +102,9 @@ def tile_relation_kernel(tc, x, w_qkv_words, w_qkv_scales, out):
                 in_=grouped[:, ry].rearrange("p rx q t -> p (rx q t)"),
             )
 
-        def columns(tile, v0, v1, x0, x1):
-            return tile[:, REACH : REACH + PATCH, v0:v1, :].rearrange("p u v (r x) -> p u (v r) x", x=GRID)[
-                :, :, :, x0:x1
-            ]
-
-        def rows(tile, u0, u1, q0, q1):
-            return tile[:, u0:u1, :, :].rearrange("p u v (n q) -> p u (v n) q", n=IMAGES)[:, :, :, q0:q1]
-
         scale_words = x_scales[:].rearrange("p u v q -> p (u v q)").bitcast(I32).rearrange(
             "p (u v q) -> p u v q", u=HALO, v=HALO
         )
-        per_grid = GRID * GRID
         for tile in (x_words, x_scales):
             nc.vector.tensor_copy(out=columns(tile, 0, 2, 1, GRID), in_=columns(tile, 4, 6, 0, GRID - 1))
             nc.vector.tensor_copy(out=columns(tile, 6, 8, 0, GRID - 1), in_=columns(tile, 2, 4, 1, GRID))
@@ -109,14 +112,14 @@ def tile_relation_kernel(tc, x, w_qkv_words, w_qkv_scales, out):
             nc.vector.tensor_copy(out=rows(tile, 0, 2, row, size), in_=rows(tile, 4, 6, 0, size - row))
             nc.vector.tensor_copy(out=rows(tile, 6, 8, 0, size - row), in_=rows(tile, 2, 4, row, size))
 
-        def convolve(first, wide, u, v0):
+        def convolve(first, wide, u, vs):
             bank = stage_ps.tile([P, PATCH * P // wide, wide], F32, tag="stage", name="bank")
             cols = slice(first, first + wide)
-            for j in range(PATCH * P // wide):
+            for j, v in enumerate(vs):
                 nc.tensor.matmul_mx(
                     out=bank[:, j, :],
-                    lhsT=x_words[:, u, v0 + j, :].bitcast(FP8X4),
-                    lhsT_scale=x_scales[:, u, v0 + j, :],
+                    lhsT=x_words[:, u, v, :].bitcast(FP8X4),
+                    lhsT_scale=x_scales[:, u, v, :],
                     rhs=w_words[:, cols].bitcast(FP8X4),
                     rhs_scale=w_scales[:, cols],
                     start=True,
@@ -124,39 +127,39 @@ def tile_relation_kernel(tc, x, w_qkv_words, w_qkv_scales, out):
                 )
             return bank
 
-        def leave(on_vector, out_ap, in_ap):
-            if on_vector:
-                nc.vector.tensor_copy(out=out_ap, in_=in_ap)
-            else:
-                nc.scalar.copy(out=out_ap, in_=in_ap)
-
         q_own = [None, None]
         k_halo = [None, None]
 
-        def load_q(half, ry, on_vector=False):
+        def load_q(half, ry):
             if q_own[half] is None:
                 q_own[half] = keep.tile([P, HEAD_DIM, SPOTS, HH], F32, name="q%d" % half)
-            bank = convolve(half * P, P, REACH + ry, REACH)
-            leave(
-                on_vector,
-                q_own[half][:, :, ry * PATCH : (ry + 1) * PATCH, :],
-                bank[:].rearrange("p r (h c) -> p c r h", c=HEAD_DIM),
+            bank = convolve(half * P, P, REACH + ry, range(REACH, REACH + PATCH))
+            nc.scalar.copy(
+                out=q_own[half][:, :, ry * PATCH : (ry + 1) * PATCH, :],
+                in_=bank[:].rearrange("p r (h c) -> p c r h", c=HEAD_DIM),
             )
 
-        def load_k(half, u, v0, on_vector=False):
+        def load_k(half, u, vs):
             if k_halo[half] is None:
-                k_halo[half] = keep.tile([P, HEAD_DIM, HALO, HALO, HH], F32, tag="k%d" % half, align_bytes=64, name="k%d" % half)
-            bank = convolve(DEPTH + half * P, P, u, v0)
-            leave(
-                on_vector,
-                k_halo[half][:, :, u, v0 : v0 + PATCH, :],
-                bank[:].rearrange("p r (h c) -> p c r h", c=HEAD_DIM),
-            )
+                k_halo[half] = keep.tile(
+                    [P, HEAD_DIM, HALO, HALO, HH], F32, tag="k%d" % half, align_bytes=64, name="k%d" % half
+                )
+            bank = convolve(DEPTH + half * P, P, u, vs)
+            row = k_halo[half][:, :, u, :, :]
+            if vs[3] - vs[0] == 3:
+                nc.scalar.copy(
+                    out=row[:, :, vs[0] : vs[0] + PATCH, :], in_=bank[:].rearrange("p r (h c) -> p c r h", c=HEAD_DIM)
+                )
+            else:
+                nc.scalar.copy(
+                    out=row.rearrange("p c (g w) h -> p c g w h", w=2)[:, :, 0:4:3],
+                    in_=bank[:].rearrange("p (g w) (h c) -> p c g w h", w=2, c=HEAD_DIM),
+                )
 
         v_halo = keep.tile([P, HALVES, HALO, HALO, P], F32, tag="v", align_bytes=64, name="v_halo")
 
-        def load_v(half, u, v0):
-            bank = convolve(2 * DEPTH, DEPTH, u, v0)
+        def load_v(u, v0):
+            bank = convolve(2 * DEPTH, DEPTH, u, (v0, v0 + 1))
             nc.scalar.copy(
                 out=v_halo[:, :, u, v0 : v0 + 2, :], in_=bank[:].rearrange("p r (f d) -> p f r d", f=HALVES)
             )
@@ -177,12 +180,9 @@ def tile_relation_kernel(tc, x, w_qkv_words, w_qkv_scales, out):
 
         def some_loads(count):
             for _ in range(min(count, len(pending))):
-                load, half, u, v0 = pending[0]
-                pending.remove(pending[0])
-                if v0 is None:
-                    load(half, u)
-                else:
-                    load(half, u, v0)
+                load = pending[0]
+                pending.remove(load)
+                load[0](*load[1:])
 
         def sum_over_channels(prod, target, loads):
             score = score_ps.tile([P, P], F32, name="score")
@@ -214,7 +214,7 @@ def tile_relation_kernel(tc, x, w_qkv_words, w_qkv_scales, out):
             sum_over_channels(prod, target, loads)
 
         def start_pair(half, t):
-            start_tile((half, 2 * t), (half, 2 * t + 1), scores[half][:, t, :])
+            start_tile((half, ORDER[2 * t]), (half, ORDER[2 * t + 1]), scores[half][:, t, :])
 
         late = [None]
 
@@ -231,29 +231,30 @@ def tile_relation_kernel(tc, x, w_qkv_words, w_qkv_scales, out):
             base = 2 * OFFSETS * GROUP + half * PIXELS
             return late[0][:, base : base + PIXELS]
 
-        lone_patch = keep.tile([P, HALVES, GROUP], F32, name="lone_patch")
         tops = [small.tile([P, SPOTS, HH], F32, name="top%d" % half) for half in range(HALVES)]
-        trees = [None, None]
+        tree = small.tile([P, 4, P], F32)
+        total = small.tile([P, SPOTS, 13 * HH], F32)
+        both = [small.tile([P, 3, GROUP], F32, name="both%d" % half) for half in range(HALVES)]
         raw = {}
 
-        def softmax_max(half):
-            tree = small.tile([P, PAIRS // 2, P], F32, tag="tree", name="tree")
-            trees[half] = tree
-            nc.vector.tensor_max(out=tree[:], in0=scores[half][:, 0:6, :], in1=scores[half][:, 6:12, :])
-            nc.vector.tensor_max(out=tree[:, 0:3, :], in0=tree[:, 0:3, :], in1=tree[:, 3:6, :])
-            nc.vector.tensor_max(out=tree[:, 0, :], in0=tree[:, 0, :], in1=tree[:, 1, :])
-            nc.vector.tensor_max(out=tree[:, 0, :], in0=tree[:, 0, :], in1=tree[:, 2, :])
+        def softmax_max(half, quarter):
+            three = scores[half][:, 3 * quarter : 3 * quarter + 3, :]
+            before = scores[half][:, 0:3, :] if quarter == 1 else tree[:, 0:3, :]
+            nc.vector.tensor_max(out=tree[:, 0:3, :], in0=before, in1=three)
+            if quarter == 3:
+                nc.vector.tensor_reduce(
+                    out=tree[:, 3, :], in_=tree[:, 0:3, :].rearrange("p k q -> p q k"), axis=AX.X, op=ALU.max
+                )
 
         def softmax_turn(half):
             bank = stage_ps.tile([P, PATCH, P], F32, tag="stage", name="bank")
             if half == 0:
                 nc.tensor.transpose(out=bank[:, 0, :], in_=lone[:], identity=ident[:])
-            nc.tensor.transpose(out=bank[:, 1, :], in_=trees[half][:, 0, :], identity=ident[:])
-            both = small.tile([P, 2, SPOTS, HH], F32, tag="both", name="both")
-            raw[half, "both"] = both
+            nc.tensor.transpose(out=bank[:, 1, :], in_=tree[:, 3, :], identity=ident[:])
             if half == 0:
-                nc.scalar.copy(out=lone_patch[:].rearrange("p f g -> p (f g)"), in_=bank[:, 0, :])
-            nc.scalar.copy(out=both[:].rearrange("p f s h -> p (f s h)"), in_=bank[:, 1, :])
+                for other in range(HALVES):
+                    nc.scalar.copy(out=both[other][:, 2, :], in_=bank[:, 0, other * GROUP : (other + 1) * GROUP])
+            nc.scalar.copy(out=both[half][:, 0:2, :].rearrange("p f g -> p (f g)"), in_=bank[:, 1, :])
             for k in range(PAIRS // 4):
                 bank = stage_ps.tile([P, PATCH, P], F32, tag="stage", name="bank")
                 raw[half, k] = bank
@@ -262,18 +263,31 @@ def tile_relation_kernel(tc, x, w_qkv_words, w_qkv_scales, out):
 
         def softmax_exp(half):
             top = tops[half]
-            both = raw[half, "both"]
-            own = lone_patch[:, half, :].rearrange("p (s h) -> p s h", h=HH)
             by_offset = att_of(half).rearrange("p s o h -> p o s h")
-            nc.vector.tensor_max(out=top[:], in0=both[:, 0], in1=both[:, 1])
-            nc.vector.tensor_max(out=top[:], in0=top[:], in1=own)
-            nc.vector.tensor_sub(out=by_offset[:, OFFSETS - 1], in0=own, in1=top[:])
+            nc.vector.tensor_reduce(
+                out=top[:].rearrange("p s h -> p (s h)"),
+                in_=both[half][:].rearrange("p f g -> p g f"),
+                axis=AX.X,
+                op=ALU.max,
+            )
             for k in range(PAIRS // 4):
-                nc.vector.tensor_sub(
-                    out=by_offset[:, 8 * k : 8 * k + 8],
-                    in0=raw[half, k][:].rearrange("p t (o s h) -> p (t o) s h", o=2, h=HH),
-                    in1=top[:].unsqueeze(1).to_broadcast([P, 8, SPOTS, HH]),
-                )
+                scored = raw[half, k][:].rearrange("p t (o s h) -> p (t o) s h", o=2, h=HH)
+                first = 0
+                while first < 8:
+                    place = ORDER[8 * k + first]
+                    size = 1
+                    while first + size < 8 and ORDER[8 * k + first + size] == place + size:
+                        size += 1
+                    nc.vector.tensor_sub(
+                        out=by_offset[:, place : place + size],
+                        in0=scored[:, first : first + size],
+                        in1=top[:].unsqueeze(1).to_broadcast([P, size, SPOTS, HH]),
+                    )
+                    first += size
+            nc.vector.tensor_sub(
+                out=by_offset[:, OFFSETS - 1], in0=both[half][:, 2, :].rearrange("p (s h) -> p s h", h=HH), in1=top[:]
+            )
+            nc.scalar.activation(out=total[:, :, 12 * HH :], in_=by_offset[:, OFFSETS - 1], func=ACT.Exp)
             flat = att_of(half).rearrange("p s o h -> p (s o h)")
             nc.scalar.activation(out=flat, in_=flat, func=ACT.Exp)
 
@@ -281,17 +295,19 @@ def tile_relation_kernel(tc, x, w_qkv_words, w_qkv_scales, out):
             weights_ready.add(half)
             att = att_of(half)
             rows_of = att.rearrange("p s o h -> p s (o h)")
-            total = small.tile([P, SPOTS, 12 * HH], F32, tag="total", name="total")
-            nc.vector.tensor_add(out=total[:], in0=rows_of[:, :, 0 : 12 * HH], in1=rows_of[:, :, 12 * HH : 24 * HH])
-            for n in (6, 3):
-                nc.vector.tensor_add(
-                    out=total[:, :, 0 : n * HH], in0=total[:, :, 0 : n * HH], in1=total[:, :, n * HH : 2 * n * HH]
-                )
-            sums = total[:, :, 0:HH]
-            nc.vector.tensor_add(out=sums, in0=sums, in1=total[:, :, HH : 2 * HH])
-            nc.vector.tensor_add(out=sums, in0=sums, in1=total[:, :, 2 * HH : 3 * HH])
-            nc.vector.tensor_add(out=sums, in0=sums, in1=att[:, :, OFFSETS - 1, :])
-            nc.vector.reciprocal(out=tops[half][:], in_=sums)
+            nc.vector.tensor_add(
+                out=total[:, :, 0 : 12 * HH], in0=rows_of[:, :, 0 : 12 * HH], in1=rows_of[:, :, 12 * HH : 24 * HH]
+            )
+            nc.vector.tensor_add(
+                out=total[:, :, 6 * HH : 12 * HH], in0=total[:, :, 0 : 6 * HH], in1=total[:, :, 6 * HH : 12 * HH]
+            )
+            nc.vector.tensor_reduce(
+                out=tops[half][:],
+                in_=total[:, :, 6 * HH :].rearrange("p s (o h) -> p s h o", h=HH),
+                axis=AX.X,
+                op=ALU.add,
+            )
+            nc.vector.reciprocal(out=tops[half][:], in_=tops[half][:])
             nc.vector.tensor_tensor(
                 out=att, in0=att, in1=tops[half][:].unsqueeze(2).to_broadcast([P, SPOTS, OFFSETS, HH]), op=ALU.mult
             )
@@ -393,28 +409,31 @@ def tile_relation_kernel(tc, x, w_qkv_words, w_qkv_scales, out):
 
         pinned = {mybir.EngineType.PE, mybir.EngineType.Activation, mybir.EngineType.DVE}
         with tc.manual_schedule(engines=pinned):
-            for ry in range(PATCH):
-                load_q(0, ry, ry % 2 == 1)
-            for v0 in (0, PATCH):
-                for u in range(PATCH):
-                    load_k(0, u, v0, v0 == 0 and u % 2 == 1)
-            pending += [(load_k, 0, u, v0) for u in range(PATCH, HALO) for v0 in (0, PATCH)]
-            pending += [(load_q, 1, ry, None) for ry in range(PATCH)]
-            pending += [(load_k, 1, u, v0) for u in range(HALO) for v0 in (0, PATCH)]
-            pending += [(load_v, 0, u, v0) for u in range(HALO) for v0 in range(0, HALO, 2)]
+            def key_loads(half):
+                loads = [(load_k, half, u, (2, 3, 4, 5)) for u in range(REACH, REACH + PATCH)]
+                loads += [(load_k, half, u, (0, 1, 6, 7)) for u in range(REACH, REACH + PATCH)]
+                loads += [(load_k, half, u, vs) for u in (0, 1, 6, 7) for vs in ((0, 1, 2, 3), (4, 5, 6, 7))]
+                return loads
+
+            pending += [(load_q, 0, ry) for ry in range(PATCH)] + key_loads(0)
+            some_loads(12)
+            pending += [(load_q, 1, ry) for ry in range(PATCH)] + key_loads(1)
+            pending += [(load_v, u, v0) for u in range(HALO) for v0 in range(0, HALO, 2)]
 
             start_pair(0, 0)
             some_loads(6)
             for t in range(1, PAIRS):
                 start_pair(0, t)
                 finish_tile(3)
+                if t in (7, 10):
+                    softmax_max(0, (t - 4) // 3)
             start_tile((0, OFFSETS - 1), (1, OFFSETS - 1), lone[:])
             finish_tile()
             some_loads(len(pending))
             scores[1] = keep.tile([P, PAIRS, P], F32, tag="scales", align_bytes=64, name="scores1")
             start_pair(1, 0)
             finish_tile()
-            softmax_max(0)
+            softmax_max(0, 3)
             start_pair(1, 1)
             finish_tile()
             softmax_turn(0)
@@ -425,6 +444,8 @@ def tile_relation_kernel(tc, x, w_qkv_words, w_qkv_scales, out):
             for t in range(3, PAIRS):
                 start_pair(1, t)
                 finish_tile()
+                if t in (7, 10):
+                    softmax_max(1, (t - 4) // 3)
                 scalar_work(3)
                 finish_earlier()
             vector_rest = [(half, s) for half in range(HALVES) for s in reversed(range(S_ITEMS[half], SPOTS))]
@@ -443,9 +464,9 @@ def tile_relation_kernel(tc, x, w_qkv_words, w_qkv_scales, out):
             vector_work()
             finish_tile()
             finish_earlier()
-            softmax_max(1)
-            scalar_work(3)
-            step(3)
+            softmax_max(1, 3)
+            scalar_work(2)
+            step(2)
             softmax_turn(1)
             softmax_exp(1)
             step(3)

@@ -30,7 +30,11 @@ HALO = PATCH + WINDOW - 1
 PAIRS = OFFSETS // 2
 ORDER = (12, 13, 14, 10, 11) + tuple(range(10)) + tuple(range(15, OFFSETS))
 GROUP = SPOTS * HH
-S_ITEMS = (8, 6)
+S_ITEMS = (8, 7)
+
+FOLD_QK = 6
+FOLD_AV = 5
+RING = 4
 
 FLOPS = 2 * 3 * DEPTH * CHANNELS_IN * PIXELS + 2 * 2 * PIXELS * HEADS * OFFSETS * HEAD_DIM
 
@@ -39,7 +43,7 @@ def tile_relation_kernel(tc, x, w_qkv_words, w_qkv_scales, out):
     nc = tc.nc
     with ExitStack() as whole:
         keep = whole.enter_context(tc.tile_pool(name="keep", bufs=1))
-        work = whole.enter_context(tc.tile_pool(name="work", bufs=2))
+        work = whole.enter_context(tc.tile_pool(name="work", bufs=RING))
         small = whole.enter_context(tc.tile_pool(name="small", bufs=1))
         stage_ps = whole.enter_context(tc.psum_pool(name="stage_ps", bufs=3))
         score_ps = whole.enter_context(tc.psum_pool(name="score_ps", bufs=2))
@@ -167,12 +171,14 @@ def tile_relation_kernel(tc, x, w_qkv_words, w_qkv_scales, out):
         scores = [keep.tile([P, PAIRS, P], F32, name="scores0"), None]
         lone = keep.tile([P, P], F32, name="lone")
 
-        def products(prod, slot, half, offset):
+        def products(block, channels, slot, half, offset):
             di, dj = divmod(offset, WINDOW)
             nc.vector.tensor_tensor(
-                out=prod[:, :, slot, :].rearrange("p c (a g) -> p c a g", a=PATCH),
-                in0=q_own[half][:].rearrange("p c (a b) h -> p c a (b h)", a=PATCH),
-                in1=k_halo[half][:, :, di : di + PATCH, dj : dj + PATCH, :].rearrange("p c a b h -> p c a (b h)"),
+                out=block[:, :, slot, :].rearrange("p c (a g) -> p c a g", a=PATCH),
+                in0=q_own[half][:, channels].rearrange("p c (a b) h -> p c a (b h)", a=PATCH),
+                in1=k_halo[half][:, channels, di : di + PATCH, dj : dj + PATCH, :].rearrange(
+                    "p c a b h -> p c a (b h)"
+                ),
                 op=ALU.mult,
             )
 
@@ -184,37 +190,51 @@ def tile_relation_kernel(tc, x, w_qkv_words, w_qkv_scales, out):
                 pending.remove(load)
                 load[0](*load[1:])
 
-        def sum_over_channels(prod, target, loads):
-            score = score_ps.tile([P, P], F32, name="score")
-            for c in range(HEAD_DIM):
-                if c == HEAD_DIM // 2:
+        def add_up(out_ap, planes, loads=0):
+            for n, plane in enumerate(planes):
+                if n == len(planes) // 2:
                     some_loads(loads)
                 nc.tensor.matmul(
-                    out=score[:],
-                    lhsT=prod[:, c, :, :].rearrange("p o g -> p (o g)"),
+                    out=out_ap,
+                    lhsT=plane,
                     rhs=ident[:],
                     is_transpose=True,
-                    start=(c == 0),
-                    stop=(c == HEAD_DIM - 1),
+                    start=(n == 0),
+                    stop=(n == len(planes) - 1),
                 )
+
+        late_sums = []
+        PIECE = HEAD_DIM // 2
+
+        def start_tile(first, second, target, fold=0):
+            blocks = []
+            for n in range(2):
+                block = work.tile([P, PIECE, 2, GROUP], F32, tag="work", name="prod")
+                blocks.append(block)
+                channels = slice(n * PIECE, (n + 1) * PIECE)
+                products(block, channels, 0, first[0], first[1])
+                if n == 1 and fold:
+                    nc.vector.tensor_add(
+                        out=blocks[0][:, 0:fold], in0=blocks[0][:, 0:fold], in1=blocks[0][:, PIECE - fold :]
+                    )
+                products(block, channels, 1, second[0], second[1])
+            planes = [
+                block[:, c].rearrange("p o g -> p (o g)")
+                for block, count in zip(blocks, (PIECE - fold, PIECE))
+                for c in range(count)
+            ]
+            late_sums.append((planes, target))
+
+        def finish_tile(loads=0):
+            planes, target = late_sums[0]
+            late_sums.remove(late_sums[0])
+            score = score_ps.tile([P, P], F32, name="score")
+            add_up(score[:], planes, loads)
             nc.scalar.copy(out=target, in_=score[:])
             some_loads(loads)
 
-        late_sums = []
-
-        def start_tile(first, second, target):
-            prod = work.tile([P, HEAD_DIM, 2, GROUP], F32, tag="work", name="prod")
-            products(prod, 0, first[0], first[1])
-            products(prod, 1, second[0], second[1])
-            late_sums.append((prod, target))
-
-        def finish_tile(loads=0):
-            prod, target = late_sums[0]
-            late_sums.remove(late_sums[0])
-            sum_over_channels(prod, target, loads)
-
-        def start_pair(half, t):
-            start_tile((half, ORDER[2 * t]), (half, ORDER[2 * t + 1]), scores[half][:, t, :])
+        def start_pair(half, t, fold=0):
+            start_tile((half, ORDER[2 * t]), (half, ORDER[2 * t + 1]), scores[half][:, t, :], fold)
 
         late = [None]
 
@@ -315,21 +335,13 @@ def tile_relation_kernel(tc, x, w_qkv_words, w_qkv_scales, out):
         banks = {}
         filled = {}
 
-        def sum_over_offsets(half, s, weighted):
+        def sum_over_offsets(half, s, planes):
             a, b = divmod(s, PATCH)
             if (half, a) not in filled:
                 banks[half, a] = out_ps.tile([P, PATCH, P], F32, tag="sums", name="sums")
                 filled[half, a] = 0
             bank = banks[half, a]
-            for off in range(OFFSETS):
-                nc.tensor.matmul(
-                    out=bank[:, b, :],
-                    lhsT=weighted[:, off, :],
-                    rhs=ident[:],
-                    is_transpose=True,
-                    start=(off == 0),
-                    stop=(off == OFFSETS - 1),
-                )
+            add_up(bank[:, b, :], planes)
             filled[half, a] += 1
             if filled[half, a] == PATCH:
                 nc.scalar.copy(
@@ -344,19 +356,29 @@ def tile_relation_kernel(tc, x, w_qkv_words, w_qkv_scales, out):
 
         def vector_item(half, s):
             a, b = divmod(s, PATCH)
-            block = work.tile([P, OFFSETS, P], F32, tag="work", name="block")
-            nc.vector.tensor_tensor(
-                out=block[:].rearrange("p (di dj) (h c) -> p di (dj h) c", di=WINDOW, c=HEAD_DIM),
-                in0=v_halo[:, half, a : a + WINDOW, b : b + WINDOW, :].rearrange(
-                    "p u v (h c) -> p u (v h) c", c=HEAD_DIM
-                ),
-                in1=att_of(half)[:, s]
-                .rearrange("p (di dj) h -> p di (dj h)", di=WINDOW)
-                .unsqueeze(3)
-                .to_broadcast([P, WINDOW, WINDOW * HH, HEAD_DIM]),
-                op=ALU.mult,
+            blocks = []
+            for d0, d1 in ((0, 3), (3, WINDOW)):
+                block = work.tile([P, (d1 - d0) * WINDOW, P], F32, tag="work", name="block")
+                blocks.append(block)
+                nc.vector.tensor_tensor(
+                    out=block[:].rearrange("p (di dj) (h c) -> p di (dj h) c", di=d1 - d0, c=HEAD_DIM),
+                    in0=v_halo[:, half, a + d0 : a + d1, b : b + WINDOW, :].rearrange(
+                        "p u v (h c) -> p u (v h) c", c=HEAD_DIM
+                    ),
+                    in1=att_of(half)[:, s]
+                    .rearrange("p (di dj) h -> p di (dj h)", di=WINDOW)[:, d0:d1]
+                    .unsqueeze(3)
+                    .to_broadcast([P, d1 - d0, WINDOW * HH, HEAD_DIM]),
+                    op=ALU.mult,
+                )
+            left = 3 * WINDOW - FOLD_AV
+            nc.vector.tensor_add(
+                out=blocks[0][:, left - FOLD_AV : left],
+                in0=blocks[0][:, left - FOLD_AV : left],
+                in1=blocks[0][:, left:],
             )
-            late_items.append((half, s, block, -1, clock[0]))
+            planes = [blocks[0][:, n] for n in range(left)] + [blocks[1][:, n] for n in range(2 * WINDOW)]
+            late_items.append((half, s, planes, -1, clock[0]))
 
         scalar_rows = [(half, s, di) for half in range(HALVES) for s in range(S_ITEMS[half]) for di in range(WINDOW)]
         blocks_s = {}
@@ -389,12 +411,13 @@ def tile_relation_kernel(tc, x, w_qkv_words, w_qkv_scales, out):
                             scale=att_of(half)[:, s, off, h : h + 1],
                         )
                 if di == WINDOW - 1:
-                    late_items.append((half, s, block, blocks_s["next"] - 1, clock[0]))
+                    planes = [block[:, off] for off in range(OFFSETS)]
+                    late_items.append((half, s, planes, blocks_s["next"] - 1, clock[0]))
 
         def finish_item():
-            half, s, block = late_items[0][0:3]
+            half, s, planes = late_items[0][0:3]
             late_items.remove(late_items[0])
-            sum_over_offsets(half, s, block)
+            sum_over_offsets(half, s, planes)
 
         def finish_earlier():
             while late_items and late_items[0][4] < clock[0]:
@@ -424,7 +447,7 @@ def tile_relation_kernel(tc, x, w_qkv_words, w_qkv_scales, out):
             some_loads(6)
             for t in range(1, PAIRS):
                 start_pair(0, t)
-                finish_tile(3)
+                finish_tile(4)
                 if t in (7, 10):
                     softmax_max(0, (t - 4) // 3)
             start_tile((0, OFFSETS - 1), (1, OFFSETS - 1), lone[:])
@@ -442,7 +465,7 @@ def tile_relation_kernel(tc, x, w_qkv_words, w_qkv_scales, out):
             finish_tile()
             softmax_norm(0)
             for t in range(3, PAIRS):
-                start_pair(1, t)
+                start_pair(1, t, FOLD_QK)
                 finish_tile()
                 if t in (7, 10):
                     softmax_max(1, (t - 4) // 3)
@@ -472,10 +495,8 @@ def tile_relation_kernel(tc, x, w_qkv_words, w_qkv_scales, out):
             step(3)
             softmax_norm(1)
             stored = 0
-            turn = 0
             while vector_rest or late_items or scalar_rows:
-                step(2 + turn % 2)
-                turn += 1
+                step(3)
                 if stored == 0 and all((0, a) in filled and filled[0, a] == PATCH for a in range(PATCH)):
                     store(0)
                     stored = 1

@@ -30,10 +30,10 @@ HALO = PATCH + WINDOW - 1
 PAIRS = OFFSETS // 2
 ORDER = (12, 13, 14, 10, 11) + tuple(range(10)) + tuple(range(15, OFFSETS))
 GROUP = SPOTS * HH
-S_ITEMS = (8, 7)
+S_ITEMS = (8, 6)
 
-FOLD_QK = 6
-FOLD_AV = 5
+FOLD_QK = ((8, 2), (6, 0))
+FOLD_AV = (7, 5)
 RING = 4
 
 FLOPS = 2 * 3 * DEPTH * CHANNELS_IN * PIXELS + 2 * 2 * PIXELS * HEADS * OFFSETS * HEAD_DIM
@@ -45,6 +45,7 @@ def tile_relation_kernel(tc, x, w_qkv_words, w_qkv_scales, out):
         keep = whole.enter_context(tc.tile_pool(name="keep", bufs=1))
         work = whole.enter_context(tc.tile_pool(name="work", bufs=RING))
         small = whole.enter_context(tc.tile_pool(name="small", bufs=1))
+        turns = whole.enter_context(tc.tile_pool(name="turns", bufs=2))
         stage_ps = whole.enter_context(tc.psum_pool(name="stage_ps", bufs=3))
         score_ps = whole.enter_context(tc.psum_pool(name="score_ps", bufs=2))
         out_ps = whole.enter_context(tc.psum_pool(name="out_ps", bufs=3))
@@ -206,35 +207,47 @@ def tile_relation_kernel(tc, x, w_qkv_words, w_qkv_scales, out):
         late_sums = []
         PIECE = HEAD_DIM // 2
 
-        def start_tile(first, second, target, fold=0):
+        late_folds = []
+
+        def fold_block(block, fold):
+            nc.vector.tensor_add(out=block[:, 0:fold], in0=block[:, 0:fold], in1=block[:, PIECE - fold :])
+
+        def fold_earlier():
+            while late_folds:
+                fold_block(*late_folds[0])
+                late_folds.remove(late_folds[0])
+
+        def start_tile(first, second, target, folds=(0, 0)):
             blocks = []
             for n in range(2):
                 block = work.tile([P, PIECE, 2, GROUP], F32, tag="work", name="prod")
                 blocks.append(block)
                 channels = slice(n * PIECE, (n + 1) * PIECE)
                 products(block, channels, 0, first[0], first[1])
-                if n == 1 and fold:
-                    nc.vector.tensor_add(
-                        out=blocks[0][:, 0:fold], in0=blocks[0][:, 0:fold], in1=blocks[0][:, PIECE - fold :]
-                    )
+                if n == 0:
+                    fold_earlier()
+                elif folds[0]:
+                    fold_block(blocks[0], folds[0])
                 products(block, channels, 1, second[0], second[1])
+            if folds[1]:
+                late_folds.append((blocks[1], folds[1]))
             planes = [
                 block[:, c].rearrange("p o g -> p (o g)")
-                for block, count in zip(blocks, (PIECE - fold, PIECE))
-                for c in range(count)
+                for block, fold in zip(blocks, folds)
+                for c in range(PIECE - fold)
             ]
             late_sums.append((planes, target))
 
         def finish_tile(loads=0):
             planes, target = late_sums[0]
             late_sums.remove(late_sums[0])
-            score = score_ps.tile([P, P], F32, name="score")
+            score = score_ps.tile([P, P], F32, tag="score", name="score")
             add_up(score[:], planes, loads)
             nc.scalar.copy(out=target, in_=score[:])
             some_loads(loads)
 
-        def start_pair(half, t, fold=0):
-            start_tile((half, ORDER[2 * t]), (half, ORDER[2 * t + 1]), scores[half][:, t, :], fold)
+        def start_pair(half, t, folds=(0, 0)):
+            start_tile((half, ORDER[2 * t]), (half, ORDER[2 * t + 1]), scores[half][:, t, :], folds)
 
         late = [None]
 
@@ -354,30 +367,58 @@ def tile_relation_kernel(tc, x, w_qkv_words, w_qkv_scales, out):
         late_items = []
         clock = [0]
 
+        per_spot = OFFSETS * HH
+        per_row = PATCH * per_spot
+        pieces = (0, P, 2 * P, per_row - P)
+        turned = {}
+        weight_banks = {}
+
+        def turn_weights(half, a):
+            first = half * OFFSETS * GROUP + a * per_row
+            bank = stage_ps.tile([P, PATCH, P], F32, tag="stage", name="bank")
+            for j, piece in enumerate(pieces):
+                nc.tensor.transpose(
+                    out=bank[:, j, :], in_=late[0][:, first + piece : first + piece + P], identity=ident[:]
+                )
+            turned[half, a] = turns.tile([P, len(pieces), P], F32, tag="turned", name="turned")
+            nc.scalar.copy(out=turned[half, a][:], in_=bank[:])
+
+        def return_weights(half, a):
+            weight_banks[half, a] = score_ps.tile([P, PATCH * P], F32, tag="score", name="weights")
+            for j, piece in enumerate(pieces):
+                nc.tensor.transpose(
+                    out=weight_banks[half, a][:, piece : piece + P], in_=turned[half, a][:, j, :], identity=ident[:]
+                )
+
+        second_blocks = []
+
         def vector_item(half, s):
             a, b = divmod(s, PATCH)
-            blocks = []
-            for d0, d1 in ((0, 3), (3, WINDOW)):
-                block = work.tile([P, (d1 - d0) * WINDOW, P], F32, tag="work", name="block")
-                blocks.append(block)
+            if not second_blocks:
+                second_blocks.append(
+                    keep.tile([P, 4, 2 * WINDOW, P], F32, tag="k1", align_bytes=64, name="second_blocks")
+                )
+            first_block = work.tile([P, 3 * WINDOW, P], F32, tag="work", name="block")
+            blocks = (first_block[:], second_blocks[0][:, (len(second_blocks) - 1) % 4])
+            second_blocks.append(s)
+            planes = []
+            for block, d0, d1, fold in ((blocks[0], 0, 3, FOLD_AV[0]), (blocks[1], 3, WINDOW, FOLD_AV[1])):
                 nc.vector.tensor_tensor(
-                    out=block[:].rearrange("p (di dj) (h c) -> p di (dj h) c", di=d1 - d0, c=HEAD_DIM),
+                    out=block.rearrange("p (di dj) (h c) -> p di (dj h) c", di=d1 - d0, c=HEAD_DIM),
                     in0=v_halo[:, half, a + d0 : a + d1, b : b + WINDOW, :].rearrange(
                         "p u v (h c) -> p u (v h) c", c=HEAD_DIM
                     ),
-                    in1=att_of(half)[:, s]
-                    .rearrange("p (di dj) h -> p di (dj h)", di=WINDOW)[:, d0:d1]
+                    in1=weight_banks[half, a][:, b * per_spot : (b + 1) * per_spot]
+                    .rearrange("p (di x) -> p di x", di=WINDOW)[:, d0:d1]
                     .unsqueeze(3)
                     .to_broadcast([P, d1 - d0, WINDOW * HH, HEAD_DIM]),
                     op=ALU.mult,
                 )
-            left = 3 * WINDOW - FOLD_AV
-            nc.vector.tensor_add(
-                out=blocks[0][:, left - FOLD_AV : left],
-                in0=blocks[0][:, left - FOLD_AV : left],
-                in1=blocks[0][:, left:],
-            )
-            planes = [blocks[0][:, n] for n in range(left)] + [blocks[1][:, n] for n in range(2 * WINDOW)]
+                count = (d1 - d0) * WINDOW
+                nc.gpsimd.tensor_tensor(
+                    out=block[:, 0:fold], in0=block[:, 0:fold], in1=block[:, count - fold :], op=ALU.add
+                )
+                planes += [block[:, n] for n in range(count - fold)]
             late_items.append((half, s, planes, -1, clock[0]))
 
         scalar_rows = [(half, s, di) for half in range(HALVES) for s in range(S_ITEMS[half]) for di in range(WINDOW)]
@@ -443,11 +484,11 @@ def tile_relation_kernel(tc, x, w_qkv_words, w_qkv_scales, out):
             pending += [(load_q, 1, ry) for ry in range(PATCH)] + key_loads(1)
             pending += [(load_v, u, v0) for u in range(HALO) for v0 in range(0, HALO, 2)]
 
-            start_pair(0, 0)
+            start_pair(0, 0, FOLD_QK[0])
             some_loads(6)
             for t in range(1, PAIRS):
-                start_pair(0, t)
-                finish_tile(4)
+                start_pair(0, t, FOLD_QK[0])
+                finish_tile(3)
                 if t in (7, 10):
                     softmax_max(0, (t - 4) // 3)
             start_tile((0, OFFSETS - 1), (1, OFFSETS - 1), lone[:])
@@ -464,11 +505,26 @@ def tile_relation_kernel(tc, x, w_qkv_words, w_qkv_scales, out):
             start_pair(1, 2)
             finish_tile()
             softmax_norm(0)
+            late_rows = [(half, a) for half in range(HALVES) for a in reversed(range(S_ITEMS[half] // PATCH, PATCH))]
+            rows_turned = []
+            rows_returned = []
+
+            def turn_next():
+                turn_weights(*late_rows[len(rows_turned)])
+                rows_turned.append(1)
+
+            def return_next():
+                if len(rows_returned) < len(late_rows):
+                    return_weights(*late_rows[len(rows_returned)])
+                    rows_returned.append(1)
+
             for t in range(3, PAIRS):
-                start_pair(1, t, FOLD_QK)
+                start_pair(1, t, FOLD_QK[1])
                 finish_tile()
                 if t in (7, 10):
                     softmax_max(1, (t - 4) // 3)
+                if t in (4, 5):
+                    turn_next()
                 scalar_work(3)
                 finish_earlier()
             vector_rest = [(half, s) for half in range(HALVES) for s in reversed(range(S_ITEMS[half], SPOTS))]
@@ -477,6 +533,10 @@ def tile_relation_kernel(tc, x, w_qkv_words, w_qkv_scales, out):
                 half, s = vector_rest[0]
                 vector_rest.remove(vector_rest[0])
                 vector_item(half, s)
+                if s % PATCH == 2:
+                    return_next()
+                if half == 1 and s == SPOTS - PATCH and len(rows_turned) < len(late_rows):
+                    turn_next()
 
             def step(count):
                 if vector_rest:
@@ -484,6 +544,7 @@ def tile_relation_kernel(tc, x, w_qkv_words, w_qkv_scales, out):
                 scalar_work(count)
                 finish_earlier()
 
+            return_next()
             vector_work()
             finish_tile()
             finish_earlier()
@@ -494,9 +555,13 @@ def tile_relation_kernel(tc, x, w_qkv_words, w_qkv_scales, out):
             softmax_exp(1)
             step(3)
             softmax_norm(1)
+            turn_next()
+            turn_next()
             stored = 0
+            turn = 0
             while vector_rest or late_items or scalar_rows:
-                step(3)
+                step(2 + turn % 2)
+                turn += 1
                 if stored == 0 and all((0, a) in filled and filled[0, a] == PATCH for a in range(PATCH)):
                     store(0)
                     stored = 1

@@ -30,10 +30,10 @@ HALO = PATCH + WINDOW - 1
 PAIRS = OFFSETS // 2
 ORDER = (12, 13, 14, 10, 11) + tuple(range(10)) + tuple(range(15, OFFSETS))
 GROUP = SPOTS * HH
-S_ITEMS = (8, 6)
+S_ITEMS = (9, 6)
 
 FOLD_QK = ((8, 2), (6, 0))
-FOLD_AV = (7, 5)
+FOLD_AV = (6, 5)
 RING = 4
 
 FLOPS = 2 * 3 * DEPTH * CHANNELS_IN * PIXELS + 2 * 2 * PIXELS * HEADS * OFFSETS * HEAD_DIM
@@ -95,7 +95,7 @@ def tile_relation_kernel(tc, x, w_qkv_words, w_qkv_scales, out):
             "p t (g ry qx rx) -> p ry rx g qx t", g=IMAGES * GRID, ry=PATCH, qx=GRID, rx=PATCH
         )
         for ry in range(PATCH):
-            copy = nc.scalar.copy if ry == PATCH - 1 else nc.vector.tensor_copy
+            copy = nc.scalar.copy if ry >= PATCH // 2 else nc.vector.tensor_copy
             copy(
                 out=grouped[:, ry].rearrange("p rx (g qx) t -> p rx g qx t", qx=GRID), in_=by_spot[:, ry]
             )
@@ -217,7 +217,7 @@ def tile_relation_kernel(tc, x, w_qkv_words, w_qkv_scales, out):
                 fold_block(*late_folds[0])
                 late_folds.remove(late_folds[0])
 
-        def start_tile(first, second, target, folds=(0, 0)):
+        def start_tile(first, second, target, folds=(0, 0), between=None):
             blocks = []
             for n in range(2):
                 block = work.tile([P, PIECE, 2, GROUP], F32, tag="work", name="prod")
@@ -229,6 +229,8 @@ def tile_relation_kernel(tc, x, w_qkv_words, w_qkv_scales, out):
                 elif folds[0]:
                     fold_block(blocks[0], folds[0])
                 products(block, channels, 1, second[0], second[1])
+                if n == 0 and between:
+                    between()
             if folds[1]:
                 late_folds.append((blocks[1], folds[1]))
             planes = [
@@ -242,12 +244,12 @@ def tile_relation_kernel(tc, x, w_qkv_words, w_qkv_scales, out):
             planes, target = late_sums[0]
             late_sums.remove(late_sums[0])
             score = score_ps.tile([P, P], F32, tag="score", name="score")
-            add_up(score[:], planes, loads)
+            add_up(score[:], planes, loads - loads // 2)
             nc.scalar.copy(out=target, in_=score[:])
-            some_loads(loads)
+            some_loads(loads // 2)
 
-        def start_pair(half, t, folds=(0, 0)):
-            start_tile((half, ORDER[2 * t]), (half, ORDER[2 * t + 1]), scores[half][:, t, :], folds)
+        def start_pair(half, t, folds=(0, 0), between=None):
+            start_tile((half, ORDER[2 * t]), (half, ORDER[2 * t + 1]), scores[half][:, t, :], folds, between)
 
         late = [None]
 
@@ -324,16 +326,19 @@ def tile_relation_kernel(tc, x, w_qkv_words, w_qkv_scales, out):
             flat = att_of(half).rearrange("p s o h -> p (s o h)")
             nc.scalar.activation(out=flat, in_=flat, func=ACT.Exp)
 
-        def softmax_norm(half):
-            weights_ready.add(half)
+        def softmax_sum(half, engine):
             att = att_of(half)
             rows_of = att.rearrange("p s o h -> p s (o h)")
-            nc.vector.tensor_add(
+            engine.tensor_add(
                 out=total[:, :, 0 : 12 * HH], in0=rows_of[:, :, 0 : 12 * HH], in1=rows_of[:, :, 12 * HH : 24 * HH]
             )
-            nc.vector.tensor_add(
+            engine.tensor_add(
                 out=total[:, :, 6 * HH : 12 * HH], in0=total[:, :, 0 : 6 * HH], in1=total[:, :, 6 * HH : 12 * HH]
             )
+
+        def softmax_norm(half, engine):
+            weights_ready.add(half)
+            att = att_of(half)
             nc.vector.tensor_reduce(
                 out=tops[half][:],
                 in_=total[:, :, 6 * HH :].rearrange("p s (o h) -> p s h o", h=HH),
@@ -341,7 +346,7 @@ def tile_relation_kernel(tc, x, w_qkv_words, w_qkv_scales, out):
                 op=ALU.add,
             )
             nc.vector.reciprocal(out=tops[half][:], in_=tops[half][:])
-            nc.vector.tensor_tensor(
+            engine.tensor_tensor(
                 out=att, in0=att, in1=tops[half][:].unsqueeze(2).to_broadcast([P, SPOTS, OFFSETS, HH]), op=ALU.mult
             )
 
@@ -391,6 +396,7 @@ def tile_relation_kernel(tc, x, w_qkv_words, w_qkv_scales, out):
                 )
 
         second_blocks = []
+        vector_rest = []
 
         def vector_item(half, s):
             a, b = divmod(s, PATCH)
@@ -402,7 +408,8 @@ def tile_relation_kernel(tc, x, w_qkv_words, w_qkv_scales, out):
             blocks = (first_block[:], second_blocks[0][:, (len(second_blocks) - 1) % 4])
             second_blocks.append(s)
             planes = []
-            for block, d0, d1, fold in ((blocks[0], 0, 3, FOLD_AV[0]), (blocks[1], 3, WINDOW, FOLD_AV[1])):
+            folds = FOLD_AV if len(vector_rest) >= 2 else (FOLD_AV[0], 0)
+            for block, d0, d1, fold in ((blocks[0], 0, 3, folds[0]), (blocks[1], 3, WINDOW, folds[1])):
                 nc.vector.tensor_tensor(
                     out=block.rearrange("p (di dj) (h c) -> p di (dj h) c", di=d1 - d0, c=HEAD_DIM),
                     in0=v_halo[:, half, a + d0 : a + d1, b : b + WINDOW, :].rearrange(
@@ -415,9 +422,10 @@ def tile_relation_kernel(tc, x, w_qkv_words, w_qkv_scales, out):
                     op=ALU.mult,
                 )
                 count = (d1 - d0) * WINDOW
-                nc.gpsimd.tensor_tensor(
-                    out=block[:, 0:fold], in0=block[:, 0:fold], in1=block[:, count - fold :], op=ALU.add
-                )
+                if fold:
+                    nc.gpsimd.tensor_tensor(
+                        out=block[:, 0:fold], in0=block[:, 0:fold], in1=block[:, count - fold :], op=ALU.add
+                    )
                 planes += [block[:, n] for n in range(count - fold)]
             late_items.append((half, s, planes, -1, clock[0]))
 
@@ -488,23 +496,22 @@ def tile_relation_kernel(tc, x, w_qkv_words, w_qkv_scales, out):
             some_loads(6)
             for t in range(1, PAIRS):
                 start_pair(0, t, FOLD_QK[0])
-                finish_tile(3)
+                finish_tile(5)
                 if t in (7, 10):
                     softmax_max(0, (t - 4) // 3)
             start_tile((0, OFFSETS - 1), (1, OFFSETS - 1), lone[:])
             finish_tile()
             some_loads(len(pending))
             scores[1] = keep.tile([P, PAIRS, P], F32, tag="scales", align_bytes=64, name="scores1")
-            start_pair(1, 0)
-            finish_tile()
-            softmax_max(0, 3)
-            start_pair(1, 1)
+            start_pair(1, 0, between=lambda: softmax_max(0, 3))
             finish_tile()
             softmax_turn(0)
+            start_pair(1, 1)
             softmax_exp(0)
-            start_pair(1, 2)
             finish_tile()
-            softmax_norm(0)
+            start_pair(1, 2, between=lambda: (softmax_sum(0, nc.vector), softmax_norm(0, nc.vector)))
+            finish_tile()
+            scalar_work(2)
             late_rows = [(half, a) for half in range(HALVES) for a in reversed(range(S_ITEMS[half] // PATCH, PATCH))]
             rows_turned = []
             rows_returned = []
@@ -525,9 +532,9 @@ def tile_relation_kernel(tc, x, w_qkv_words, w_qkv_scales, out):
                     softmax_max(1, (t - 4) // 3)
                 if t in (4, 5):
                     turn_next()
-                scalar_work(3)
+                scalar_work(3 + t % 2)
                 finish_earlier()
-            vector_rest = [(half, s) for half in range(HALVES) for s in reversed(range(S_ITEMS[half], SPOTS))]
+            vector_rest += [(half, s) for half in range(HALVES) for s in reversed(range(S_ITEMS[half], SPOTS))]
 
             def vector_work():
                 half, s = vector_rest[0]
@@ -554,7 +561,10 @@ def tile_relation_kernel(tc, x, w_qkv_words, w_qkv_scales, out):
             softmax_turn(1)
             softmax_exp(1)
             step(3)
-            softmax_norm(1)
+            softmax_sum(1, nc.gpsimd)
+            step(3)
+            softmax_norm(1, nc.gpsimd)
+            step(3)
             turn_next()
             turn_next()
             stored = 0

@@ -23,42 +23,50 @@ HH = HEADS // HALVES
 WINDOW = 5
 OFFSETS = WINDOW * WINDOW
 PATCH = 4
-SPOTS = PATCH * PATCH
 GRID = SIDE // PATCH
 REACH = WINDOW // 2
 HALO = PATCH + WINDOW - 1
-PAIRS = OFFSETS // 2
-ORDER = (12, 13, 14, 10, 11) + tuple(range(10)) + tuple(range(15, OFFSETS))
-GROUP = SPOTS * HH
-S_ITEMS = (9, 6)
-
-FOLD_QK = ((8, 2), (6, 0))
-FOLD_AV = (6, 5)
-RING = 4
+PART = HALO // 2
+UNITS = HALVES * PATCH
+STRIP = PATCH * HH
+SLOTS = P // STRIP
+TILES = UNITS * OFFSETS // SLOTS
 
 FLOPS = 2 * 3 * DEPTH * CHANNELS_IN * PIXELS + 2 * 2 * PIXELS * HEADS * OFFSETS * HEAD_DIM
+
+SHARES = ("SSGG",) * 6 + ("SSGV", "SVVG")
+LOADS = (4, 3)
+ROWS = 4
 
 
 def tile_relation_kernel(tc, x, w_qkv_words, w_qkv_scales, out):
     nc = tc.nc
     with ExitStack() as whole:
         keep = whole.enter_context(tc.tile_pool(name="keep", bufs=1))
-        work = whole.enter_context(tc.tile_pool(name="work", bufs=RING))
-        small = whole.enter_context(tc.tile_pool(name="small", bufs=1))
-        turns = whole.enter_context(tc.tile_pool(name="turns", bufs=2))
+        halo = whole.enter_context(tc.tile_pool(name="halo", bufs=6))
+        prod = whole.enter_context(tc.tile_pool(name="prod", bufs=2))
+        blocks_s = whole.enter_context(tc.tile_pool(name="blocks_s", bufs=2))
+        blocks_g = whole.enter_context(tc.tile_pool(name="blocks_g", bufs=2))
+        few = whole.enter_context(tc.tile_pool(name="few", bufs=3))
+        turned = whole.enter_context(tc.tile_pool(name="turned", bufs=6))
+        ends = whole.enter_context(tc.tile_pool(name="ends", bufs=2))
+        q_ps = whole.enter_context(tc.psum_pool(name="q_ps", bufs=2))
         stage_ps = whole.enter_context(tc.psum_pool(name="stage_ps", bufs=3))
         score_ps = whole.enter_context(tc.psum_pool(name="score_ps", bufs=2))
-        out_ps = whole.enter_context(tc.psum_pool(name="out_ps", bufs=3))
+        out_ps = whole.enter_context(tc.psum_pool(name="out_ps", bufs=1))
 
         ident = keep.tile([P, P], F32)
         make_identity(nc, ident[:])
         w_words = keep.tile([P, 3 * DEPTH], I32, align_bytes=64)
         w_scales = keep.tile([P, 3 * DEPTH], U8, align_bytes=64)
-        x_words = keep.tile([P, HALO, HALO, P], I32, align_bytes=64, tag="words")
-        x_scales = keep.tile([P, HALO, HALO, P], U8, align_bytes=64, tag="scales")
-        front = keep.tile([P, 2, PACK * PIXELS], BF16, align_bytes=64, tag="v")
-        x_sb = front[:, 0].rearrange("p (t s) -> p t s", t=PACK)
-        grouped = front[:, 1].rearrange("p (ry rx q t) -> p ry rx q t", ry=PATCH, rx=PATCH, t=PACK)
+        qk_words = keep.tile([P, 2 * DEPTH], I32, align_bytes=64)
+        qk_scales = keep.tile([P, 2 * DEPTH], U8, align_bytes=64)
+        x_words = keep.tile([P, HALO, HALO, P], I32, align_bytes=64)
+        x_scales = keep.tile([P, HALO, HALO, P], U8, align_bytes=64)
+        x_tile = halo.tile([P, PACK * PIXELS], BF16, tag="halo", align_bytes=64, name="x_tile")
+        g_tile = halo.tile([P, PACK * PIXELS], BF16, tag="halo", align_bytes=64, name="g_tile")
+        x_sb = x_tile[:].rearrange("p (t s) -> p t s", t=PACK)
+        grouped = g_tile[:].rearrange("p (ry rx q t) -> p ry rx q t", ry=PATCH, rx=PATCH, t=PACK)
 
         def columns(tile, v0, v1, x0, x1):
             return tile[:, REACH : REACH + PATCH, v0:v1, :].rearrange("p u v (r x) -> p u (v r) x", x=GRID)[
@@ -87,9 +95,14 @@ def tile_relation_kernel(tc, x, w_qkv_words, w_qkv_scales, out):
         nc.vector.memset(columns(x_words, 6, 8, GRID - PATCH, GRID), 0)
         nc.vector.memset(rows(x_words, 0, 2, 0, GRID), 0)
         nc.vector.memset(rows(x_words, 6, 8, per_grid - GRID, per_grid), 0)
-        spark = small.tile([P, 1], F32)
+        spark = keep.tile([P, 1], F32)
         nc.vector.memset(spark[:], 0.0)
         nc.scalar.activation(out=spark[:], in_=spark[:], func=ACT.Exp)
+        for whole_w, part_w in ((w_words, qk_words), (w_scales, qk_scales)):
+            nc.vector.tensor_copy(
+                out=part_w[:].rearrange("p (g c h) -> p g c h", c=HEAD_DIM, h=HH),
+                in_=whole_w[:, 0 : 2 * DEPTH].rearrange("p (g h c) -> p g c h", h=HH, c=HEAD_DIM),
+            )
 
         by_spot = x_sb.rearrange(
             "p t (g ry qx rx) -> p ry rx g qx t", g=IMAGES * GRID, ry=PATCH, qx=GRID, rx=PATCH
@@ -117,84 +130,108 @@ def tile_relation_kernel(tc, x, w_qkv_words, w_qkv_scales, out):
             nc.vector.tensor_copy(out=rows(tile, 0, 2, row, size), in_=rows(tile, 4, 6, 0, size - row))
             nc.vector.tensor_copy(out=rows(tile, 6, 8, 0, size - row), in_=rows(tile, 2, 4, row, size))
 
-        def convolve(first, wide, u, vs):
-            bank = stage_ps.tile([P, PATCH * P // wide, wide], F32, tag="stage", name="bank")
-            cols = slice(first, first + wide)
-            for j, v in enumerate(vs):
+        k_tiles = {}
+        v_tiles = {}
+        q_banks = {}
+
+        def convolve(pool, tag, words, scales, first, places):
+            bank = pool.tile([P, PATCH, P], F32, tag=tag, name=tag)
+            cols = slice(first, first + P)
+            for j, (u, v) in enumerate(places):
                 nc.tensor.matmul_mx(
                     out=bank[:, j, :],
                     lhsT=x_words[:, u, v, :].bitcast(FP8X4),
                     lhsT_scale=x_scales[:, u, v, :],
-                    rhs=w_words[:, cols].bitcast(FP8X4),
-                    rhs_scale=w_scales[:, cols],
+                    rhs=words[:, cols].bitcast(FP8X4),
+                    rhs_scale=scales[:, cols],
                     start=True,
                     stop=True,
                 )
             return bank
 
-        q_own = [None, None]
-        k_halo = [None, None]
-
-        def load_q(half, ry):
-            if q_own[half] is None:
-                q_own[half] = keep.tile([P, HEAD_DIM, SPOTS, HH], F32, name="q%d" % half)
-            bank = convolve(half * P, P, REACH + ry, range(REACH, REACH + PATCH))
-            nc.scalar.copy(
-                out=q_own[half][:, :, ry * PATCH : (ry + 1) * PATCH, :],
-                in_=bank[:].rearrange("p r (h c) -> p c r h", c=HEAD_DIM),
-            )
+        def load_q(half, a):
+            places = [(REACH + a, REACH + b) for b in range(PATCH)]
+            q_banks[half, a] = convolve(q_ps, "q", qk_words, qk_scales, half * P, places)
 
         def load_k(half, u, vs):
-            if k_halo[half] is None:
-                k_halo[half] = keep.tile(
-                    [P, HEAD_DIM, HALO, HALO, HH], F32, tag="k%d" % half, align_bytes=64, name="k%d" % half
+            if (half, u // PART) not in k_tiles:
+                k_tiles[half, u // PART] = halo.tile(
+                    [P, PART, HALO, P], F32, tag="halo", align_bytes=64, name="k_tile"
                 )
-            bank = convolve(DEPTH + half * P, P, u, vs)
-            row = k_halo[half][:, :, u, :, :]
+            bank = convolve(stage_ps, "stage", qk_words, qk_scales, DEPTH + half * P, [(u, v) for v in vs])
+            row = k_tiles[half, u // PART][:, u % PART]
             if vs[3] - vs[0] == 3:
-                nc.scalar.copy(
-                    out=row[:, :, vs[0] : vs[0] + PATCH, :], in_=bank[:].rearrange("p r (h c) -> p c r h", c=HEAD_DIM)
-                )
+                to = row[:, vs[0] : vs[0] + PATCH, :]
+                what = bank[:]
             else:
-                nc.scalar.copy(
-                    out=row.rearrange("p c (g w) h -> p c g w h", w=2)[:, :, 0:4:3],
-                    in_=bank[:].rearrange("p (g w) (h c) -> p c g w h", w=2, c=HEAD_DIM),
+                to = row.rearrange("p (g w) x -> p g w x", w=2)[:, 0:4:3]
+                what = bank[:].rearrange("p (g w) x -> p g w x", w=2)
+            return lambda: nc.scalar.copy(out=to, in_=what)
+
+        def load_v(half, u, v0):
+            if (half, u // PART) not in v_tiles:
+                v_tiles[half, u // PART] = halo.tile(
+                    [P, PART, HALO, P], F32, tag="halo", align_bytes=64, name="v_tile"
                 )
-
-        v_halo = keep.tile([P, HALVES, HALO, HALO, P], F32, tag="v", align_bytes=64, name="v_halo")
-
-        def load_v(u, v0):
-            bank = convolve(2 * DEPTH, DEPTH, u, (v0, v0 + 1))
-            nc.scalar.copy(
-                out=v_halo[:, :, u, v0 : v0 + 2, :], in_=bank[:].rearrange("p r (f d) -> p f r d", f=HALVES)
+            bank = convolve(
+                stage_ps, "stage", w_words, w_scales, 2 * DEPTH + half * P, [(u, v0 + j) for j in range(PATCH)]
             )
-
-        scores = [keep.tile([P, PAIRS, P], F32, name="scores0"), None]
-        lone = keep.tile([P, P], F32, name="lone")
-
-        def products(block, channels, slot, half, offset):
-            di, dj = divmod(offset, WINDOW)
-            nc.vector.tensor_tensor(
-                out=block[:, :, slot, :].rearrange("p c (a g) -> p c a g", a=PATCH),
-                in0=q_own[half][:, channels].rearrange("p c (a b) h -> p c a (b h)", a=PATCH),
-                in1=k_halo[half][:, channels, di : di + PATCH, dj : dj + PATCH, :].rearrange(
-                    "p c a b h -> p c a (b h)"
-                ),
-                op=ALU.mult,
-            )
+            to = v_tiles[half, u // PART][:, u % PART, v0 : v0 + PATCH, :]
+            return lambda: nc.scalar.copy(out=to, in_=bank[:])
 
         pending = []
 
         def some_loads(count):
+            copies = []
             for _ in range(min(count, len(pending))):
                 load = pending[0]
                 pending.remove(load)
-                load[0](*load[1:])
+                copies.append(load[0](*load[1:]))
+            for copy in copies:
+                if copy:
+                    copy()
 
-        def add_up(out_ap, planes, loads=0):
+        def parts_of(half, a):
+            if half == 0 and a == 0:
+                return ((2, 4), (4, 5), (0, 2))
+            return ((0, PART - a), (PART - a, WINDOW))
+
+        unit_of = [(half, a) for half in range(HALVES) for a in range(PATCH)]
+        runs = []
+        for n, (half, a) in enumerate(unit_of):
+            slot = OFFSETS * n
+            for d0, d1 in parts_of(half, a):
+                for dj in range(WINDOW):
+                    runs.append((slot, n, dj, d0, d1))
+                    slot += d1 - d0
+
+        def products(t):
+            block = prod.tile([P, HEAD_DIM, SLOTS, STRIP], F32, tag="prod", align_bytes=64, name="block")
+            for slot, n, dj, d0, d1 in runs:
+                first = max(slot, SLOTS * t)
+                last = min(slot + d1 - d0, SLOTS * (t + 1))
+                if first >= last:
+                    continue
+                half, a = unit_of[n]
+                count = last - first
+                u = a + d0 + first - slot
+                nc.vector.tensor_tensor(
+                    out=block[:, :, first - SLOTS * t : last - SLOTS * t, :].rearrange(
+                        "p c k (b h) -> p k b c h", h=HH
+                    ),
+                    in0=q_banks[half, a][:]
+                    .rearrange("p b (c h) -> p b c h", h=HH)
+                    .unsqueeze(1)
+                    .to_broadcast([P, count, PATCH, HEAD_DIM, HH]),
+                    in1=k_tiles[half, u // PART][:, u % PART : u % PART + count, dj : dj + PATCH, :].rearrange(
+                        "p k b (c h) -> p k b c h", h=HH
+                    ),
+                    op=ALU.mult,
+                )
+            return block
+
+        def add_up(out_ap, planes):
             for n, plane in enumerate(planes):
-                if n == len(planes) // 2:
-                    some_loads(loads)
                 nc.tensor.matmul(
                     out=out_ap,
                     lhsT=plane,
@@ -204,375 +241,243 @@ def tile_relation_kernel(tc, x, w_qkv_words, w_qkv_scales, out):
                     stop=(n == len(planes) - 1),
                 )
 
-        late_sums = []
-        PIECE = HEAD_DIM // 2
+        product_blocks = {}
+        scores = {}
 
-        late_folds = []
+        def sum_scores(t):
+            block = product_blocks[t]
+            bank = score_ps.tile([P, P], F32, tag="score", name="score")
+            add_up(bank[:], [block[:, c].rearrange("p k x -> p (k x)") for c in range(HEAD_DIM)])
+            scores[t] = turned.tile([P, P], F32, tag="turned", name="turned_score")
+            return lambda: nc.scalar.copy(out=scores[t][:], in_=bank[:])
 
-        def fold_block(block, fold):
-            nc.vector.tensor_add(out=block[:, 0:fold], in0=block[:, 0:fold], in1=block[:, PIECE - fold :])
+        last_tile = [(OFFSETS * (n + 1) - 1) // SLOTS for n in range(UNITS)]
+        first_tile = [OFFSETS * n // SLOTS for n in range(UNITS)]
+        raws = {}
+        atts = {}
+        tops = {}
 
-        def fold_earlier():
-            while late_folds:
-                fold_block(*late_folds[0])
-                late_folds.remove(late_folds[0])
+        def return_scores(n):
+            raws[n] = score_ps.tile([P, 4, P], F32, tag="score", name="raw")
+            for j, t in enumerate(range(first_tile[n], last_tile[n] + 1)):
+                nc.tensor.transpose(out=raws[n][:, j, :], in_=scores[t][:], identity=ident[:])
 
-        def start_tile(first, second, target, folds=(0, 0), between=None):
-            blocks = []
-            for n in range(2):
-                block = work.tile([P, PIECE, 2, GROUP], F32, tag="work", name="prod")
-                blocks.append(block)
-                channels = slice(n * PIECE, (n + 1) * PIECE)
-                products(block, channels, 0, first[0], first[1])
-                if n == 0:
-                    fold_earlier()
-                elif folds[0]:
-                    fold_block(blocks[0], folds[0])
-                products(block, channels, 1, second[0], second[1])
-                if n == 0 and between:
-                    between()
-            if folds[1]:
-                late_folds.append((blocks[1], folds[1]))
-            planes = [
-                block[:, c].rearrange("p o g -> p (o g)")
-                for block, fold in zip(blocks, folds)
-                for c in range(PIECE - fold)
-            ]
-            late_sums.append((planes, target))
-
-        def finish_tile(loads=0):
-            planes, target = late_sums[0]
-            late_sums.remove(late_sums[0])
-            score = score_ps.tile([P, P], F32, tag="score", name="score")
-            add_up(score[:], planes, loads - loads // 2)
-            nc.scalar.copy(out=target, in_=score[:])
-            some_loads(loads // 2)
-
-        def start_pair(half, t, folds=(0, 0), between=None):
-            start_tile((half, ORDER[2 * t]), (half, ORDER[2 * t + 1]), scores[half][:, t, :], folds, between)
-
-        late = [None]
-
-        def att_of(half):
-            if late[0] is None:
-                late[0] = keep.tile(
-                    [P, 2 * OFFSETS * GROUP + 2 * PIXELS], F32, tag="words", align_bytes=64, name="late"
-                )
-            return late[0][:, half * OFFSETS * GROUP : (half + 1) * OFFSETS * GROUP].rearrange(
-                "p (s o h) -> p s o h", s=SPOTS, o=OFFSETS
-            )
-
-        def result_of(half):
-            base = 2 * OFFSETS * GROUP + half * PIXELS
-            return late[0][:, base : base + PIXELS]
-
-        tops = [small.tile([P, SPOTS, HH], F32, name="top%d" % half) for half in range(HALVES)]
-        tree = small.tile([P, 4, P], F32)
-        total = small.tile([P, SPOTS, 13 * HH], F32)
-        both = [small.tile([P, 3, GROUP], F32, name="both%d" % half) for half in range(HALVES)]
-        raw = {}
-
-        def softmax_max(half, quarter):
-            three = scores[half][:, 3 * quarter : 3 * quarter + 3, :]
-            before = scores[half][:, 0:3, :] if quarter == 1 else tree[:, 0:3, :]
-            nc.vector.tensor_max(out=tree[:, 0:3, :], in0=before, in1=three)
-            if quarter == 3:
-                nc.vector.tensor_reduce(
-                    out=tree[:, 3, :], in_=tree[:, 0:3, :].rearrange("p k q -> p q k"), axis=AX.X, op=ALU.max
-                )
-
-        def softmax_turn(half):
-            bank = stage_ps.tile([P, PATCH, P], F32, tag="stage", name="bank")
-            if half == 0:
-                nc.tensor.transpose(out=bank[:, 0, :], in_=lone[:], identity=ident[:])
-            nc.tensor.transpose(out=bank[:, 1, :], in_=tree[:, 3, :], identity=ident[:])
-            if half == 0:
-                for other in range(HALVES):
-                    nc.scalar.copy(out=both[other][:, 2, :], in_=bank[:, 0, other * GROUP : (other + 1) * GROUP])
-            nc.scalar.copy(out=both[half][:, 0:2, :].rearrange("p f g -> p (f g)"), in_=bank[:, 1, :])
-            for k in range(PAIRS // 4):
-                bank = stage_ps.tile([P, PATCH, P], F32, tag="stage", name="bank")
-                raw[half, k] = bank
-                for j in range(4):
-                    nc.tensor.transpose(out=bank[:, j, :], in_=scores[half][:, 4 * k + j, :], identity=ident[:])
-
-        def softmax_exp(half):
-            top = tops[half]
-            by_offset = att_of(half).rearrange("p s o h -> p o s h")
+        def subtract_top(n):
+            first = (OFFSETS * n - SLOTS * first_tile[n]) * STRIP
+            raw = raws[n][:].rearrange("p t x -> p (t x)")[:, first : first + OFFSETS * STRIP]
+            tops[n] = few.tile([P, 2, STRIP], F32, tag="top", name="top")
+            top = tops[n][:, 0]
             nc.vector.tensor_reduce(
-                out=top[:].rearrange("p s h -> p (s h)"),
-                in_=both[half][:].rearrange("p f g -> p g f"),
-                axis=AX.X,
-                op=ALU.max,
+                out=top, in_=raw.rearrange("p (o x) -> p x o", x=STRIP), axis=AX.X, op=ALU.max
             )
-            for k in range(PAIRS // 4):
-                scored = raw[half, k][:].rearrange("p t (o s h) -> p (t o) s h", o=2, h=HH)
-                first = 0
-                while first < 8:
-                    place = ORDER[8 * k + first]
-                    size = 1
-                    while first + size < 8 and ORDER[8 * k + first + size] == place + size:
-                        size += 1
-                    nc.vector.tensor_sub(
-                        out=by_offset[:, place : place + size],
-                        in0=scored[:, first : first + size],
-                        in1=top[:].unsqueeze(1).to_broadcast([P, size, SPOTS, HH]),
-                    )
-                    first += size
+            atts[n] = few.tile([P, PATCH, OFFSETS, HH], F32, tag="att", align_bytes=64, name="att")
             nc.vector.tensor_sub(
-                out=by_offset[:, OFFSETS - 1], in0=both[half][:, 2, :].rearrange("p (s h) -> p s h", h=HH), in1=top[:]
+                out=atts[n][:].rearrange("p b o h -> p o b h"),
+                in0=raw.rearrange("p (o b h) -> p o b h", b=PATCH, h=HH),
+                in1=top.rearrange("p (b h) -> p b h", h=HH).unsqueeze(1).to_broadcast([P, OFFSETS, PATCH, HH]),
             )
-            nc.scalar.activation(out=total[:, :, 12 * HH :], in_=by_offset[:, OFFSETS - 1], func=ACT.Exp)
-            flat = att_of(half).rearrange("p s o h -> p (s o h)")
+
+        def exponential(n):
+            flat = atts[n][:].rearrange("p b o h -> p (b o h)")
             nc.scalar.activation(out=flat, in_=flat, func=ACT.Exp)
 
-        def softmax_sum(half, engine):
-            att = att_of(half)
-            rows_of = att.rearrange("p s o h -> p s (o h)")
-            engine.tensor_add(
-                out=total[:, :, 0 : 12 * HH], in0=rows_of[:, :, 0 : 12 * HH], in1=rows_of[:, :, 12 * HH : 24 * HH]
-            )
-            engine.tensor_add(
-                out=total[:, :, 6 * HH : 12 * HH], in0=total[:, :, 0 : 6 * HH], in1=total[:, :, 6 * HH : 12 * HH]
-            )
-
-        def softmax_norm(half, engine):
-            weights_ready.add(half)
-            att = att_of(half)
+        def sum_weights(n):
+            total = tops[n][:, 1].rearrange("p (b h) -> p b h", h=HH)
             nc.vector.tensor_reduce(
-                out=tops[half][:],
-                in_=total[:, :, 6 * HH :].rearrange("p s (o h) -> p s h o", h=HH),
-                axis=AX.X,
-                op=ALU.add,
+                out=total, in_=atts[n][:].rearrange("p b o h -> p b h o"), axis=AX.X, op=ALU.add
             )
-            nc.vector.reciprocal(out=tops[half][:], in_=tops[half][:])
+            nc.vector.reciprocal(out=tops[n][:, 1], in_=tops[n][:, 1])
+
+        def normalise(n, engine):
+            factor = tops[n][:, 1].rearrange("p (b h) -> p b h", h=HH)
             engine.tensor_tensor(
-                out=att, in0=att, in1=tops[half][:].unsqueeze(2).to_broadcast([P, SPOTS, OFFSETS, HH]), op=ALU.mult
+                out=atts[n][:],
+                in0=atts[n][:],
+                in1=factor.unsqueeze(2).to_broadcast([P, PATCH, OFFSETS, HH]),
+                op=ALU.mult,
             )
 
-        banks = {}
-        filled = {}
+        def slot_of(n, di, dj):
+            slot = 0
+            for d0, d1 in parts_of(*unit_of[n]):
+                if d0 <= di < d1:
+                    return slot + dj * (d1 - d0) + di - d0
+                slot += WINDOW * (d1 - d0)
 
-        def sum_over_offsets(half, s, planes):
-            a, b = divmod(s, PATCH)
-            if (half, a) not in filled:
-                banks[half, a] = out_ps.tile([P, PATCH, P], F32, tag="sums", name="sums")
-                filled[half, a] = 0
-            bank = banks[half, a]
-            add_up(bank[:, b, :], planes)
-            filled[half, a] += 1
-            if filled[half, a] == PATCH:
-                nc.scalar.copy(
-                    out=result_of(half).rearrange(
-                        "c (g a qx b) -> c a g qx b", g=IMAGES * GRID, a=PATCH, qx=GRID, b=PATCH
-                    )[:, a],
-                    in_=bank[:].rearrange("c b (g qx) -> c g qx b", qx=GRID),
-                )
+        def places_of(half, u, b):
+            return v_tiles[half, u // PART][:, u % PART, b : b + WINDOW, :]
 
-        late_items = []
-        clock = [0]
+        def scalar_row(n, b, di, block):
+            half, a = unit_of[n]
+            place = places_of(half, a + di, b)
+            for dj in range(WINDOW):
+                off = slot_of(n, di, dj)
+                for h in range(HH):
+                    ch = slice(h * HEAD_DIM, (h + 1) * HEAD_DIM)
+                    nc.scalar.activation(
+                        out=block[:, off, ch], in_=place[:, dj, ch], func=ACT.Copy, scale=atts[n][:, b, off, h : h + 1]
+                    )
 
-        per_spot = OFFSETS * HH
-        per_row = PATCH * per_spot
-        pieces = (0, P, 2 * P, per_row - P)
-        turned = {}
-        weight_banks = {}
-
-        def turn_weights(half, a):
-            first = half * OFFSETS * GROUP + a * per_row
-            bank = stage_ps.tile([P, PATCH, P], F32, tag="stage", name="bank")
-            for j, piece in enumerate(pieces):
-                nc.tensor.transpose(
-                    out=bank[:, j, :], in_=late[0][:, first + piece : first + piece + P], identity=ident[:]
-                )
-            turned[half, a] = turns.tile([P, len(pieces), P], F32, tag="turned", name="turned")
-            nc.scalar.copy(out=turned[half, a][:], in_=bank[:])
-
-        def return_weights(half, a):
-            weight_banks[half, a] = score_ps.tile([P, PATCH * P], F32, tag="score", name="weights")
-            for j, piece in enumerate(pieces):
-                nc.tensor.transpose(
-                    out=weight_banks[half, a][:, piece : piece + P], in_=turned[half, a][:, j, :], identity=ident[:]
-                )
-
-        second_blocks = []
-        vector_rest = []
-
-        def vector_item(half, s):
-            a, b = divmod(s, PATCH)
-            if not second_blocks:
-                second_blocks.append(
-                    keep.tile([P, 4, 2 * WINDOW, P], F32, tag="k1", align_bytes=64, name="second_blocks")
-                )
-            first_block = work.tile([P, 3 * WINDOW, P], F32, tag="work", name="block")
-            blocks = (first_block[:], second_blocks[0][:, (len(second_blocks) - 1) % 4])
-            second_blocks.append(s)
-            planes = []
-            folds = FOLD_AV if len(vector_rest) >= 2 else (FOLD_AV[0], 0)
-            for block, d0, d1, fold in ((blocks[0], 0, 3, folds[0]), (blocks[1], 3, WINDOW, folds[1])):
-                nc.vector.tensor_tensor(
-                    out=block.rearrange("p (di dj) (h c) -> p di (dj h) c", di=d1 - d0, c=HEAD_DIM),
-                    in0=v_halo[:, half, a + d0 : a + d1, b : b + WINDOW, :].rearrange(
-                        "p u v (h c) -> p u (v h) c", c=HEAD_DIM
+        def whole_pixel(n, b, block, engine):
+            half, a = unit_of[n]
+            slot = 0
+            for d0, d1 in parts_of(half, a):
+                u = a + d0
+                count = WINDOW * (d1 - d0)
+                slots = slice(slot, slot + count)
+                slot += count
+                engine.tensor_tensor(
+                    out=block[:, slots, :].rearrange("p (j i) (h c) -> p j i h c", j=WINDOW, h=HH),
+                    in0=v_tiles[half, u // PART][:, u % PART : u % PART + d1 - d0, b : b + WINDOW, :].rearrange(
+                        "p u v (h c) -> p v u h c", h=HH
                     ),
-                    in1=weight_banks[half, a][:, b * per_spot : (b + 1) * per_spot]
-                    .rearrange("p (di x) -> p di x", di=WINDOW)[:, d0:d1]
-                    .unsqueeze(3)
-                    .to_broadcast([P, d1 - d0, WINDOW * HH, HEAD_DIM]),
+                    in1=atts[n][:, b, slots, :]
+                    .rearrange("p (j i) h -> p j i h", j=WINDOW)
+                    .unsqueeze(4)
+                    .to_broadcast([P, WINDOW, d1 - d0, HH, HEAD_DIM]),
                     op=ALU.mult,
                 )
-                count = (d1 - d0) * WINDOW
-                if fold:
-                    nc.gpsimd.tensor_tensor(
-                        out=block[:, 0:fold], in0=block[:, 0:fold], in1=block[:, count - fold :], op=ALU.add
-                    )
-                planes += [block[:, n] for n in range(count - fold)]
-            late_items.append((half, s, planes, -1, clock[0]))
 
-        scalar_rows = [(half, s, di) for half in range(HALVES) for s in range(S_ITEMS[half]) for di in range(WINDOW)]
-        blocks_s = {}
-        weights_ready = set()
+        banks = {}
+        finished = {}
+        due = []
 
-        def scalar_work(count):
-            for _ in range(min(count, len(scalar_rows))):
-                half, s, di = scalar_rows[0]
-                if half not in weights_ready:
-                    return
-                scalar_rows.remove(scalar_rows[0])
-                a, b = divmod(s, PATCH)
-                if di == 0:
-                    while any(0 <= item[3] < blocks_s.get("next", 0) - 1 for item in late_items):
-                        finish_item()
-                    if "pair" not in blocks_s:
-                        blocks_s["pair"] = keep.tile([P, 2, OFFSETS, P], F32, tag="k0", align_bytes=64, name="pair_s")
-                        blocks_s["next"] = 0
-                    blocks_s["now"] = blocks_s["pair"][:, blocks_s["next"] % 2]
-                    blocks_s["next"] += 1
-                block = blocks_s["now"]
-                for dj in range(WINDOW):
-                    off = di * WINDOW + dj
-                    for h in range(HH):
-                        ch = slice(h * HEAD_DIM, (h + 1) * HEAD_DIM)
-                        nc.scalar.activation(
-                            out=block[:, off, ch],
-                            in_=v_halo[:, half, a + di, b + dj, ch],
-                            func=ACT.Copy,
-                            scale=att_of(half)[:, s, off, h : h + 1],
-                        )
-                if di == WINDOW - 1:
-                    planes = [block[:, off] for off in range(OFFSETS)]
-                    late_items.append((half, s, planes, blocks_s["next"] - 1, clock[0]))
+        def sum_pixel(n, b, block):
+            if n not in banks:
+                banks[n] = out_ps.tile([P, PATCH, P], F32, tag="sums", name="sums")
+                finished[n] = 0
+            add_up(banks[n][:, b, :], [block[:, off] for off in range(OFFSETS)])
+            finished[n] += 1
 
-        def finish_item():
-            half, s, planes = late_items[0][0:3]
-            late_items.remove(late_items[0])
-            sum_over_offsets(half, s, planes)
-
-        def finish_earlier():
-            while late_items and late_items[0][4] < clock[0]:
-                finish_item()
-            clock[0] += 1
-
-        def store(half):
-            nc.sync.dma_start(
-                out=out.rearrange("n (f c) h w -> f c n (h w)", f=HALVES)[half],
-                in_=result_of(half).rearrange("c (n s) -> c n s", n=IMAGES),
+        def store(n):
+            half, a = unit_of[n]
+            result = ends.tile([P, IMAGES, GRID, GRID, PATCH], F32, tag="result", name="result")
+            nc.scalar.copy(
+                out=result[:].rearrange("c n g x b -> c (n g) x b"),
+                in_=banks[n][:].rearrange("c b (g x) -> c g x b", x=GRID),
             )
+            to = out.rearrange("n (f c) (g a) w -> f a n c g w", f=HALVES, a=PATCH)[half, a]
+            for image in range(IMAGES):
+                nc.sync.dma_start(out=to[image], in_=result[:, image].rearrange("c g x b -> c g (x b)"))
 
-        pinned = {mybir.EngineType.PE, mybir.EngineType.Activation, mybir.EngineType.DVE}
+        row_queue = []
+        pixel_queue = []
+        block_now = {}
+
+        def waiting(who):
+            return len([item for item in due if SHARES[item[1]][item[2]] == who])
+
+        def scalar_rows(count, t):
+            for _ in range(min(count, len(row_queue))):
+                n, b, di = row_queue[0]
+                if di == 0 and waiting("S") >= 2:
+                    return
+                row_queue.remove(row_queue[0])
+                if di == 0:
+                    block_now["s"] = blocks_s.tile([P, OFFSETS, P], F32, tag="block_s", align_bytes=64, name="block_s")
+                scalar_row(n, b, di, block_now["s"])
+                if di == WINDOW - 1:
+                    due.append((t + 1, n, b, block_now["s"]))
+
+        def gpsimd_pixel(t):
+            if pixel_queue and waiting("G") < 2:
+                n, b = pixel_queue[0]
+                pixel_queue.remove(pixel_queue[0])
+                block = blocks_g.tile([P, OFFSETS, P], F32, tag="block_g", align_bytes=64, name="block_g")
+                whole_pixel(n, b, block, nc.gpsimd)
+                due.append((t + 2, n, b, block))
+
+        vector_queue = []
+
+        def vector_pixel(t):
+            if vector_queue and waiting("V") < 2:
+                n, b = vector_queue[0]
+                vector_queue.remove(vector_queue[0])
+                block = prod.tile([P, OFFSETS, P], F32, tag="prod", align_bytes=64, name="block_v")
+                whole_pixel(n, b, block, nc.vector)
+                due.append((t, n, b, block))
+
+        def share_out(n):
+            for b, who in enumerate(SHARES[n]):
+                if who == "S":
+                    row_queue.extend([(n, b, di) for di in range(WINDOW)])
+                elif who == "G":
+                    pixel_queue.append((n, b))
+                else:
+                    vector_queue.append((n, b))
+
+        def pixel_sums(t, count, unit):
+            for _ in range(count):
+                ready = [item for item in due if item[0] <= t and item[1] == unit]
+                if not ready:
+                    return
+                due.remove(ready[0])
+                sum_pixel(*ready[0][1:])
+
+        own = (2, 3, 4, 5)
+        beside = (0, 1, 6, 7)
+        left = (0, 1, 2, 3)
+        right = (4, 5, 6, 7)
+        for vs in (own, beside):
+            pending.extend([(load_k, 0, u, vs) for u in (2, 3)])
+        pending.extend([(load_k, 0, 4, vs) for vs in (own, beside)])
+        pending.extend([(load_k, 0, u, vs) for u in (0, 1) for vs in (left, right)])
+        pending.extend([(load_v, 0, u, v0) for u in (0, 1) for v0 in (0, PART)])
+        pending.extend([(load_k, 0, 5, vs) for vs in (left, right)])
+        pending.extend([(load_v, 0, u, v0) for u in (2, 3, 4) for v0 in (0, PART)])
+        for a in range(2, PATCH):
+            pending.extend([(load_v, 0, a + 3, v0) for v0 in (0, PART)])
+            pending.extend([(load_k, 0, a + 4, vs) for vs in (left, right)])
+        pending.extend([(load_k, 1, u, vs) for u in range(WINDOW) for vs in (left, right)])
+        pending.extend([(load_v, 0, HALO - 1, v0) for v0 in (0, PART)])
+        pending.extend([(load_k, 1, WINDOW, vs) for vs in (left, right)])
+        pending.extend([(load_v, 1, u, v0) for u in range(WINDOW) for v0 in (0, PART)])
+        for a in range(2, PATCH):
+            pending.extend([(load_k, 1, a + 4, vs) for vs in (left, right)])
+            pending.extend([(load_v, 1, a + 3, v0) for v0 in (0, PART)])
+        pending.extend([(load_v, 1, HALO - 1, v0) for v0 in (0, PART)])
+
+        pinned = {
+            mybir.EngineType.PE,
+            mybir.EngineType.Activation,
+            mybir.EngineType.DVE,
+            mybir.EngineType.Pool,
+        }
         with tc.manual_schedule(engines=pinned):
-            def key_loads(half):
-                loads = [(load_k, half, u, (2, 3, 4, 5)) for u in range(REACH, REACH + PATCH)]
-                loads += [(load_k, half, u, (0, 1, 6, 7)) for u in range(REACH, REACH + PATCH)]
-                loads += [(load_k, half, u, vs) for u in (0, 1, 6, 7) for vs in ((0, 1, 2, 3), (4, 5, 6, 7))]
-                return loads
-
-            pending += [(load_q, 0, ry) for ry in range(PATCH)] + key_loads(0)
-            some_loads(12)
-            pending += [(load_q, 1, ry) for ry in range(PATCH)] + key_loads(1)
-            pending += [(load_v, u, v0) for u in range(HALO) for v0 in range(0, HALO, 2)]
-
-            start_pair(0, 0, FOLD_QK[0])
-            some_loads(6)
-            for t in range(1, PAIRS):
-                start_pair(0, t, FOLD_QK[0])
-                finish_tile(5)
-                if t in (7, 10):
-                    softmax_max(0, (t - 4) // 3)
-            start_tile((0, OFFSETS - 1), (1, OFFSETS - 1), lone[:])
-            finish_tile()
-            some_loads(len(pending))
-            scores[1] = keep.tile([P, PAIRS, P], F32, tag="scales", align_bytes=64, name="scores1")
-            start_pair(1, 0, between=lambda: softmax_max(0, 3))
-            finish_tile()
-            softmax_turn(0)
-            start_pair(1, 1)
-            softmax_exp(0)
-            finish_tile()
-            start_pair(1, 2, between=lambda: (softmax_sum(0, nc.vector), softmax_norm(0, nc.vector)))
-            finish_tile()
-            scalar_work(2)
-            late_rows = [(half, a) for half in range(HALVES) for a in reversed(range(S_ITEMS[half] // PATCH, PATCH))]
-            rows_turned = []
-            rows_returned = []
-
-            def turn_next():
-                turn_weights(*late_rows[len(rows_turned)])
-                rows_turned.append(1)
-
-            def return_next():
-                if len(rows_returned) < len(late_rows):
-                    return_weights(*late_rows[len(rows_returned)])
-                    rows_returned.append(1)
-
-            for t in range(3, PAIRS):
-                start_pair(1, t, FOLD_QK[1])
-                finish_tile()
-                if t in (7, 10):
-                    softmax_max(1, (t - 4) // 3)
-                if t in (4, 5):
-                    turn_next()
-                scalar_work(3 + t % 2)
-                finish_earlier()
-            vector_rest += [(half, s) for half in range(HALVES) for s in reversed(range(S_ITEMS[half], SPOTS))]
-
-            def vector_work():
-                half, s = vector_rest[0]
-                vector_rest.remove(vector_rest[0])
-                vector_item(half, s)
-                if s % PATCH == 2:
-                    return_next()
-                if half == 1 and s == SPOTS - PATCH and len(rows_turned) < len(late_rows):
-                    turn_next()
-
-            def step(count):
-                if vector_rest:
-                    vector_work()
-                scalar_work(count)
-                finish_earlier()
-
-            return_next()
-            vector_work()
-            finish_tile()
-            finish_earlier()
-            softmax_max(1, 3)
-            scalar_work(2)
-            step(2)
-            softmax_turn(1)
-            softmax_exp(1)
-            step(3)
-            softmax_sum(1, nc.gpsimd)
-            step(3)
-            softmax_norm(1, nc.gpsimd)
-            step(3)
-            turn_next()
-            turn_next()
+            load_q(0, 0)
+            some_loads(2)
+            some_loads(2)
+            t = 0
             stored = 0
-            turn = 0
-            while vector_rest or late_items or scalar_rows:
-                step(2 + turn % 2)
-                turn += 1
-                if stored == 0 and all((0, a) in filled and filled[0, a] == PATCH for a in range(PATCH)):
-                    store(0)
-                    stored = 1
-            store(1)
+            while stored < UNITS:
+                copy_score = None
+                for n in range(1, UNITS):
+                    if t == (1 if n == 1 else last_tile[n - 2] + 2):
+                        load_q(*unit_of[n])
+                some_loads(LOADS[t >= 6])
+                if finished.get(stored, 0) == PATCH:
+                    store(stored)
+                    stored += 1
+                turning = [n for n in range(UNITS) if last_tile[n] + 2 == t]
+                summing = [n for n in range(UNITS) if last_tile[n] + 3 == t]
+                if t < TILES:
+                    product_blocks[t] = products(t)
+                for n in turning:
+                    return_scores(n)
+                    subtract_top(n)
+                if 1 <= t <= TILES:
+                    copy_score = sum_scores(t - 1)
+                scalar_rows(ROWS // 2, t)
+                if copy_score:
+                    copy_score()
+                for n in turning:
+                    exponential(n)
+                for n in summing:
+                    sum_weights(n)
+                    normalise(n, nc.vector if n == UNITS - 1 else nc.gpsimd)
+                    share_out(n)
+                vector_pixel(t)
+                pixel_sums(t, 2, stored)
+                scalar_rows(ROWS - ROWS // 2, t)
+                gpsimd_pixel(t)
+                t += 1

@@ -36,7 +36,6 @@ FLOPS = 2 * 3 * DEPTH * CHANNELS_IN * PIXELS + 2 * 2 * PIXELS * HEADS * OFFSETS 
 
 SHARES = ("SSGG",) * 6 + ("SSGV", "SVVG")
 LOADS = (4, 3)
-ROWS = 4
 
 
 def tile_relation_kernel(tc, x, w_qkv_words, w_qkv_scales, out):
@@ -45,8 +44,7 @@ def tile_relation_kernel(tc, x, w_qkv_words, w_qkv_scales, out):
         keep = whole.enter_context(tc.tile_pool(name="keep", bufs=1))
         halo = whole.enter_context(tc.tile_pool(name="halo", bufs=6))
         prod = whole.enter_context(tc.tile_pool(name="prod", bufs=2))
-        blocks_s = whole.enter_context(tc.tile_pool(name="blocks_s", bufs=2))
-        blocks_g = whole.enter_context(tc.tile_pool(name="blocks_g", bufs=2))
+        weighted = whole.enter_context(tc.tile_pool(name="weighted", bufs=4))
         few = whole.enter_context(tc.tile_pool(name="few", bufs=3))
         turned = whole.enter_context(tc.tile_pool(name="turned", bufs=6))
         ends = whole.enter_context(tc.tile_pool(name="ends", bufs=2))
@@ -230,8 +228,10 @@ def tile_relation_kernel(tc, x, w_qkv_words, w_qkv_scales, out):
                 )
             return block
 
-        def add_up(out_ap, planes):
+        def add_up(out_ap, planes, between=None):
             for n, plane in enumerate(planes):
+                if between and n == len(planes) // 2:
+                    between()
                 nc.tensor.matmul(
                     out=out_ap,
                     lhsT=plane,
@@ -244,10 +244,10 @@ def tile_relation_kernel(tc, x, w_qkv_words, w_qkv_scales, out):
         product_blocks = {}
         scores = {}
 
-        def sum_scores(t):
+        def sum_scores(t, between):
             block = product_blocks[t]
             bank = score_ps.tile([P, P], F32, tag="score", name="score")
-            add_up(bank[:], [block[:, c].rearrange("p k x -> p (k x)") for c in range(HEAD_DIM)])
+            add_up(bank[:], [block[:, c].rearrange("p k x -> p (k x)") for c in range(HEAD_DIM)], between)
             scores[t] = turned.tile([P, P], F32, tag="turned", name="turned_score")
             return lambda: nc.scalar.copy(out=scores[t][:], in_=bank[:])
 
@@ -364,36 +364,41 @@ def tile_relation_kernel(tc, x, w_qkv_words, w_qkv_scales, out):
         pixel_queue = []
         block_now = {}
 
-        def waiting(who):
-            return len([item for item in due if SHARES[item[1]][item[2]] == who])
+        def new_block():
+            return weighted.tile([P, OFFSETS, P], F32, tag="weighted", align_bytes=64, name="weighted_v")
+
+        def full(who):
+            mine = [item for item in due if SHARES[item[1]][item[2]] == who]
+            return len(mine) >= 2 or len(due) + ("s" in block_now) >= 4
 
         def scalar_rows(count, t):
             for _ in range(min(count, len(row_queue))):
                 n, b, di = row_queue[0]
-                if di == 0 and waiting("S") >= 2:
+                if di == 0 and full("S"):
                     return
                 row_queue.remove(row_queue[0])
                 if di == 0:
-                    block_now["s"] = blocks_s.tile([P, OFFSETS, P], F32, tag="block_s", align_bytes=64, name="block_s")
+                    block_now["s"] = new_block()
                 scalar_row(n, b, di, block_now["s"])
                 if di == WINDOW - 1:
                     due.append((t + 1, n, b, block_now["s"]))
+                    block_now.clear()
 
         def gpsimd_pixel(t):
-            if pixel_queue and waiting("G") < 2:
+            if pixel_queue and not full("G"):
                 n, b = pixel_queue[0]
                 pixel_queue.remove(pixel_queue[0])
-                block = blocks_g.tile([P, OFFSETS, P], F32, tag="block_g", align_bytes=64, name="block_g")
+                block = new_block()
                 whole_pixel(n, b, block, nc.gpsimd)
                 due.append((t + 2, n, b, block))
 
         vector_queue = []
 
         def vector_pixel(t):
-            if vector_queue and waiting("V") < 2:
+            if vector_queue and not full("V"):
                 n, b = vector_queue[0]
                 vector_queue.remove(vector_queue[0])
-                block = prod.tile([P, OFFSETS, P], F32, tag="prod", align_bytes=64, name="block_v")
+                block = new_block()
                 whole_pixel(n, b, block, nc.vector)
                 due.append((t, n, b, block))
 
@@ -406,11 +411,9 @@ def tile_relation_kernel(tc, x, w_qkv_words, w_qkv_scales, out):
                 else:
                     vector_queue.append((n, b))
 
-        def pixel_sums(t, count, unit):
-            for _ in range(count):
-                ready = [item for item in due if item[0] <= t and item[1] == unit]
-                if not ready:
-                    return
+        def pixel_sum(t, unit):
+            ready = [item for item in due if item[0] <= t and item[1] == unit]
+            if ready:
                 due.remove(ready[0])
                 sum_pixel(*ready[0][1:])
 
@@ -454,7 +457,14 @@ def tile_relation_kernel(tc, x, w_qkv_words, w_qkv_scales, out):
                 for n in range(1, UNITS):
                     if t == (1 if n == 1 else last_tile[n - 2] + 2):
                         load_q(*unit_of[n])
-                some_loads(LOADS[t >= 6])
+                quota = [LOADS[t >= 6]]
+
+                def one_load():
+                    if quota[0]:
+                        quota[0] -= 1
+                        some_loads(1)
+
+                one_load()
                 if finished.get(stored, 0) == PATCH:
                     store(stored)
                     stored += 1
@@ -465,9 +475,12 @@ def tile_relation_kernel(tc, x, w_qkv_words, w_qkv_scales, out):
                 for n in turning:
                     return_scores(n)
                     subtract_top(n)
+                scalar_rows(1, t)
                 if 1 <= t <= TILES:
-                    copy_score = sum_scores(t - 1)
-                scalar_rows(ROWS // 2, t)
+                    copy_score = sum_scores(t - 1, one_load)
+                else:
+                    one_load()
+                scalar_rows(1, t)
                 if copy_score:
                     copy_score()
                 for n in turning:
@@ -477,7 +490,9 @@ def tile_relation_kernel(tc, x, w_qkv_words, w_qkv_scales, out):
                     normalise(n, nc.vector if n == UNITS - 1 else nc.gpsimd)
                     share_out(n)
                 vector_pixel(t)
-                pixel_sums(t, 2, stored)
-                scalar_rows(ROWS - ROWS // 2, t)
+                for _ in range(2):
+                    one_load()
+                    pixel_sum(t, stored)
+                    scalar_rows(1, t)
                 gpsimd_pixel(t)
                 t += 1

@@ -34,8 +34,12 @@ TILES = UNITS * OFFSETS // SLOTS
 
 FLOPS = 2 * 3 * DEPTH * CHANNELS_IN * PIXELS + 2 * 2 * PIXELS * HEADS * OFFSETS * HEAD_DIM
 
-SHARES = ("SSGG",) * 6 + ("SSGV", "SVVG")
-LOADS = (4, 3)
+SHARES = ("SSSV",) * 6 + ("SSVV", "SVVV")
+DIRECT = 6
+HALF_C = HEAD_DIM // 2
+FOLD_AV = OFFSETS // 2
+GROUP = 2
+RING = 3
 
 
 def tile_relation_kernel(tc, x, w_qkv_words, w_qkv_scales, out):
@@ -43,15 +47,16 @@ def tile_relation_kernel(tc, x, w_qkv_words, w_qkv_scales, out):
     with ExitStack() as whole:
         keep = whole.enter_context(tc.tile_pool(name="keep", bufs=1))
         halo = whole.enter_context(tc.tile_pool(name="halo", bufs=6))
-        prod = whole.enter_context(tc.tile_pool(name="prod", bufs=2))
-        weighted = whole.enter_context(tc.tile_pool(name="weighted", bufs=4))
+        prod = whole.enter_context(tc.tile_pool(name="prod", bufs=5))
+        weighted = whole.enter_context(tc.tile_pool(name="weighted", bufs=RING))
         few = whole.enter_context(tc.tile_pool(name="few", bufs=3))
         turned = whole.enter_context(tc.tile_pool(name="turned", bufs=6))
         ends = whole.enter_context(tc.tile_pool(name="ends", bufs=2))
         q_ps = whole.enter_context(tc.psum_pool(name="q_ps", bufs=2))
-        stage_ps = whole.enter_context(tc.psum_pool(name="stage_ps", bufs=3))
+        stage_ps = whole.enter_context(tc.psum_pool(name="stage_ps", bufs=GROUP))
         score_ps = whole.enter_context(tc.psum_pool(name="score_ps", bufs=2))
         out_ps = whole.enter_context(tc.psum_pool(name="out_ps", bufs=1))
+        weight_ps = whole.enter_context(tc.psum_pool(name="weight_ps", bufs=1))
 
         ident = keep.tile([P, P], F32)
         make_identity(nc, ident[:])
@@ -179,12 +184,13 @@ def tile_relation_kernel(tc, x, w_qkv_words, w_qkv_scales, out):
 
         pending = []
 
-        def some_loads(count):
+        def some_loads(count, t):
             copies = []
-            for _ in range(min(count, len(pending))):
-                load = pending[0]
-                pending.remove(load)
-                copies.append(load[0](*load[1:]))
+            for _ in range(count):
+                if pending and pending[0][0] <= t:
+                    load = pending[0]
+                    pending.remove(load)
+                    copies.append(load[1](*load[2:]))
             for copy in copies:
                 if copy:
                     copy()
@@ -204,29 +210,34 @@ def tile_relation_kernel(tc, x, w_qkv_words, w_qkv_scales, out):
                     slot += d1 - d0
 
         def products(t):
-            block = prod.tile([P, HEAD_DIM, SLOTS, STRIP], F32, tag="prod", align_bytes=64, name="block")
-            for slot, n, dj, d0, d1 in runs:
-                first = max(slot, SLOTS * t)
-                last = min(slot + d1 - d0, SLOTS * (t + 1))
-                if first >= last:
-                    continue
-                half, a = unit_of[n]
-                count = last - first
-                u = a + d0 + first - slot
-                nc.vector.tensor_tensor(
-                    out=block[:, :, first - SLOTS * t : last - SLOTS * t, :].rearrange(
-                        "p c k (b h) -> p k b c h", h=HH
-                    ),
-                    in0=q_banks[half, a][:]
-                    .rearrange("p b (c h) -> p b c h", h=HH)
-                    .unsqueeze(1)
-                    .to_broadcast([P, count, PATCH, HEAD_DIM, HH]),
-                    in1=k_tiles[half, u // PART][:, u % PART : u % PART + count, dj : dj + PATCH, :].rearrange(
-                        "p k b (c h) -> p k b c h", h=HH
-                    ),
-                    op=ALU.mult,
-                )
-            return block
+            blocks = []
+            for part in range(2):
+                block = prod.tile([P, HALF_C, SLOTS, STRIP], F32, tag="prod", align_bytes=64, name="block")
+                blocks.append(block)
+                channels = slice(part * HALF_C * HH, (part + 1) * HALF_C * HH)
+                for slot, n, dj, d0, d1 in runs:
+                    first = max(slot, SLOTS * t)
+                    last = min(slot + d1 - d0, SLOTS * (t + 1))
+                    if first >= last:
+                        continue
+                    half, a = unit_of[n]
+                    count = last - first
+                    u = a + d0 + first - slot
+                    nc.vector.tensor_tensor(
+                        out=block[:, :, first - SLOTS * t : last - SLOTS * t, :].rearrange(
+                            "p c k (b h) -> p k b c h", h=HH
+                        ),
+                        in0=q_banks[half, a][:, :, channels]
+                        .rearrange("p b (c h) -> p b c h", h=HH)
+                        .unsqueeze(1)
+                        .to_broadcast([P, count, PATCH, HALF_C, HH]),
+                        in1=k_tiles[half, u // PART][
+                            :, u % PART : u % PART + count, dj : dj + PATCH, channels
+                        ].rearrange("p k b (c h) -> p k b c h", h=HH),
+                        op=ALU.mult,
+                    )
+            nc.gpsimd.tensor_tensor(out=blocks[0][:], in0=blocks[0][:], in1=blocks[1][:], op=ALU.add)
+            return blocks[0]
 
         def add_up(out_ap, planes, between=None):
             for n, plane in enumerate(planes):
@@ -247,7 +258,7 @@ def tile_relation_kernel(tc, x, w_qkv_words, w_qkv_scales, out):
         def sum_scores(t, between):
             block = product_blocks[t]
             bank = score_ps.tile([P, P], F32, tag="score", name="score")
-            add_up(bank[:], [block[:, c].rearrange("p k x -> p (k x)") for c in range(HEAD_DIM)], between)
+            add_up(bank[:], [block[:, c].rearrange("p k x -> p (k x)") for c in range(HALF_C)], between)
             scores[t] = turned.tile([P, P], F32, tag="turned", name="turned_score")
             return lambda: nc.scalar.copy(out=scores[t][:], in_=bank[:])
 
@@ -318,20 +329,55 @@ def tile_relation_kernel(tc, x, w_qkv_words, w_qkv_scales, out):
                         out=block[:, off, ch], in_=place[:, dj, ch], func=ACT.Copy, scale=atts[n][:, b, off, h : h + 1]
                     )
 
-        def whole_pixel(n, b, block, engine):
+        per_pixel = OFFSETS * HH
+        turned_weights = {}
+        weight_banks = {}
+
+        def pieces(n):
+            first = sum(who != "V" for who in SHARES[n]) * per_pixel
+            last = PATCH * per_pixel - P
+            return (first, last) if first < last else (last,)
+
+        def turn_weights(n):
+            bank = score_ps.tile([P, 2, P], F32, tag="score", name="turn")
+            flat = atts[n][:].rearrange("p b o h -> p (b o h)")
+            starts = pieces(n)
+            for j, first in enumerate(starts):
+                nc.tensor.transpose(out=bank[:, j, :], in_=flat[:, first : first + P], identity=ident[:])
+            turned_weights[n] = ends.tile([P, 2, P], F32, tag="weights", name="turned_w")
+            return lambda: nc.scalar.copy(
+                out=turned_weights[n][:, 0 : len(starts), :], in_=bank[:, 0 : len(starts), :]
+            )
+
+        def return_weights(n):
+            weight_banks[n] = weight_ps.tile([P, 2 * P], F32, tag="weights", name="weights")
+            starts = pieces(n)
+            for j, first in enumerate(starts):
+                nc.tensor.transpose(
+                    out=weight_banks[n][:, first - starts[0] : first - starts[0] + P],
+                    in_=turned_weights[n][:, j, :],
+                    identity=ident[:],
+                )
+
+        def whole_pixel(n, b, block):
             half, a = unit_of[n]
+            if n < DIRECT:
+                first = b * per_pixel - pieces(n)[0]
+                weights = weight_banks[n][:, first : first + per_pixel].rearrange("p (o h) -> p o h", h=HH)
+            else:
+                weights = atts[n][:, b]
             slot = 0
             for d0, d1 in parts_of(half, a):
                 u = a + d0
                 count = WINDOW * (d1 - d0)
                 slots = slice(slot, slot + count)
                 slot += count
-                engine.tensor_tensor(
+                nc.vector.tensor_tensor(
                     out=block[:, slots, :].rearrange("p (j i) (h c) -> p j i h c", j=WINDOW, h=HH),
                     in0=v_tiles[half, u // PART][:, u % PART : u % PART + d1 - d0, b : b + WINDOW, :].rearrange(
                         "p u v (h c) -> p v u h c", h=HH
                     ),
-                    in1=atts[n][:, b, slots, :]
+                    in1=weights[:, slots, :]
                     .rearrange("p (j i) h -> p j i h", j=WINDOW)
                     .unsqueeze(4)
                     .to_broadcast([P, WINDOW, d1 - d0, HH, HEAD_DIM]),
@@ -342,11 +388,11 @@ def tile_relation_kernel(tc, x, w_qkv_words, w_qkv_scales, out):
         finished = {}
         due = []
 
-        def sum_pixel(n, b, block):
+        def sum_pixel(n, b, block, planes):
             if n not in banks:
                 banks[n] = out_ps.tile([P, PATCH, P], F32, tag="sums", name="sums")
                 finished[n] = 0
-            add_up(banks[n][:, b, :], [block[:, off] for off in range(OFFSETS)])
+            add_up(banks[n][:, b, :], [block[:, off] for off in range(planes)])
             finished[n] += 1
 
         def store(n):
@@ -361,7 +407,6 @@ def tile_relation_kernel(tc, x, w_qkv_words, w_qkv_scales, out):
                 nc.sync.dma_start(out=to[image], in_=result[:, image].rearrange("c g x b -> c g (x b)"))
 
         row_queue = []
-        pixel_queue = []
         block_now = {}
 
         def new_block():
@@ -369,7 +414,7 @@ def tile_relation_kernel(tc, x, w_qkv_words, w_qkv_scales, out):
 
         def full(who):
             mine = [item for item in due if SHARES[item[1]][item[2]] == who]
-            return len(mine) >= 2 or len(due) + ("s" in block_now) >= 4
+            return len(mine) >= 2 or len(due) + ("s" in block_now) >= RING
 
         def scalar_rows(count, t):
             for _ in range(min(count, len(row_queue))):
@@ -381,16 +426,8 @@ def tile_relation_kernel(tc, x, w_qkv_words, w_qkv_scales, out):
                     block_now["s"] = new_block()
                 scalar_row(n, b, di, block_now["s"])
                 if di == WINDOW - 1:
-                    due.append((t + 1, n, b, block_now["s"]))
+                    due.append((t + 1, n, b, block_now["s"], OFFSETS))
                     block_now.clear()
-
-        def gpsimd_pixel(t):
-            if pixel_queue and not full("G"):
-                n, b = pixel_queue[0]
-                pixel_queue.remove(pixel_queue[0])
-                block = new_block()
-                whole_pixel(n, b, block, nc.gpsimd)
-                due.append((t + 2, n, b, block))
 
         vector_queue = []
 
@@ -399,16 +436,20 @@ def tile_relation_kernel(tc, x, w_qkv_words, w_qkv_scales, out):
                 n, b = vector_queue[0]
                 vector_queue.remove(vector_queue[0])
                 block = new_block()
-                whole_pixel(n, b, block, nc.vector)
-                due.append((t, n, b, block))
+                whole_pixel(n, b, block)
+                if n < DIRECT:
+                    nc.gpsimd.tensor_tensor(
+                        out=block[:, 0:FOLD_AV], in0=block[:, 0:FOLD_AV], in1=block[:, OFFSETS - FOLD_AV :], op=ALU.add
+                    )
+                    due.append((t + 1, n, b, block, OFFSETS - FOLD_AV))
+                else:
+                    due.append((t, n, b, block, OFFSETS))
 
         def share_out(n):
             for b, who in enumerate(SHARES[n]):
                 if who == "S":
                     row_queue.extend([(n, b, di) for di in range(WINDOW)])
-                elif who == "G":
-                    pixel_queue.append((n, b))
-                else:
+                elif n >= DIRECT:
                     vector_queue.append((n, b))
 
         def pixel_sum(t, unit):
@@ -421,24 +462,25 @@ def tile_relation_kernel(tc, x, w_qkv_words, w_qkv_scales, out):
         beside = (0, 1, 6, 7)
         left = (0, 1, 2, 3)
         right = (4, 5, 6, 7)
+
+        def ask(*loads, since=0):
+            pending.extend([(since,) + load for load in loads])
+
         for vs in (own, beside):
-            pending.extend([(load_k, 0, u, vs) for u in (2, 3)])
-        pending.extend([(load_k, 0, 4, vs) for vs in (own, beside)])
-        pending.extend([(load_k, 0, u, vs) for u in (0, 1) for vs in (left, right)])
-        pending.extend([(load_v, 0, u, v0) for u in (0, 1) for v0 in (0, PART)])
-        pending.extend([(load_k, 0, 5, vs) for vs in (left, right)])
-        pending.extend([(load_v, 0, u, v0) for u in (2, 3, 4) for v0 in (0, PART)])
+            ask(*[(load_k, 0, u, vs) for u in (2, 3)])
+        ask(*[(load_k, 0, 4, vs) for vs in (own, beside)])
+        ask(*[(load_k, 0, u, vs) for u in (0, 1) for vs in (left, right)])
+        ask(*[(load_v, 0, u, v0) for u in (0, 1) for v0 in (0, PART)])
+        ask(*[(load_k, 0, 5, vs) for vs in (left, right)])
+        ask(*[(load_v, 0, u, v0) for u in (2, 3, 4) for v0 in (0, PART)])
         for a in range(2, PATCH):
-            pending.extend([(load_v, 0, a + 3, v0) for v0 in (0, PART)])
-            pending.extend([(load_k, 0, a + 4, vs) for vs in (left, right)])
-        pending.extend([(load_k, 1, u, vs) for u in range(WINDOW) for vs in (left, right)])
-        pending.extend([(load_v, 0, HALO - 1, v0) for v0 in (0, PART)])
-        pending.extend([(load_k, 1, WINDOW, vs) for vs in (left, right)])
-        pending.extend([(load_v, 1, u, v0) for u in range(WINDOW) for v0 in (0, PART)])
-        for a in range(2, PATCH):
-            pending.extend([(load_k, 1, a + 4, vs) for vs in (left, right)])
-            pending.extend([(load_v, 1, a + 3, v0) for v0 in (0, PART)])
-        pending.extend([(load_v, 1, HALO - 1, v0) for v0 in (0, PART)])
+            ask(*[(load_v, 0, a + 3, v0) for v0 in (0, PART)])
+            ask(*[(load_k, 0, a + 4, vs) for vs in (left, right)])
+        ask(*[(load_k, 1, u, vs) for u in range(WINDOW) for vs in (left, right)])
+        ask(*[(load_v, 0, HALO - 1, v0) for v0 in (0, PART)])
+        ask(*[(load_k, 1, u, vs) for u in range(WINDOW, HALO) for vs in (left, right)])
+        ask(*[(load_v, 1, u, v0) for u in range(PART) for v0 in (0, PART)], since=first_tile[PATCH - 1] + 3)
+        ask(*[(load_v, 1, u, v0) for u in range(PART, HALO) for v0 in (0, PART)], since=first_tile[PATCH] + 2)
 
         pinned = {
             mybir.EngineType.PE,
@@ -448,51 +490,54 @@ def tile_relation_kernel(tc, x, w_qkv_words, w_qkv_scales, out):
         }
         with tc.manual_schedule(engines=pinned):
             load_q(0, 0)
-            some_loads(2)
-            some_loads(2)
+            some_loads(GROUP, 0)
+            some_loads(GROUP, 0)
             t = 0
             stored = 0
             while stored < UNITS:
-                copy_score = None
                 for n in range(1, UNITS):
                     if t == (1 if n == 1 else last_tile[n - 2] + 2):
                         load_q(*unit_of[n])
-                quota = [LOADS[t >= 6]]
-
-                def one_load():
-                    if quota[0]:
-                        quota[0] -= 1
-                        some_loads(1)
-
-                one_load()
+                some_loads(GROUP, t)
                 if finished.get(stored, 0) == PATCH:
                     store(stored)
                     stored += 1
-                turning = [n for n in range(UNITS) if last_tile[n] + 2 == t]
-                summing = [n for n in range(UNITS) if last_tile[n] + 3 == t]
+
+                def units_at(steps):
+                    return [n for n in range(UNITS) if last_tile[n] + steps == t]
+
+                for n in units_at(6):
+                    if n < DIRECT:
+                        return_weights(n)
+                        vector_queue.extend([(n, b) for b in range(PATCH) if SHARES[n][b] == "V"])
+                for n in units_at(5):
+                    share_out(n)
                 if t < TILES:
                     product_blocks[t] = products(t)
-                for n in turning:
+                for n in units_at(4):
+                    sum_weights(n)
+                    normalise(n, nc.vector if n == UNITS - 1 else nc.gpsimd)
+                vector_pixel(t)
+                for n in units_at(3):
                     return_scores(n)
                     subtract_top(n)
                 scalar_rows(1, t)
-                if 1 <= t <= TILES:
-                    copy_score = sum_scores(t - 1, one_load)
+                copies = []
+                if 2 <= t < TILES + 2:
+                    copies.append(sum_scores(t - 2, lambda: some_loads(GROUP, t)))
                 else:
-                    one_load()
+                    some_loads(GROUP, t)
+                for n in units_at(5):
+                    if n < DIRECT:
+                        copies.append(turn_weights(n))
                 scalar_rows(1, t)
-                if copy_score:
-                    copy_score()
-                for n in turning:
+                for copy in copies:
+                    copy()
+                for n in units_at(3):
                     exponential(n)
-                for n in summing:
-                    sum_weights(n)
-                    normalise(n, nc.vector if n == UNITS - 1 else nc.gpsimd)
-                    share_out(n)
-                vector_pixel(t)
-                for _ in range(2):
-                    one_load()
+                for turn in range(2):
+                    if turn and t >= 6:
+                        some_loads(GROUP, t)
                     pixel_sum(t, stored)
-                    scalar_rows(1, t)
-                gpsimd_pixel(t)
+                    scalar_rows(2 if t >= TILES else 1 + turn % 2, t)
                 t += 1

@@ -34,12 +34,14 @@ TILES = UNITS * OFFSETS // SLOTS
 
 FLOPS = 2 * 3 * DEPTH * CHANNELS_IN * PIXELS + 2 * 2 * PIXELS * HEADS * OFFSETS * HEAD_DIM
 
-SHARES = ("SSSV",) * 6 + ("SSVV", "SVVV")
+SHARES = ("SSGV", "SSGV", "SSGV", "SSGV", "SSGV", "SSGV", "SSVV", "SVVV")
 DIRECT = 6
 HALF_C = HEAD_DIM // 2
+FOLD_QK = 10
+FOLD_FROM = 4
 FOLD_AV = OFFSETS // 2
 GROUP = 2
-RING = 3
+RING = 4
 
 
 def tile_relation_kernel(tc, x, w_qkv_words, w_qkv_scales, out):
@@ -47,7 +49,7 @@ def tile_relation_kernel(tc, x, w_qkv_words, w_qkv_scales, out):
     with ExitStack() as whole:
         keep = whole.enter_context(tc.tile_pool(name="keep", bufs=1))
         halo = whole.enter_context(tc.tile_pool(name="halo", bufs=6))
-        prod = whole.enter_context(tc.tile_pool(name="prod", bufs=5))
+        prod = whole.enter_context(tc.tile_pool(name="prod", bufs=6))
         weighted = whole.enter_context(tc.tile_pool(name="weighted", bufs=RING))
         few = whole.enter_context(tc.tile_pool(name="few", bufs=3))
         turned = whole.enter_context(tc.tile_pool(name="turned", bufs=6))
@@ -64,23 +66,19 @@ def tile_relation_kernel(tc, x, w_qkv_words, w_qkv_scales, out):
         w_scales = keep.tile([P, 3 * DEPTH], U8, align_bytes=64)
         qk_words = keep.tile([P, 2 * DEPTH], I32, align_bytes=64)
         qk_scales = keep.tile([P, 2 * DEPTH], U8, align_bytes=64)
-        x_words = keep.tile([P, HALO, HALO, P], I32, align_bytes=64)
-        x_scales = keep.tile([P, HALO, HALO, P], U8, align_bytes=64)
+        x_words = keep.tile([P, PATCH, HALO, P], I32, align_bytes=64)
+        x_scales = keep.tile([P, PATCH, HALO, P], U8, align_bytes=64)
+        zeros = keep.tile([P, HALO, P], F32, align_bytes=64)
+        nc.gpsimd.memset(zeros[:], 0.0)
         x_tile = halo.tile([P, PACK * PIXELS], BF16, tag="halo", align_bytes=64, name="x_tile")
         g_tile = halo.tile([P, PACK * PIXELS], BF16, tag="halo", align_bytes=64, name="g_tile")
         x_sb = x_tile[:].rearrange("p (t s) -> p t s", t=PACK)
         grouped = g_tile[:].rearrange("p (ry rx q t) -> p ry rx q t", ry=PATCH, rx=PATCH, t=PACK)
 
         def columns(tile, v0, v1, x0, x1):
-            return tile[:, REACH : REACH + PATCH, v0:v1, :].rearrange("p u v (r x) -> p u (v r) x", x=GRID)[
-                :, :, :, x0:x1
-            ]
-
-        def rows(tile, u0, u1, q0, q1):
-            return tile[:, u0:u1, :, :].rearrange("p u v (n q) -> p u (v n) q", n=IMAGES)[:, :, :, q0:q1]
+            return tile[:, :, v0:v1, :].rearrange("p u v (r x) -> p u (v r) x", x=GRID)[:, :, :, x0:x1]
 
         per_image = SIDE * SIDE
-        per_grid = GRID * GRID
         for n in range(IMAGES):
             nc.scalar.dma_start(
                 out=x_sb[:, :, n * per_image : (n + 1) * per_image],
@@ -96,8 +94,6 @@ def tile_relation_kernel(tc, x, w_qkv_words, w_qkv_scales, out):
         nc.vector.memset(x_scales[:].rearrange("p u v q -> p (u v q)").bitcast(I32), 0)
         nc.vector.memset(columns(x_words, 0, 2, 0, PATCH), 0)
         nc.vector.memset(columns(x_words, 6, 8, GRID - PATCH, GRID), 0)
-        nc.vector.memset(rows(x_words, 0, 2, 0, GRID), 0)
-        nc.vector.memset(rows(x_words, 6, 8, per_grid - GRID, per_grid), 0)
         spark = keep.tile([P, 1], F32)
         nc.vector.memset(spark[:], 0.0)
         nc.scalar.activation(out=spark[:], in_=spark[:], func=ACT.Exp)
@@ -118,20 +114,14 @@ def tile_relation_kernel(tc, x, w_qkv_words, w_qkv_scales, out):
         for ry in range(PATCH):
             mid = slice(REACH, REACH + PATCH)
             nc.vector.quantize_mx(
-                out=x_words[:, REACH + ry, mid, :].rearrange("p v q -> p (v q)").bitcast(FP8X4),
-                scales=x_scales[:, REACH + ry, mid, :].rearrange("p v q -> p (v q)"),
+                out=x_words[:, ry, mid, :].rearrange("p v q -> p (v q)").bitcast(FP8X4),
+                scales=x_scales[:, ry, mid, :].rearrange("p v q -> p (v q)"),
                 in_=grouped[:, ry].rearrange("p rx q t -> p (rx q t)"),
             )
 
-        scale_words = x_scales[:].rearrange("p u v q -> p (u v q)").bitcast(I32).rearrange(
-            "p (u v q) -> p u v q", u=HALO, v=HALO
-        )
         for tile in (x_words, x_scales):
             nc.vector.tensor_copy(out=columns(tile, 0, 2, 1, GRID), in_=columns(tile, 4, 6, 0, GRID - 1))
             nc.vector.tensor_copy(out=columns(tile, 6, 8, 0, GRID - 1), in_=columns(tile, 2, 4, 1, GRID))
-        for tile, row, size in ((x_words, GRID, per_grid), (scale_words, GRID // 4, per_grid // 4)):
-            nc.vector.tensor_copy(out=rows(tile, 0, 2, row, size), in_=rows(tile, 4, 6, 0, size - row))
-            nc.vector.tensor_copy(out=rows(tile, 6, 8, 0, size - row), in_=rows(tile, 2, 4, row, size))
 
         k_tiles = {}
         v_tiles = {}
@@ -143,8 +133,8 @@ def tile_relation_kernel(tc, x, w_qkv_words, w_qkv_scales, out):
             for j, (u, v) in enumerate(places):
                 nc.tensor.matmul_mx(
                     out=bank[:, j, :],
-                    lhsT=x_words[:, u, v, :].bitcast(FP8X4),
-                    lhsT_scale=x_scales[:, u, v, :],
+                    lhsT=x_words[:, u - REACH, v, :].bitcast(FP8X4),
+                    lhsT_scale=x_scales[:, u - REACH, v, :],
                     rhs=words[:, cols].bitcast(FP8X4),
                     rhs_scale=scales[:, cols],
                     start=True,
@@ -182,18 +172,34 @@ def tile_relation_kernel(tc, x, w_qkv_words, w_qkv_scales, out):
             to = v_tiles[half, u // PART][:, u % PART, v0 : v0 + PATCH, :]
             return lambda: nc.scalar.copy(out=to, in_=bank[:])
 
+        def share_rows(tiles, half, up):
+            upper, lower = tiles[half, 0], tiles[half, 1]
+            if up:
+                to, source, shift = upper[:, 0:REACH], lower[:, 0:REACH], GRID
+            else:
+                to, source, shift = lower[:, PART - REACH :], upper[:, PART - REACH :], -GRID
+            per_grid = GRID * GRID
+            for first in (0, per_grid):
+                a, b = (first + GRID, first + per_grid) if up else (first, first + per_grid - GRID)
+                edge = first if up else first + per_grid - GRID
+                nc.sync.dma_start(out=to[a:b], in_=source[a - shift : b - shift])
+                nc.sync.dma_start(out=to[edge : edge + GRID], in_=zeros[edge : edge + GRID].unsqueeze(1).to_broadcast([GRID, REACH, HALO, P]))
+
         pending = []
 
         def some_loads(count, t):
             copies = []
             for _ in range(count):
-                if pending and pending[0][0] <= t:
+                if pending and pending[0][0] <= t and pending[0][1] != share_rows:
                     load = pending[0]
                     pending.remove(load)
                     copies.append(load[1](*load[2:]))
             for copy in copies:
-                if copy:
-                    copy()
+                copy()
+            while pending and pending[0][1] == share_rows:
+                load = pending[0]
+                pending.remove(load)
+                load[1](*load[2:])
 
         def parts_of(half, a):
             if half == 0 and a == 0:
@@ -209,9 +215,11 @@ def tile_relation_kernel(tc, x, w_qkv_words, w_qkv_scales, out):
                     runs.append((slot, n, dj, d0, d1))
                     slot += d1 - d0
 
-        def products(t):
+        def products(t, between):
             blocks = []
             for part in range(2):
+                if part:
+                    between()
                 block = prod.tile([P, HALF_C, SLOTS, STRIP], F32, tag="prod", align_bytes=64, name="block")
                 blocks.append(block)
                 channels = slice(part * HALF_C * HH, (part + 1) * HALF_C * HH)
@@ -236,8 +244,15 @@ def tile_relation_kernel(tc, x, w_qkv_words, w_qkv_scales, out):
                         ].rearrange("p k b (c h) -> p k b c h", h=HH),
                         op=ALU.mult,
                     )
-            nc.gpsimd.tensor_tensor(out=blocks[0][:], in0=blocks[0][:], in1=blocks[1][:], op=ALU.add)
-            return blocks[0]
+            return blocks
+
+        def fold_products(blocks, t):
+            fold = FOLD_QK if t >= FOLD_FROM else 0
+            if fold:
+                nc.gpsimd.tensor_tensor(
+                    out=blocks[0][:, 0:fold], in0=blocks[0][:, 0:fold], in1=blocks[1][:, HALF_C - fold :], op=ALU.add
+                )
+            return [blocks[0][:, c] for c in range(HALF_C)] + [blocks[1][:, c] for c in range(HALF_C - fold)]
 
         def add_up(out_ap, planes, between=None):
             for n, plane in enumerate(planes):
@@ -256,9 +271,9 @@ def tile_relation_kernel(tc, x, w_qkv_words, w_qkv_scales, out):
         scores = {}
 
         def sum_scores(t, between):
-            block = product_blocks[t]
+            planes = product_blocks[t]
             bank = score_ps.tile([P, P], F32, tag="score", name="score")
-            add_up(bank[:], [block[:, c].rearrange("p k x -> p (k x)") for c in range(HALF_C)], between)
+            add_up(bank[:], [plane.rearrange("p k x -> p (k x)") for plane in planes], between)
             scores[t] = turned.tile([P, P], F32, tag="turned", name="turned_score")
             return lambda: nc.scalar.copy(out=scores[t][:], in_=bank[:])
 
@@ -359,9 +374,9 @@ def tile_relation_kernel(tc, x, w_qkv_words, w_qkv_scales, out):
                     identity=ident[:],
                 )
 
-        def whole_pixel(n, b, block):
+        def whole_pixel(n, b, block, engine):
             half, a = unit_of[n]
-            if n < DIRECT:
+            if n < DIRECT and SHARES[n][b] == "V":
                 first = b * per_pixel - pieces(n)[0]
                 weights = weight_banks[n][:, first : first + per_pixel].rearrange("p (o h) -> p o h", h=HH)
             else:
@@ -372,7 +387,7 @@ def tile_relation_kernel(tc, x, w_qkv_words, w_qkv_scales, out):
                 count = WINDOW * (d1 - d0)
                 slots = slice(slot, slot + count)
                 slot += count
-                nc.vector.tensor_tensor(
+                engine.tensor_tensor(
                     out=block[:, slots, :].rearrange("p (j i) (h c) -> p j i h c", j=WINDOW, h=HH),
                     in0=v_tiles[half, u // PART][:, u % PART : u % PART + d1 - d0, b : b + WINDOW, :].rearrange(
                         "p u v (h c) -> p v u h c", h=HH
@@ -426,29 +441,43 @@ def tile_relation_kernel(tc, x, w_qkv_words, w_qkv_scales, out):
                     block_now["s"] = new_block()
                 scalar_row(n, b, di, block_now["s"])
                 if di == WINDOW - 1:
-                    due.append((t + 1, n, b, block_now["s"], OFFSETS))
+                    hand_over(t, n, b, block_now["s"], None)
                     block_now.clear()
 
+        def hand_over(t, n, b, block, fold):
+            if fold:
+                fold.tensor_tensor(
+                    out=block[:, 0:FOLD_AV], in0=block[:, 0:FOLD_AV], in1=block[:, OFFSETS - FOLD_AV :], op=ALU.add
+                )
+                due.append((t + 2, n, b, block, OFFSETS - FOLD_AV))
+            else:
+                due.append((t + 1, n, b, block, OFFSETS))
+
+        def gpsimd_pixel(t):
+            if pixel_queue and not full("G"):
+                n, b = pixel_queue[0]
+                pixel_queue.remove(pixel_queue[0])
+                block = new_block()
+                whole_pixel(n, b, block, nc.gpsimd)
+                due.append((t + 2, n, b, block, OFFSETS))
+
         vector_queue = []
+        pixel_queue = []
 
         def vector_pixel(t):
             if vector_queue and not full("V"):
                 n, b = vector_queue[0]
                 vector_queue.remove(vector_queue[0])
                 block = new_block()
-                whole_pixel(n, b, block)
-                if n < DIRECT:
-                    nc.gpsimd.tensor_tensor(
-                        out=block[:, 0:FOLD_AV], in0=block[:, 0:FOLD_AV], in1=block[:, OFFSETS - FOLD_AV :], op=ALU.add
-                    )
-                    due.append((t + 1, n, b, block, OFFSETS - FOLD_AV))
-                else:
-                    due.append((t, n, b, block, OFFSETS))
+                whole_pixel(n, b, block, nc.vector)
+                hand_over(t - 1, n, b, block, nc.gpsimd if n < DIRECT else nc.vector)
 
         def share_out(n):
             for b, who in enumerate(SHARES[n]):
                 if who == "S":
                     row_queue.extend([(n, b, di) for di in range(WINDOW)])
+                elif who == "G":
+                    pixel_queue.append((n, b))
                 elif n >= DIRECT:
                     vector_queue.append((n, b))
 
@@ -466,21 +495,17 @@ def tile_relation_kernel(tc, x, w_qkv_words, w_qkv_scales, out):
         def ask(*loads, since=0):
             pending.extend([(since,) + load for load in loads])
 
-        for vs in (own, beside):
-            ask(*[(load_k, 0, u, vs) for u in (2, 3)])
-        ask(*[(load_k, 0, 4, vs) for vs in (own, beside)])
-        ask(*[(load_k, 0, u, vs) for u in (0, 1) for vs in (left, right)])
-        ask(*[(load_v, 0, u, v0) for u in (0, 1) for v0 in (0, PART)])
-        ask(*[(load_k, 0, 5, vs) for vs in (left, right)])
-        ask(*[(load_v, 0, u, v0) for u in (2, 3, 4) for v0 in (0, PART)])
-        for a in range(2, PATCH):
-            ask(*[(load_v, 0, a + 3, v0) for v0 in (0, PART)])
-            ask(*[(load_k, 0, a + 4, vs) for vs in (left, right)])
-        ask(*[(load_k, 1, u, vs) for u in range(WINDOW) for vs in (left, right)])
-        ask(*[(load_v, 0, HALO - 1, v0) for v0 in (0, PART)])
-        ask(*[(load_k, 1, u, vs) for u in range(WINDOW, HALO) for vs in (left, right)])
-        ask(*[(load_v, 1, u, v0) for u in range(PART) for v0 in (0, PART)], since=first_tile[PATCH - 1] + 3)
-        ask(*[(load_v, 1, u, v0) for u in range(PART, HALO) for v0 in (0, PART)], since=first_tile[PATCH] + 2)
+        def ask_halo(load, half, order, tiles, since=0):
+            for u, vs in order:
+                ask((load, half, u, vs), since=since)
+            for up in (True, False):
+                ask((share_rows, tiles, half, up))
+
+        own_rows = range(REACH, REACH + PATCH)
+        ask_halo(load_k, 0, [(u, vs) for r in (2, 4) for vs in (own, beside) for u in (r, r + 1)], k_tiles)
+        ask_halo(load_v, 0, [(u, v0) for u in own_rows for v0 in (0, PART)], v_tiles)
+        ask_halo(load_k, 1, [(u, vs) for u in own_rows for vs in (left, right)], k_tiles)
+        ask_halo(load_v, 1, [(u, v0) for u in own_rows for v0 in (0, PART)], v_tiles, since=first_tile[PATCH] + 2)
 
         pinned = {
             mybir.EngineType.PE,
@@ -506,38 +531,44 @@ def tile_relation_kernel(tc, x, w_qkv_words, w_qkv_scales, out):
                 def units_at(steps):
                     return [n for n in range(UNITS) if last_tile[n] + steps == t]
 
-                for n in units_at(6):
+                for n in units_at(4):
                     if n < DIRECT:
                         return_weights(n)
                         vector_queue.extend([(n, b) for b in range(PATCH) if SHARES[n][b] == "V"])
-                for n in units_at(5):
+                for n in units_at(3):
                     share_out(n)
+
+                def subtract():
+                    for n in units_at(2):
+                        subtract_top(n)
+
                 if t < TILES:
-                    product_blocks[t] = products(t)
-                for n in units_at(4):
+                    blocks = products(t, subtract)
+                else:
+                    subtract()
+                scalar_rows(1, t)
+                for n in units_at(2):
+                    exponential(n)
                     sum_weights(n)
                     normalise(n, nc.vector if n == UNITS - 1 else nc.gpsimd)
+                if t < TILES:
+                    product_blocks[t] = fold_products(blocks, t)
                 vector_pixel(t)
-                for n in units_at(3):
-                    return_scores(n)
-                    subtract_top(n)
-                scalar_rows(1, t)
                 copies = []
-                if 2 <= t < TILES + 2:
-                    copies.append(sum_scores(t - 2, lambda: some_loads(GROUP, t)))
+                if 1 <= t < TILES + 1:
+                    copies.append(sum_scores(t - 1, lambda: some_loads(GROUP, t)))
                 else:
                     some_loads(GROUP, t)
-                for n in units_at(5):
+                for n in units_at(3):
                     if n < DIRECT:
                         copies.append(turn_weights(n))
                 scalar_rows(1, t)
                 for copy in copies:
                     copy()
-                for n in units_at(3):
-                    exponential(n)
                 for turn in range(2):
-                    if turn and t >= 6:
-                        some_loads(GROUP, t)
                     pixel_sum(t, stored)
                     scalar_rows(2 if t >= TILES else 1 + turn % 2, t)
+                gpsimd_pixel(t)
+                for n in units_at(1):
+                    return_scores(n)
                 t += 1

@@ -36,7 +36,6 @@ FLOPS = 2 * 3 * DEPTH * CHANNELS_IN * PIXELS + 2 * 2 * PIXELS * HEADS * OFFSETS 
 
 SHARES = ("SSGV", "SSGV", "SSGV", "SSGV", "SSGV", "SSGV", "SSVV", "SVVV")
 DIRECT = 6
-HALF_C = HEAD_DIM // 2
 FOLD_QK = 10
 FOLD_FROM = 4
 FOLD_AV = OFFSETS // 2
@@ -49,7 +48,7 @@ def tile_relation_kernel(tc, x, w_qkv_words, w_qkv_scales, out):
     with ExitStack() as whole:
         keep = whole.enter_context(tc.tile_pool(name="keep", bufs=1))
         halo = whole.enter_context(tc.tile_pool(name="halo", bufs=6))
-        prod = whole.enter_context(tc.tile_pool(name="prod", bufs=6))
+        prod = whole.enter_context(tc.tile_pool(name="prod", bufs=3))
         weighted = whole.enter_context(tc.tile_pool(name="weighted", bufs=RING))
         few = whole.enter_context(tc.tile_pool(name="few", bufs=3))
         turned = whole.enter_context(tc.tile_pool(name="turned", bufs=6))
@@ -207,52 +206,36 @@ def tile_relation_kernel(tc, x, w_qkv_words, w_qkv_scales, out):
             return ((0, PART - a), (PART - a, WINDOW))
 
         unit_of = [(half, a) for half in range(HALVES) for a in range(PATCH)]
-        runs = []
+        offsets = []
         for n, (half, a) in enumerate(unit_of):
-            slot = OFFSETS * n
             for d0, d1 in parts_of(half, a):
-                for dj in range(WINDOW):
-                    runs.append((slot, n, dj, d0, d1))
-                    slot += d1 - d0
+                offsets.extend([(n, di, dj) for dj in range(WINDOW) for di in range(d0, d1)])
 
         def products(t, between):
-            blocks = []
-            for part in range(2):
-                if part:
+            block = prod.tile([P, HEAD_DIM, SLOTS, STRIP], F32, tag="prod", align_bytes=64, name="block")
+            for slot in range(SLOTS):
+                if slot == SLOTS // 2:
                     between()
-                block = prod.tile([P, HALF_C, SLOTS, STRIP], F32, tag="prod", align_bytes=64, name="block")
-                blocks.append(block)
-                channels = slice(part * HALF_C * HH, (part + 1) * HALF_C * HH)
-                for slot, n, dj, d0, d1 in runs:
-                    first = max(slot, SLOTS * t)
-                    last = min(slot + d1 - d0, SLOTS * (t + 1))
-                    if first >= last:
-                        continue
-                    half, a = unit_of[n]
-                    count = last - first
-                    u = a + d0 + first - slot
-                    nc.vector.tensor_tensor(
-                        out=block[:, :, first - SLOTS * t : last - SLOTS * t, :].rearrange(
-                            "p c k (b h) -> p k b c h", h=HH
-                        ),
-                        in0=q_banks[half, a][:, :, channels]
-                        .rearrange("p b (c h) -> p b c h", h=HH)
-                        .unsqueeze(1)
-                        .to_broadcast([P, count, PATCH, HALF_C, HH]),
-                        in1=k_tiles[half, u // PART][
-                            :, u % PART : u % PART + count, dj : dj + PATCH, channels
-                        ].rearrange("p k b (c h) -> p k b c h", h=HH),
-                        op=ALU.mult,
-                    )
-            return blocks
+                n, di, dj = offsets[SLOTS * t + slot]
+                half, a = unit_of[n]
+                u = a + di
+                nc.vector.tensor_tensor(
+                    out=block[:, :, slot, :].rearrange("p c (b h) -> p c b h", h=HH),
+                    in0=q_banks[half, a][:].rearrange("p b (c h) -> p c b h", h=HH),
+                    in1=k_tiles[half, u // PART][:, u % PART, dj : dj + PATCH, :].rearrange(
+                        "p b (c h) -> p c b h", h=HH
+                    ),
+                    op=ALU.mult,
+                )
+            return block
 
-        def fold_products(blocks, t):
+        def fold_products(block, t):
             fold = FOLD_QK if t >= FOLD_FROM else 0
             if fold:
                 nc.gpsimd.tensor_tensor(
-                    out=blocks[0][:, 0:fold], in0=blocks[0][:, 0:fold], in1=blocks[1][:, HALF_C - fold :], op=ALU.add
+                    out=block[:, 0:fold], in0=block[:, 0:fold], in1=block[:, HEAD_DIM - fold :], op=ALU.add
                 )
-            return [blocks[0][:, c] for c in range(HALF_C)] + [blocks[1][:, c] for c in range(HALF_C - fold)]
+            return [block[:, c] for c in range(HEAD_DIM - fold)]
 
         def add_up(out_ap, planes, between=None):
             for n, plane in enumerate(planes):
@@ -543,7 +526,7 @@ def tile_relation_kernel(tc, x, w_qkv_words, w_qkv_scales, out):
                         subtract_top(n)
 
                 if t < TILES:
-                    blocks = products(t, subtract)
+                    block = products(t, subtract)
                 else:
                     subtract()
                 scalar_rows(1, t)
@@ -552,7 +535,7 @@ def tile_relation_kernel(tc, x, w_qkv_words, w_qkv_scales, out):
                     sum_weights(n)
                     normalise(n, nc.vector if n == UNITS - 1 else nc.gpsimd)
                 if t < TILES:
-                    product_blocks[t] = fold_products(blocks, t)
+                    product_blocks[t] = fold_products(block, t)
                 vector_pixel(t)
                 copies = []
                 if 1 <= t < TILES + 1:

@@ -221,10 +221,10 @@ def tile_relation_kernel(tc, x, w_qkv_words, w_qkv_scales, out):
                 u = a + di
                 nc.vector.tensor_tensor(
                     out=block[:, :, slot, :].rearrange("p c (b h) -> p c b h", h=HH),
-                    in0=q_banks[half, a][:].rearrange("p b (c h) -> p c b h", h=HH),
-                    in1=k_tiles[half, u // PART][:, u % PART, dj : dj + PATCH, :].rearrange(
+                    in0=k_tiles[half, u // PART][:, u % PART, dj : dj + PATCH, :].rearrange(
                         "p b (c h) -> p c b h", h=HH
                     ),
+                    in1=q_banks[half, a][:].rearrange("p b (c h) -> p c b h", h=HH),
                     op=ALU.mult,
                 )
             return block

@@ -34,10 +34,8 @@ TILES = UNITS * OFFSETS // SLOTS
 
 FLOPS = 2 * 3 * DEPTH * CHANNELS_IN * PIXELS + 2 * 2 * PIXELS * HEADS * OFFSETS * HEAD_DIM
 
-SHARES = ("SSGV", "SSGV", "SSGV", "SSGV", "SSGV", "SSGV", "SSVV", "SVVV")
+SHARES = ("SSSV", "SSGV", "SSSV", "SSGV", "SSSV", "SSGV", "SSGV", "SVVV")
 DIRECT = 6
-FOLD_QK = 10
-FOLD_FROM = 4
 FOLD_AV = OFFSETS // 2
 GROUP = 2
 RING = 4
@@ -229,14 +227,6 @@ def tile_relation_kernel(tc, x, w_qkv_words, w_qkv_scales, out):
                 )
             return block
 
-        def fold_products(block, t):
-            fold = FOLD_QK if t >= FOLD_FROM else 0
-            if fold:
-                nc.gpsimd.tensor_tensor(
-                    out=block[:, 0:fold], in0=block[:, 0:fold], in1=block[:, HEAD_DIM - fold :], op=ALU.add
-                )
-            return [block[:, c] for c in range(HEAD_DIM - fold)]
-
         def add_up(out_ap, planes, between=None):
             for n, plane in enumerate(planes):
                 if between and n == len(planes) // 2:
@@ -254,9 +244,9 @@ def tile_relation_kernel(tc, x, w_qkv_words, w_qkv_scales, out):
         scores = {}
 
         def sum_scores(t, between):
-            planes = product_blocks[t]
+            block = product_blocks[t]
             bank = score_ps.tile([P, P], F32, tag="score", name="score")
-            add_up(bank[:], [plane.rearrange("p k x -> p (k x)") for plane in planes], between)
+            add_up(bank[:], [block[:, c].rearrange("p k x -> p (k x)") for c in range(HEAD_DIM)], between)
             scores[t] = turned.tile([P, P], F32, tag="turned", name="turned_score")
             return lambda: nc.scalar.copy(out=scores[t][:], in_=bank[:])
 
@@ -526,7 +516,7 @@ def tile_relation_kernel(tc, x, w_qkv_words, w_qkv_scales, out):
                         subtract_top(n)
 
                 if t < TILES:
-                    block = products(t, subtract)
+                    product_blocks[t] = products(t, subtract)
                 else:
                     subtract()
                 scalar_rows(1, t)
@@ -534,8 +524,6 @@ def tile_relation_kernel(tc, x, w_qkv_words, w_qkv_scales, out):
                     exponential(n)
                     sum_weights(n)
                     normalise(n, nc.vector if n == UNITS - 1 else nc.gpsimd)
-                if t < TILES:
-                    product_blocks[t] = fold_products(block, t)
                 vector_pixel(t)
                 copies = []
                 if 1 <= t < TILES + 1:

@@ -34,9 +34,13 @@ TILES = UNITS * OFFSETS // SLOTS
 
 FLOPS = 2 * 3 * DEPTH * CHANNELS_IN * PIXELS + 2 * 2 * PIXELS * HEADS * OFFSETS * HEAD_DIM
 
-SHARES = ("SSSV", "SSGV", "SSSV", "SSGV", "SSSV", "SSGV", "SSGV", "SVVV")
+SHARES = ("SSSV", "SSGV", "SSSV", "SSGV", "SSSV", "SSGV", "SSVV", "SSVV")
 DIRECT = 6
+FOLD_QK = 4
+FOLD_FROM = 4
 FOLD_AV = OFFSETS // 2
+ROW_ORDER = (1, 2, 0, 3)
+WINDOW_PARTS = (((2, 4), (4, 5), (0, 2)), ((3, 5), (1, 3), (0, 1)), ((0, 2), (2, 5)), ((0, 1), (1, 5)))
 GROUP = 2
 RING = 4
 
@@ -124,6 +128,11 @@ def tile_relation_kernel(tc, x, w_qkv_words, w_qkv_scales, out):
         v_tiles = {}
         q_banks = {}
 
+        def halo_tile(tiles, half, part):
+            if (half, part) not in tiles:
+                tiles[half, part] = halo.tile([P, PART, HALO, P], F32, tag="halo", align_bytes=64, name="halo_rows")
+            return tiles[half, part]
+
         def convolve(pool, tag, words, scales, first, places):
             bank = pool.tile([P, PATCH, P], F32, tag=tag, name=tag)
             cols = slice(first, first + P)
@@ -144,12 +153,8 @@ def tile_relation_kernel(tc, x, w_qkv_words, w_qkv_scales, out):
             q_banks[half, a] = convolve(q_ps, "q", qk_words, qk_scales, half * P, places)
 
         def load_k(half, u, vs):
-            if (half, u // PART) not in k_tiles:
-                k_tiles[half, u // PART] = halo.tile(
-                    [P, PART, HALO, P], F32, tag="halo", align_bytes=64, name="k_tile"
-                )
             bank = convolve(stage_ps, "stage", qk_words, qk_scales, DEPTH + half * P, [(u, v) for v in vs])
-            row = k_tiles[half, u // PART][:, u % PART]
+            row = halo_tile(k_tiles, half, u // PART)[:, u % PART]
             if vs[3] - vs[0] == 3:
                 to = row[:, vs[0] : vs[0] + PATCH, :]
                 what = bank[:]
@@ -159,28 +164,24 @@ def tile_relation_kernel(tc, x, w_qkv_words, w_qkv_scales, out):
             return lambda: nc.scalar.copy(out=to, in_=what)
 
         def load_v(half, u, v0):
-            if (half, u // PART) not in v_tiles:
-                v_tiles[half, u // PART] = halo.tile(
-                    [P, PART, HALO, P], F32, tag="halo", align_bytes=64, name="v_tile"
-                )
             bank = convolve(
                 stage_ps, "stage", w_words, w_scales, 2 * DEPTH + half * P, [(u, v0 + j) for j in range(PATCH)]
             )
-            to = v_tiles[half, u // PART][:, u % PART, v0 : v0 + PATCH, :]
+            to = halo_tile(v_tiles, half, u // PART)[:, u % PART, v0 : v0 + PATCH, :]
             return lambda: nc.scalar.copy(out=to, in_=bank[:])
 
         def share_rows(tiles, half, up):
-            upper, lower = tiles[half, 0], tiles[half, 1]
+            upper, lower = halo_tile(tiles, half, 0), halo_tile(tiles, half, 1)
             if up:
                 to, source, shift = upper[:, 0:REACH], lower[:, 0:REACH], GRID
             else:
                 to, source, shift = lower[:, PART - REACH :], upper[:, PART - REACH :], -GRID
             per_grid = GRID * GRID
-            for first in (0, per_grid):
+            for first, queue in ((0, nc.sync), (per_grid, nc.scalar)):
                 a, b = (first + GRID, first + per_grid) if up else (first, first + per_grid - GRID)
                 edge = first if up else first + per_grid - GRID
-                nc.sync.dma_start(out=to[a:b], in_=source[a - shift : b - shift])
-                nc.sync.dma_start(out=to[edge : edge + GRID], in_=zeros[edge : edge + GRID].unsqueeze(1).to_broadcast([GRID, REACH, HALO, P]))
+                queue.dma_start(out=to[a:b], in_=source[a - shift : b - shift])
+                queue.dma_start(out=to[edge : edge + GRID], in_=zeros[edge : edge + GRID].unsqueeze(1).to_broadcast([GRID, REACH, HALO, P]))
 
         pending = []
 
@@ -199,11 +200,9 @@ def tile_relation_kernel(tc, x, w_qkv_words, w_qkv_scales, out):
                 load[1](*load[2:])
 
         def parts_of(half, a):
-            if half == 0 and a == 0:
-                return ((2, 4), (4, 5), (0, 2))
-            return ((0, PART - a), (PART - a, WINDOW))
+            return WINDOW_PARTS[a]
 
-        unit_of = [(half, a) for half in range(HALVES) for a in range(PATCH)]
+        unit_of = [(half, a) for half in range(HALVES) for a in ROW_ORDER]
         offsets = []
         for n, (half, a) in enumerate(unit_of):
             for d0, d1 in parts_of(half, a):
@@ -227,6 +226,17 @@ def tile_relation_kernel(tc, x, w_qkv_words, w_qkv_scales, out):
                 )
             return block
 
+        def fold_of(t):
+            return FOLD_QK if t >= FOLD_FROM else 0
+
+        def fold_products(t):
+            fold = fold_of(t)
+            if fold:
+                block = product_blocks[t]
+                nc.gpsimd.tensor_tensor(
+                    out=block[:, 0:fold], in0=block[:, 0:fold], in1=block[:, HEAD_DIM - fold :], op=ALU.add
+                )
+
         def add_up(out_ap, planes, between=None):
             for n, plane in enumerate(planes):
                 if between and n == len(planes) // 2:
@@ -246,7 +256,7 @@ def tile_relation_kernel(tc, x, w_qkv_words, w_qkv_scales, out):
         def sum_scores(t, between):
             block = product_blocks[t]
             bank = score_ps.tile([P, P], F32, tag="score", name="score")
-            add_up(bank[:], [block[:, c].rearrange("p k x -> p (k x)") for c in range(HEAD_DIM)], between)
+            add_up(bank[:], [block[:, c].rearrange("p k x -> p (k x)") for c in range(HEAD_DIM - fold_of(t))], between)
             scores[t] = turned.tile([P, P], F32, tag="turned", name="turned_score")
             return lambda: nc.scalar.copy(out=scores[t][:], in_=bank[:])
 
@@ -269,31 +279,27 @@ def tile_relation_kernel(tc, x, w_qkv_words, w_qkv_scales, out):
             nc.vector.tensor_reduce(
                 out=top, in_=raw.rearrange("p (o x) -> p x o", x=STRIP), axis=AX.X, op=ALU.max
             )
-            atts[n] = few.tile([P, PATCH, OFFSETS, HH], F32, tag="att", align_bytes=64, name="att")
+            atts[n] = few.tile([P, PATCH, HH, OFFSETS], F32, tag="att", align_bytes=64, name="att")
             nc.vector.tensor_sub(
-                out=atts[n][:].rearrange("p b o h -> p o b h"),
-                in0=raw.rearrange("p (o b h) -> p o b h", b=PATCH, h=HH),
-                in1=top.rearrange("p (b h) -> p b h", h=HH).unsqueeze(1).to_broadcast([P, OFFSETS, PATCH, HH]),
+                out=atts[n][:].rearrange("p b h o -> p (b h) o"),
+                in0=raw.rearrange("p (o x) -> p x o", x=STRIP),
+                in1=top.unsqueeze(2).to_broadcast([P, STRIP, OFFSETS]),
             )
 
         def exponential(n):
-            flat = atts[n][:].rearrange("p b o h -> p (b o h)")
+            flat = atts[n][:].rearrange("p b h o -> p (b h o)")
             nc.scalar.activation(out=flat, in_=flat, func=ACT.Exp)
 
         def sum_weights(n):
-            total = tops[n][:, 1].rearrange("p (b h) -> p b h", h=HH)
             nc.vector.tensor_reduce(
-                out=total, in_=atts[n][:].rearrange("p b o h -> p b h o"), axis=AX.X, op=ALU.add
+                out=tops[n][:, 1], in_=atts[n][:].rearrange("p b h o -> p (b h) o"), axis=AX.X, op=ALU.add
             )
             nc.vector.reciprocal(out=tops[n][:, 1], in_=tops[n][:, 1])
 
         def normalise(n, engine):
-            factor = tops[n][:, 1].rearrange("p (b h) -> p b h", h=HH)
+            weights = atts[n][:].rearrange("p b h o -> p (b h) o")
             engine.tensor_tensor(
-                out=atts[n][:],
-                in0=atts[n][:],
-                in1=factor.unsqueeze(2).to_broadcast([P, PATCH, OFFSETS, HH]),
-                op=ALU.mult,
+                out=weights, in0=weights, in1=tops[n][:, 1].unsqueeze(2).to_broadcast([P, STRIP, OFFSETS]), op=ALU.mult
             )
 
         def slot_of(n, di, dj):
@@ -314,7 +320,7 @@ def tile_relation_kernel(tc, x, w_qkv_words, w_qkv_scales, out):
                 for h in range(HH):
                     ch = slice(h * HEAD_DIM, (h + 1) * HEAD_DIM)
                     nc.scalar.activation(
-                        out=block[:, off, ch], in_=place[:, dj, ch], func=ACT.Copy, scale=atts[n][:, b, off, h : h + 1]
+                        out=block[:, off, ch], in_=place[:, dj, ch], func=ACT.Copy, scale=atts[n][:, b, h, off : off + 1]
                     )
 
         per_pixel = OFFSETS * HH
@@ -328,7 +334,7 @@ def tile_relation_kernel(tc, x, w_qkv_words, w_qkv_scales, out):
 
         def turn_weights(n):
             bank = score_ps.tile([P, 2, P], F32, tag="score", name="turn")
-            flat = atts[n][:].rearrange("p b o h -> p (b o h)")
+            flat = atts[n][:].rearrange("p b h o -> p (b h o)")
             starts = pieces(n)
             for j, first in enumerate(starts):
                 nc.tensor.transpose(out=bank[:, j, :], in_=flat[:, first : first + P], identity=ident[:])
@@ -351,7 +357,7 @@ def tile_relation_kernel(tc, x, w_qkv_words, w_qkv_scales, out):
             half, a = unit_of[n]
             if n < DIRECT and SHARES[n][b] == "V":
                 first = b * per_pixel - pieces(n)[0]
-                weights = weight_banks[n][:, first : first + per_pixel].rearrange("p (o h) -> p o h", h=HH)
+                weights = weight_banks[n][:, first : first + per_pixel].rearrange("p (h o) -> p h o", h=HH)
             else:
                 weights = atts[n][:, b]
             slot = 0
@@ -365,8 +371,8 @@ def tile_relation_kernel(tc, x, w_qkv_words, w_qkv_scales, out):
                     in0=v_tiles[half, u // PART][:, u % PART : u % PART + d1 - d0, b : b + WINDOW, :].rearrange(
                         "p u v (h c) -> p v u h c", h=HH
                     ),
-                    in1=weights[:, slots, :]
-                    .rearrange("p (j i) h -> p j i h", j=WINDOW)
+                    in1=weights[:, :, slots]
+                    .rearrange("p h (j i) -> p j i h", j=WINDOW)
                     .unsqueeze(4)
                     .to_broadcast([P, WINDOW, d1 - d0, HH, HEAD_DIM]),
                     op=ALU.mult,
@@ -469,13 +475,14 @@ def tile_relation_kernel(tc, x, w_qkv_words, w_qkv_scales, out):
             pending.extend([(since,) + load for load in loads])
 
         def ask_halo(load, half, order, tiles, since=0):
-            for u, vs in order:
+            for n, (u, vs) in enumerate(order):
                 ask((load, half, u, vs), since=since)
-            for up in (True, False):
-                ask((share_rows, tiles, half, up))
+                if n == len(order) // 2 - 1:
+                    ask((share_rows, tiles, half, True), since=since)
+            ask((share_rows, tiles, half, False), since=since)
 
-        own_rows = range(REACH, REACH + PATCH)
-        ask_halo(load_k, 0, [(u, vs) for r in (2, 4) for vs in (own, beside) for u in (r, r + 1)], k_tiles)
+        own_rows = (4, 5, 2, 3)
+        ask_halo(load_k, 0, [(u, vs) for r in (4, 2) for vs in (own, beside) for u in (r, r + 1)], k_tiles)
         ask_halo(load_v, 0, [(u, v0) for u in own_rows for v0 in (0, PART)], v_tiles)
         ask_halo(load_k, 1, [(u, vs) for u in own_rows for vs in (left, right)], k_tiles)
         ask_halo(load_v, 1, [(u, v0) for u in own_rows for v0 in (0, PART)], v_tiles, since=first_tile[PATCH] + 2)
@@ -487,7 +494,7 @@ def tile_relation_kernel(tc, x, w_qkv_words, w_qkv_scales, out):
             mybir.EngineType.Pool,
         }
         with tc.manual_schedule(engines=pinned):
-            load_q(0, 0)
+            load_q(*unit_of[0])
             some_loads(GROUP, 0)
             some_loads(GROUP, 0)
             t = 0
@@ -517,6 +524,7 @@ def tile_relation_kernel(tc, x, w_qkv_words, w_qkv_scales, out):
 
                 if t < TILES:
                     product_blocks[t] = products(t, subtract)
+                    fold_products(t)
                 else:
                     subtract()
                 scalar_rows(1, t)
@@ -533,13 +541,18 @@ def tile_relation_kernel(tc, x, w_qkv_words, w_qkv_scales, out):
                 for n in units_at(3):
                     if n < DIRECT:
                         copies.append(turn_weights(n))
-                scalar_rows(1, t)
+                if t < TILES:
+                    scalar_rows(1, t)
                 for copy in copies:
                     copy()
+                if t >= TILES:
+                    for n in units_at(1):
+                        return_scores(n)
                 for turn in range(2):
                     pixel_sum(t, stored)
                     scalar_rows(2 if t >= TILES else 1 + turn % 2, t)
                 gpsimd_pixel(t)
-                for n in units_at(1):
-                    return_scores(n)
+                if t < TILES:
+                    for n in units_at(1):
+                        return_scores(n)
                 t += 1

@@ -34,10 +34,9 @@ TILES = UNITS * OFFSETS // SLOTS
 
 FLOPS = 2 * 3 * DEPTH * CHANNELS_IN * PIXELS + 2 * 2 * PIXELS * HEADS * OFFSETS * HEAD_DIM
 
-SHARES = ("SSSV", "SSGV", "SSSV", "SSGV", "SSSV", "SSGV", "SSVV", "SSVV")
+SHARES = ("SSSV", "SSSV", "SSSV", "SSSV", "SSSV", "SSSV", "SSVV", "SSVV")
 DIRECT = 6
-FOLD_QK = 4
-FOLD_FROM = 4
+FOLD_QK = 12
 FOLD_AV = OFFSETS // 2
 ROW_ORDER = (1, 2, 0, 3)
 WINDOW_PARTS = (((2, 4), (4, 5), (0, 2)), ((3, 5), (1, 3), (0, 1)), ((0, 2), (2, 5)), ((0, 1), (1, 5)))
@@ -107,11 +106,14 @@ def tile_relation_kernel(tc, x, w_qkv_words, w_qkv_scales, out):
         by_spot = x_sb.rearrange(
             "p t (g ry qx rx) -> p ry rx g qx t", g=IMAGES * GRID, ry=PATCH, qx=GRID, rx=PATCH
         )
-        for ry in range(PATCH):
-            copy = nc.scalar.copy if ry >= PATCH // 2 else nc.vector.tensor_copy
-            copy(
-                out=grouped[:, ry].rearrange("p rx (g qx) t -> p rx g qx t", qx=GRID), in_=by_spot[:, ry]
-            )
+        for n in range(IMAGES):
+            strips = slice(n * GRID, (n + 1) * GRID)
+            for ry in range(PATCH):
+                copy = nc.scalar.copy if ry >= PATCH // 2 else nc.vector.tensor_copy
+                copy(
+                    out=grouped[:, ry].rearrange("p rx (g qx) t -> p rx g qx t", qx=GRID)[:, :, strips],
+                    in_=by_spot[:, ry, :, strips],
+                )
         for ry in range(PATCH):
             mid = slice(REACH, REACH + PATCH)
             nc.vector.quantize_mx(
@@ -226,16 +228,10 @@ def tile_relation_kernel(tc, x, w_qkv_words, w_qkv_scales, out):
                 )
             return block
 
-        def fold_of(t):
-            return FOLD_QK if t >= FOLD_FROM else 0
-
-        def fold_products(t):
-            fold = fold_of(t)
-            if fold:
-                block = product_blocks[t]
-                nc.gpsimd.tensor_tensor(
-                    out=block[:, 0:fold], in0=block[:, 0:fold], in1=block[:, HEAD_DIM - fold :], op=ALU.add
-                )
+        def fold_products(block):
+            nc.gpsimd.tensor_tensor(
+                out=block[:, 0:FOLD_QK], in0=block[:, 0:FOLD_QK], in1=block[:, HEAD_DIM - FOLD_QK :], op=ALU.add
+            )
 
         def add_up(out_ap, planes, between=None):
             for n, plane in enumerate(planes):
@@ -256,7 +252,7 @@ def tile_relation_kernel(tc, x, w_qkv_words, w_qkv_scales, out):
         def sum_scores(t, between):
             block = product_blocks[t]
             bank = score_ps.tile([P, P], F32, tag="score", name="score")
-            add_up(bank[:], [block[:, c].rearrange("p k x -> p (k x)") for c in range(HEAD_DIM - fold_of(t))], between)
+            add_up(bank[:], [block[:, c].rearrange("p k x -> p (k x)") for c in range(HEAD_DIM - FOLD_QK)], between)
             scores[t] = turned.tile([P, P], F32, tag="turned", name="turned_score")
             return lambda: nc.scalar.copy(out=scores[t][:], in_=bank[:])
 
@@ -484,7 +480,7 @@ def tile_relation_kernel(tc, x, w_qkv_words, w_qkv_scales, out):
         own_rows = (4, 5, 2, 3)
         ask_halo(load_k, 0, [(u, vs) for r in (4, 2) for vs in (own, beside) for u in (r, r + 1)], k_tiles)
         ask_halo(load_v, 0, [(u, v0) for u in own_rows for v0 in (0, PART)], v_tiles)
-        ask_halo(load_k, 1, [(u, vs) for u in own_rows for vs in (left, right)], k_tiles)
+        ask_halo(load_k, 1, [(u, vs) for u in own_rows for vs in (left, right)], k_tiles, since=5)
         ask_halo(load_v, 1, [(u, v0) for u in own_rows for v0 in (0, PART)], v_tiles, since=first_tile[PATCH] + 2)
 
         pinned = {
@@ -524,7 +520,7 @@ def tile_relation_kernel(tc, x, w_qkv_words, w_qkv_scales, out):
 
                 if t < TILES:
                     product_blocks[t] = products(t, subtract)
-                    fold_products(t)
+                    fold_products(product_blocks[t])
                 else:
                     subtract()
                 scalar_rows(1, t)

@@ -34,8 +34,8 @@ TILES = UNITS * OFFSETS // SLOTS
 
 FLOPS = 2 * 3 * DEPTH * CHANNELS_IN * PIXELS + 2 * 2 * PIXELS * HEADS * OFFSETS * HEAD_DIM
 
-SHARES = ("SSSV", "SSSV", "SSSV", "SSSV", "SSSV", "SSSV", "SSVV", "SSVV")
-DIRECT = 6
+SHARES = ("SSSV", "SSSV", "SSSV", "SSSV", "SSSV", "SSSV", "SSGV", "SSVV")
+DIRECT = 7
 FOLD_QK = 12
 FOLD_AV = OFFSETS // 2
 ROW_ORDER = (1, 2, 0, 3)
@@ -163,14 +163,14 @@ def tile_relation_kernel(tc, x, w_qkv_words, w_qkv_scales, out):
             else:
                 to = row.rearrange("p (g w) x -> p g w x", w=2)[:, 0:4:3]
                 what = bank[:].rearrange("p (g w) x -> p g w x", w=2)
-            return lambda: nc.scalar.copy(out=to, in_=what)
+            return lambda copy: copy(out=to, in_=what)
 
         def load_v(half, u, v0):
             bank = convolve(
                 stage_ps, "stage", w_words, w_scales, 2 * DEPTH + half * P, [(u, v0 + j) for j in range(PATCH)]
             )
             to = halo_tile(v_tiles, half, u // PART)[:, u % PART, v0 : v0 + PATCH, :]
-            return lambda: nc.scalar.copy(out=to, in_=bank[:])
+            return lambda copy: copy(out=to, in_=bank[:])
 
         def share_rows(tiles, half, up):
             upper, lower = halo_tile(tiles, half, 0), halo_tile(tiles, half, 1)
@@ -179,7 +179,8 @@ def tile_relation_kernel(tc, x, w_qkv_words, w_qkv_scales, out):
             else:
                 to, source, shift = lower[:, PART - REACH :], upper[:, PART - REACH :], -GRID
             per_grid = GRID * GRID
-            for first, queue in ((0, nc.sync), (per_grid, nc.scalar)):
+            second = nc.scalar if half == 0 and tiles is k_tiles else nc.sync
+            for first, queue in ((0, nc.sync), (per_grid, second)):
                 a, b = (first + GRID, first + per_grid) if up else (first, first + per_grid - GRID)
                 edge = first if up else first + per_grid - GRID
                 queue.dma_start(out=to[a:b], in_=source[a - shift : b - shift])
@@ -187,45 +188,75 @@ def tile_relation_kernel(tc, x, w_qkv_words, w_qkv_scales, out):
 
         pending = []
 
-        def some_loads(count, t):
-            copies = []
-            for _ in range(count):
-                if pending and pending[0][0] <= t and pending[0][1] != share_rows:
-                    load = pending[0]
-                    pending.remove(load)
-                    copies.append(load[1](*load[2:]))
-            for copy in copies:
-                copy()
+        for_vector = []
+
+        def share_loaded():
             while pending and pending[0][1] == share_rows:
                 load = pending[0]
                 pending.remove(load)
                 load[1](*load[2:])
 
+        def vector_copies():
+            while for_vector:
+                for_vector[0](nc.vector.tensor_copy)
+                for_vector.remove(for_vector[0])
+            share_loaded()
+
+        def some_loads(count, t, second=False):
+            copies = []
+            for _ in range(count):
+                if pending and pending[0][0] <= t and pending[0][1] != share_rows:
+                    load = pending[0]
+                    if load[2] == 1 and second:
+                        return
+                    pending.remove(load)
+                    copies.append((load[2], load[1](*load[2:])))
+            for half, copy in copies:
+                if half == 1:
+                    for_vector.append(copy)
+                else:
+                    copy(nc.scalar.copy)
+            if not for_vector:
+                share_loaded()
+
         def parts_of(half, a):
             return WINDOW_PARTS[a]
 
         unit_of = [(half, a) for half in range(HALVES) for a in ROW_ORDER]
-        offsets = []
+        runs = []
         for n, (half, a) in enumerate(unit_of):
+            slot = OFFSETS * n
             for d0, d1 in parts_of(half, a):
-                offsets.extend([(n, di, dj) for dj in range(WINDOW) for di in range(d0, d1)])
+                for dj in range(WINDOW):
+                    runs.append((slot, n, dj, d0, d1))
+                    slot += d1 - d0
 
         def products(t, between):
             block = prod.tile([P, HEAD_DIM, SLOTS, STRIP], F32, tag="prod", align_bytes=64, name="block")
-            for slot in range(SLOTS):
-                if slot == SLOTS // 2:
-                    between()
-                n, di, dj = offsets[SLOTS * t + slot]
+            middle = SLOTS * t + SLOTS // 2
+            for slot, n, dj, d0, d1 in runs:
+                first = max(slot, SLOTS * t)
+                last = min(slot + d1 - d0, SLOTS * (t + 1))
+                if first >= last:
+                    continue
                 half, a = unit_of[n]
-                u = a + di
+                count = last - first
+                u = a + d0 + first - slot
                 nc.vector.tensor_tensor(
-                    out=block[:, :, slot, :].rearrange("p c (b h) -> p c b h", h=HH),
-                    in0=k_tiles[half, u // PART][:, u % PART, dj : dj + PATCH, :].rearrange(
-                        "p b (c h) -> p c b h", h=HH
+                    out=block[:, :, first - SLOTS * t : last - SLOTS * t, :].rearrange(
+                        "p c k (b h) -> p k b c h", h=HH
                     ),
-                    in1=q_banks[half, a][:].rearrange("p b (c h) -> p c b h", h=HH),
+                    in0=k_tiles[half, u // PART][:, u % PART : u % PART + count, dj : dj + PATCH, :].rearrange(
+                        "p k b (c h) -> p k b c h", h=HH
+                    ),
+                    in1=q_banks[half, a][:]
+                    .rearrange("p b (c h) -> p b c h", h=HH)
+                    .unsqueeze(1)
+                    .to_broadcast([P, count, PATCH, HEAD_DIM, HH]),
                     op=ALU.mult,
                 )
+                if first < middle <= last:
+                    between()
             return block
 
         def fold_products(block):
@@ -252,7 +283,7 @@ def tile_relation_kernel(tc, x, w_qkv_words, w_qkv_scales, out):
         def sum_scores(t, between):
             block = product_blocks[t]
             bank = score_ps.tile([P, P], F32, tag="score", name="score")
-            add_up(bank[:], [block[:, c].rearrange("p k x -> p (k x)") for c in range(HEAD_DIM - FOLD_QK)], between)
+            add_up(bank[:], [block[:, c].rearrange("p k x -> p (k x)") for c in range(HEAD_DIM - (FOLD_QK if t < TILES - 1 else 0))], between)
             scores[t] = turned.tile([P, P], F32, tag="turned", name="turned_score")
             return lambda: nc.scalar.copy(out=scores[t][:], in_=bank[:])
 
@@ -388,7 +419,7 @@ def tile_relation_kernel(tc, x, w_qkv_words, w_qkv_scales, out):
         def store(n):
             half, a = unit_of[n]
             result = ends.tile([P, IMAGES, GRID, GRID, PATCH], F32, tag="result", name="result")
-            nc.scalar.copy(
+            nc.vector.tensor_copy(
                 out=result[:].rearrange("c n g x b -> c (n g) x b"),
                 in_=banks[n][:].rearrange("c b (g x) -> c g x b", x=GRID),
             )
@@ -500,9 +531,7 @@ def tile_relation_kernel(tc, x, w_qkv_words, w_qkv_scales, out):
                     if t == (1 if n == 1 else last_tile[n - 2] + 2):
                         load_q(*unit_of[n])
                 some_loads(GROUP, t)
-                if finished.get(stored, 0) == PATCH:
-                    store(stored)
-                    stored += 1
+                ready = finished.get(stored, 0) == PATCH
 
                 def units_at(steps):
                     return [n for n in range(UNITS) if last_tile[n] + steps == t]
@@ -520,9 +549,14 @@ def tile_relation_kernel(tc, x, w_qkv_words, w_qkv_scales, out):
 
                 if t < TILES:
                     product_blocks[t] = products(t, subtract)
-                    fold_products(product_blocks[t])
+                    if t < TILES - 1:
+                        fold_products(product_blocks[t])
                 else:
                     subtract()
+                vector_copies()
+                if ready:
+                    store(stored)
+                    stored += 1
                 scalar_rows(1, t)
                 for n in units_at(2):
                     exponential(n)
@@ -531,9 +565,9 @@ def tile_relation_kernel(tc, x, w_qkv_words, w_qkv_scales, out):
                 vector_pixel(t)
                 copies = []
                 if 1 <= t < TILES + 1:
-                    copies.append(sum_scores(t - 1, lambda: some_loads(GROUP, t)))
+                    copies.append(sum_scores(t - 1, lambda: some_loads(GROUP, t, True)))
                 else:
-                    some_loads(GROUP, t)
+                    some_loads(GROUP, t, True)
                 for n in units_at(3):
                     if n < DIRECT:
                         copies.append(turn_weights(n))

from contextlib import ExitStack

import concourse.mybir as mybir
from concourse.masks import make_identity

F32 = mybir.dt.float32
BF16 = mybir.dt.bfloat16
I32 = mybir.dt.int32
U8 = mybir.dt.uint8
FP8X4 = mybir.dt.float8_e4m3fn_x4
ALU = mybir.AluOpType
ACT = mybir.ActivationFunctionType
AX = mybir.AxisListType

P = 128
PACK = 4
IMAGES, CHANNELS_IN, SIDE = 2, 512, 32
PIXELS = IMAGES * SIDE * SIDE
HEADS, HEAD_DIM = 8, 32
DEPTH = HEADS * HEAD_DIM
HALVES = 2
HH = HEADS // HALVES
WINDOW = 5
OFFSETS = WINDOW * WINDOW
PATCH = 4
GRID = SIDE // PATCH
REACH = WINDOW // 2
HALO = PATCH + WINDOW - 1
PART = HALO // 2
UNITS = HALVES * PATCH
STRIP = PATCH * HH
SLOTS = P // STRIP
TILES = UNITS * OFFSETS // SLOTS

FLOPS = 2 * 3 * DEPTH * CHANNELS_IN * PIXELS + 2 * 2 * PIXELS * HEADS * OFFSETS * HEAD_DIM

SHARES = ("SSSV", "SSSV", "SSSV", "SSSV", "SSSV", "SSSV", "SSGV", "SSVV")
DIRECT = 7
FOLD_QK = 12
FOLD_AV = OFFSETS // 2
ROW_ORDER = (1, 2, 0, 3)
WINDOW_PARTS = (((2, 4), (4, 5), (0, 2)), ((3, 5), (1, 3), (0, 1)), ((0, 2), (2, 5)), ((0, 1), (1, 5)))
GROUP = 2
RING = 4


def tile_relation_kernel(tc, x, w_qkv_words, w_qkv_scales, out):
    nc = tc.nc
    with ExitStack() as whole:
        keep = whole.enter_context(tc.tile_pool(name="keep", bufs=1))
        halo = whole.enter_context(tc.tile_pool(name="halo", bufs=6))
        prod = whole.enter_context(tc.tile_pool(name="prod", bufs=3))
        weighted = whole.enter_context(tc.tile_pool(name="weighted", bufs=RING))
        few = whole.enter_context(tc.tile_pool(name="few", bufs=3))
        turned = whole.enter_context(tc.tile_pool(name="turned", bufs=6))
        ends = whole.enter_context(tc.tile_pool(name="ends", bufs=2))
        q_ps = whole.enter_context(tc.psum_pool(name="q_ps", bufs=2))
        stage_ps = whole.enter_context(tc.psum_pool(name="stage_ps", bufs=GROUP))
        score_ps = whole.enter_context(tc.psum_pool(name="score_ps", bufs=2))
        out_ps = whole.enter_context(tc.psum_pool(name="out_ps", bufs=1))
        weight_ps = whole.enter_context(tc.psum_pool(name="weight_ps", bufs=1))

        ident = keep.tile([P, P], F32)
        make_identity(nc, ident[:])
        w_words = keep.tile([P, 3 * DEPTH], I32, align_bytes=64)
        w_scales = keep.tile([P, 3 * DEPTH], U8, align_bytes=64)
        qk_words = keep.tile([P, 2 * DEPTH], I32, align_bytes=64)
        qk_scales = keep.tile([P, 2 * DEPTH], U8, align_bytes=64)
        x_words = keep.tile([P, PATCH, HALO, P], I32, align_bytes=64)
        x_scales = keep.tile([P, PATCH, HALO, P], U8, align_bytes=64)
        zeros = keep.tile([P, HALO, P], F32, align_bytes=64)
        nc.gpsimd.memset(zeros[:], 0.0)
        x_tile = halo.tile([P, PACK * PIXELS], BF16, tag="halo", align_bytes=64, name="x_tile")
        g_tile = halo.tile([P, PACK * PIXELS], BF16, tag="halo", align_bytes=64, name="g_tile")
        x_sb = x_tile[:].rearrange("p (t s) -> p t s", t=PACK)
        grouped = g_tile[:].rearrange("p (ry rx q t) -> p ry rx q t", ry=PATCH, rx=PATCH, t=PACK)

        def columns(tile, v0, v1, x0, x1):
            return tile[:, :, v0:v1, :].rearrange("p u v (r x) -> p u (v r) x", x=GRID)[:, :, :, x0:x1]

        per_image = SIDE * SIDE
        for n in range(IMAGES):
            nc.scalar.dma_start(
                out=x_sb[:, :, n * per_image : (n + 1) * per_image],
                in_=x[n].rearrange("(p t) h w -> p t (h w)", t=PACK),
            )
        nc.vector.memset(w_scales[:].bitcast(I32), 0)
        nc.sync.dma_start(out=w_words[:], in_=w_qkv_words[0].rearrange("p n t -> p (n t)").bitcast(I32))
        for quad in range(4):
            nc.sync.dma_start(
                out=w_scales[32 * quad : 32 * quad + 4, :].bitcast(I32),
                in_=w_qkv_scales[0, 4 * quad : 4 * quad + 4, :].bitcast(I32),
            )
        nc.vector.memset(x_scales[:].rearrange("p u v q -> p (u v q)").bitcast(I32), 0)
        nc.vector.memset(columns(x_words, 0, 2, 0, PATCH), 0)
        nc.vector.memset(columns(x_words, 6, 8, GRID - PATCH, GRID), 0)
        spark = keep.tile([P, 1], F32)
        nc.vector.memset(spark[:], 0.0)
        nc.scalar.activation(out=spark[:], in_=spark[:], func=ACT.Exp)
        for whole_w, part_w in ((w_words, qk_words), (w_scales, qk_scales)):
            nc.vector.tensor_copy(
                out=part_w[:].rearrange("p (g c h) -> p g c h", c=HEAD_DIM, h=HH),
                in_=whole_w[:, 0 : 2 * DEPTH].rearrange("p (g h c) -> p g c h", h=HH, c=HEAD_DIM),
            )

        by_spot = x_sb.rearrange(
            "p t (g ry qx rx) -> p ry rx g qx t", g=IMAGES * GRID, ry=PATCH, qx=GRID, rx=PATCH
        )
        for n in range(IMAGES):
            strips = slice(n * GRID, (n + 1) * GRID)
            for ry in range(PATCH):
                copy = nc.scalar.copy if ry >= PATCH // 2 else nc.vector.tensor_copy
                copy(
                    out=grouped[:, ry].rearrange("p rx (g qx) t -> p rx g qx t", qx=GRID)[:, :, strips],
                    in_=by_spot[:, ry, :, strips],
                )
        for ry in range(PATCH):
            mid = slice(REACH, REACH + PATCH)
            nc.vector.quantize_mx(
                out=x_words[:, ry, mid, :].rearrange("p v q -> p (v q)").bitcast(FP8X4),
                scales=x_scales[:, ry, mid, :].rearrange("p v q -> p (v q)"),
                in_=grouped[:, ry].rearrange("p rx q t -> p (rx q t)"),
            )

        for tile in (x_words, x_scales):
            nc.vector.tensor_copy(out=columns(tile, 0, 2, 1, GRID), in_=columns(tile, 4, 6, 0, GRID - 1))
            nc.vector.tensor_copy(out=columns(tile, 6, 8, 0, GRID - 1), in_=columns(tile, 2, 4, 1, GRID))

        k_tiles = {}
        v_tiles = {}
        q_banks = {}

        def halo_tile(tiles, half, part):
            if (half, part) not in tiles:
                tiles[half, part] = halo.tile([P, PART, HALO, P], F32, tag="halo", align_bytes=64, name="halo_rows")
            return tiles[half, part]

        def convolve(pool, tag, words, scales, first, places):
            bank = pool.tile([P, PATCH, P], F32, tag=tag, name=tag)
            cols = slice(first, first + P)
            for j, (u, v) in enumerate(places):
                nc.tensor.matmul_mx(
                    out=bank[:, j, :],
                    lhsT=x_words[:, u - REACH, v, :].bitcast(FP8X4),
                    lhsT_scale=x_scales[:, u - REACH, v, :],
                    rhs=words[:, cols].bitcast(FP8X4),
                    rhs_scale=scales[:, cols],
                    start=True,
                    stop=True,
                )
            return bank

        def load_q(half, a):
            places = [(REACH + a, REACH + b) for b in range(PATCH)]
            q_banks[half, a] = convolve(q_ps, "q", qk_words, qk_scales, half * P, places)

        def load_k(half, u, vs):
            bank = convolve(stage_ps, "stage", qk_words, qk_scales, DEPTH + half * P, [(u, v) for v in vs])
            row = halo_tile(k_tiles, half, u // PART)[:, u % PART]
            if vs[3] - vs[0] == 3:
                to = row[:, vs[0] : vs[0] + PATCH, :]
                what = bank[:]
            else:
                to = row.rearrange("p (g w) x -> p g w x", w=2)[:, 0:4:3]
                what = bank[:].rearrange("p (g w) x -> p g w x", w=2)
            return lambda copy: copy(out=to, in_=what)

        def load_v(half, u, v0):
            bank = convolve(
                stage_ps, "stage", w_words, w_scales, 2 * DEPTH + half * P, [(u, v0 + j) for j in range(PATCH)]
            )
            to = halo_tile(v_tiles, half, u // PART)[:, u % PART, v0 : v0 + PATCH, :]
            return lambda copy: copy(out=to, in_=bank[:])

        def share_rows(tiles, half, up):
            upper, lower = halo_tile(tiles, half, 0), halo_tile(tiles, half, 1)
            if up:
                to, source, shift = upper[:, 0:REACH], lower[:, 0:REACH], GRID
            else:
                to, source, shift = lower[:, PART - REACH :], upper[:, PART - REACH :], -GRID
            per_grid = GRID * GRID
            second = nc.scalar if half == 0 and tiles is k_tiles else nc.sync
            for first, queue in ((0, nc.sync), (per_grid, second)):
                a, b = (first + GRID, first + per_grid) if up else (first, first + per_grid - GRID)
                edge = first if up else first + per_grid - GRID
                queue.dma_start(out=to[a:b], in_=source[a - shift : b - shift])
                queue.dma_start(out=to[edge : edge + GRID], in_=zeros[edge : edge + GRID].unsqueeze(1).to_broadcast([GRID, REACH, HALO, P]))

        pending = []

        for_vector = []

        def share_loaded():
            while pending and pending[0][1] == share_rows:
                load = pending[0]
                pending.remove(load)
                load[1](*load[2:])

        def vector_copies():
            while for_vector:
                for_vector[0](nc.vector.tensor_copy)
                for_vector.remove(for_vector[0])
            share_loaded()

        def some_loads(count, t, second=False):
            copies = []
            for _ in range(count):
                if pending and pending[0][0] <= t and pending[0][1] != share_rows:
                    load = pending[0]
                    if load[2] == 1 and second:
                        return
                    pending.remove(load)
                    copies.append((load[2], load[1](*load[2:])))
            for half, copy in copies:
                if half == 1:
                    for_vector.append(copy)
                else:
                    copy(nc.scalar.copy)
            if not for_vector:
                share_loaded()

        def parts_of(half, a):
            return WINDOW_PARTS[a]

        unit_of = [(half, a) for half in range(HALVES) for a in ROW_ORDER]
        runs = []
        for n, (half, a) in enumerate(unit_of):
            slot = OFFSETS * n
            for d0, d1 in parts_of(half, a):
                for dj in range(WINDOW):
                    runs.append((slot, n, dj, d0, d1))
                    slot += d1 - d0

        def products(t, between):
            block = prod.tile([P, HEAD_DIM, SLOTS, STRIP], F32, tag="prod", align_bytes=64, name="block")
            middle = SLOTS * t + SLOTS // 2
            for slot, n, dj, d0, d1 in runs:
                first = max(slot, SLOTS * t)
                last = min(slot + d1 - d0, SLOTS * (t + 1))
                if first >= last:
                    continue
                half, a = unit_of[n]
                count = last - first
                u = a + d0 + first - slot
                nc.vector.tensor_tensor(
                    out=block[:, :, first - SLOTS * t : last - SLOTS * t, :].rearrange(
                        "p c k (b h) -> p k b c h", h=HH
                    ),
                    in0=k_tiles[half, u // PART][:, u % PART : u % PART + count, dj : dj + PATCH, :].rearrange(
                        "p k b (c h) -> p k b c h", h=HH
                    ),
                    in1=q_banks[half, a][:]
                    .rearrange("p b (c h) -> p b c h", h=HH)
                    .unsqueeze(1)
                    .to_broadcast([P, count, PATCH, HEAD_DIM, HH]),
                    op=ALU.mult,
                )
                if first < middle <= last:
                    between()
            return block

        def fold_products(block):
            nc.gpsimd.tensor_tensor(
                out=block[:, 0:FOLD_QK], in0=block[:, 0:FOLD_QK], in1=block[:, HEAD_DIM - FOLD_QK :], op=ALU.add
            )

        def add_up(out_ap, planes, between=None):
            for n, plane in enumerate(planes):
                if between and n == len(planes) // 2:
                    between()
                nc.tensor.matmul(
                    out=out_ap,
                    lhsT=plane,
                    rhs=ident[:],
                    is_transpose=True,
                    start=(n == 0),
                    stop=(n == len(planes) - 1),
                )

        product_blocks = {}
        scores = {}

        def sum_scores(t, between):
            block = product_blocks[t]
            bank = score_ps.tile([P, P], F32, tag="score", name="score")
            add_up(bank[:], [block[:, c].rearrange("p k x -> p (k x)") for c in range(HEAD_DIM - (FOLD_QK if t < TILES - 1 else 0))], between)
            scores[t] = turned.tile([P, P], F32, tag="turned", name="turned_score")
            return lambda: nc.scalar.copy(out=scores[t][:], in_=bank[:])

        last_tile = [(OFFSETS * (n + 1) - 1) // SLOTS for n in range(UNITS)]
        first_tile = [OFFSETS * n // SLOTS for n in range(UNITS)]
        raws = {}
        atts = {}
        tops = {}

        def return_scores(n):
            raws[n] = score_ps.tile([P, 4, P], F32, tag="score", name="raw")
            for j, t in enumerate(range(first_tile[n], last_tile[n] + 1)):
                nc.tensor.transpose(out=raws[n][:, j, :], in_=scores[t][:], identity=ident[:])

        def subtract_top(n):
            first = (OFFSETS * n - SLOTS * first_tile[n]) * STRIP
            raw = raws[n][:].rearrange("p t x -> p (t x)")[:, first : first + OFFSETS * STRIP]
            tops[n] = few.tile([P, 2, STRIP], F32, tag="top", name="top")
            top = tops[n][:, 0]
            nc.vector.tensor_reduce(
                out=top, in_=raw.rearrange("p (o x) -> p x o", x=STRIP), axis=AX.X, op=ALU.max
            )
            atts[n] = few.tile([P, PATCH, HH, OFFSETS], F32, tag="att", align_bytes=64, name="att")
            nc.vector.tensor_sub(
                out=atts[n][:].rearrange("p b h o -> p (b h) o"),
                in0=raw.rearrange("p (o x) -> p x o", x=STRIP),
                in1=top.unsqueeze(2).to_broadcast([P, STRIP, OFFSETS]),
            )

        def exponential(n):
            flat = atts[n][:].rearrange("p b h o -> p (b h o)")
            nc.scalar.activation(out=flat, in_=flat, func=ACT.Exp)

        def sum_weights(n):
            nc.vector.tensor_reduce(
                out=tops[n][:, 1], in_=atts[n][:].rearrange("p b h o -> p (b h) o"), axis=AX.X, op=ALU.add
            )
            nc.vector.reciprocal(out=tops[n][:, 1], in_=tops[n][:, 1])

        def normalise(n, engine):
            weights = atts[n][:].rearrange("p b h o -> p (b h) o")
            engine.tensor_tensor(
                out=weights, in0=weights, in1=tops[n][:, 1].unsqueeze(2).to_broadcast([P, STRIP, OFFSETS]), op=ALU.mult
            )

        def slot_of(n, di, dj):
            slot = 0
            for d0, d1 in parts_of(*unit_of[n]):
                if d0 <= di < d1:
                    return slot + dj * (d1 - d0) + di - d0
                slot += WINDOW * (d1 - d0)

        def places_of(half, u, b):
            return v_tiles[half, u // PART][:, u % PART, b : b + WINDOW, :]

        def scalar_row(n, b, di, block):
            half, a = unit_of[n]
            place = places_of(half, a + di, b)
            for dj in range(WINDOW):
                off = slot_of(n, di, dj)
                for h in range(HH):
                    ch = slice(h * HEAD_DIM, (h + 1) * HEAD_DIM)
                    nc.scalar.activation(
                        out=block[:, off, ch], in_=place[:, dj, ch], func=ACT.Copy, scale=atts[n][:, b, h, off : off + 1]
                    )

        per_pixel = OFFSETS * HH
        turned_weights = {}
        weight_banks = {}

        def pieces(n):
            first = sum(who != "V" for who in SHARES[n]) * per_pixel
            last = PATCH * per_pixel - P
            return (first, last) if first < last else (last,)

        def turn_weights(n):
            bank = score_ps.tile([P, 2, P], F32, tag="score", name="turn")
            flat = atts[n][:].rearrange("p b h o -> p (b h o)")
            starts = pieces(n)
            for j, first in enumerate(starts):
                nc.tensor.transpose(out=bank[:, j, :], in_=flat[:, first : first + P], identity=ident[:])
            turned_weights[n] = ends.tile([P, 2, P], F32, tag="weights", name="turned_w")
            return lambda: nc.scalar.copy(
                out=turned_weights[n][:, 0 : len(starts), :], in_=bank[:, 0 : len(starts), :]
            )

        def return_weights(n):
            weight_banks[n] = weight_ps.tile([P, 2 * P], F32, tag="weights", name="weights")
            starts = pieces(n)
            for j, first in enumerate(starts):
                nc.tensor.transpose(
                    out=weight_banks[n][:, first - starts[0] : first - starts[0] + P],
                    in_=turned_weights[n][:, j, :],
                    identity=ident[:],
                )

        def whole_pixel(n, b, block, engine):
            half, a = unit_of[n]
            if n < DIRECT and SHARES[n][b] == "V":
                first = b * per_pixel - pieces(n)[0]
                weights = weight_banks[n][:, first : first + per_pixel].rearrange("p (h o) -> p h o", h=HH)
            else:
                weights = atts[n][:, b]
            slot = 0
            for d0, d1 in parts_of(half, a):
                u = a + d0
                count = WINDOW * (d1 - d0)
                slots = slice(slot, slot + count)
                slot += count
                engine.tensor_tensor(
                    out=block[:, slots, :].rearrange("p (j i) (h c) -> p j i h c", j=WINDOW, h=HH),
                    in0=v_tiles[half, u // PART][:, u % PART : u % PART + d1 - d0, b : b + WINDOW, :].rearrange(
                        "p u v (h c) -> p v u h c", h=HH
                    ),
                    in1=weights[:, :, slots]
                    .rearrange("p h (j i) -> p j i h", j=WINDOW)
                    .unsqueeze(4)
                    .to_broadcast([P, WINDOW, d1 - d0, HH, HEAD_DIM]),
                    op=ALU.mult,
                )

        banks = {}
        finished = {}
        due = []

        def sum_pixel(n, b, block, planes):
            if n not in banks:
                banks[n] = out_ps.tile([P, PATCH, P], F32, tag="sums", name="sums")
                finished[n] = 0
            add_up(banks[n][:, b, :], [block[:, off] for off in range(planes)])
            finished[n] += 1

        def store(n):
            half, a = unit_of[n]
            result = ends.tile([P, IMAGES, GRID, GRID, PATCH], F32, tag="result", name="result")
            nc.vector.tensor_copy(
                out=result[:].rearrange("c n g x b -> c (n g) x b"),
                in_=banks[n][:].rearrange("c b (g x) -> c g x b", x=GRID),
            )
            to = out.rearrange("n (f c) (g a) w -> f a n c g w", f=HALVES, a=PATCH)[half, a]
            for image in range(IMAGES):
                nc.sync.dma_start(out=to[image], in_=result[:, image].rearrange("c g x b -> c g (x b)"))

        row_queue = []
        block_now = {}

        def new_block():
            return weighted.tile([P, OFFSETS, P], F32, tag="weighted", align_bytes=64, name="weighted_v")

        def full(who):
            mine = [item for item in due if SHARES[item[1]][item[2]] == who]
            return len(mine) >= 2 or len(due) + ("s" in block_now) >= RING

        def scalar_rows(count, t):
            for _ in range(min(count, len(row_queue))):
                n, b, di = row_queue[0]
                if di == 0 and full("S"):
                    return
                row_queue.remove(row_queue[0])
                if di == 0:
                    block_now["s"] = new_block()
                scalar_row(n, b, di, block_now["s"])
                if di == WINDOW - 1:
                    hand_over(t, n, b, block_now["s"], None)
                    block_now.clear()

        def hand_over(t, n, b, block, fold):
            if fold:
                fold.tensor_tensor(
                    out=block[:, 0:FOLD_AV], in0=block[:, 0:FOLD_AV], in1=block[:, OFFSETS - FOLD_AV :], op=ALU.add
                )
                due.append((t + 2, n, b, block, OFFSETS - FOLD_AV))
            else:
                due.append((t + 1, n, b, block, OFFSETS))

        def gpsimd_pixel(t):
            if pixel_queue and not full("G"):
                n, b = pixel_queue[0]
                pixel_queue.remove(pixel_queue[0])
                block = new_block()
                whole_pixel(n, b, block, nc.gpsimd)
                due.append((t + 2, n, b, block, OFFSETS))

        vector_queue = []
        pixel_queue = []

        def vector_pixel(t):
            if vector_queue and not full("V"):
                n, b = vector_queue[0]
                vector_queue.remove(vector_queue[0])
                block = new_block()
                whole_pixel(n, b, block, nc.vector)
                hand_over(t - 1, n, b, block, nc.gpsimd if n < DIRECT else nc.vector)

        def share_out(n):
            for b, who in enumerate(SHARES[n]):
                if who == "S":
                    row_queue.extend([(n, b, di) for di in range(WINDOW)])
                elif who == "G":
                    pixel_queue.append((n, b))
                elif n >= DIRECT:
                    vector_queue.append((n, b))

        def pixel_sum(t, unit):
            ready = [item for item in due if item[0] <= t and item[1] == unit]
            if ready:
                due.remove(ready[0])
                sum_pixel(*ready[0][1:])

        own = (2, 3, 4, 5)
        beside = (0, 1, 6, 7)
        left = (0, 1, 2, 3)
        right = (4, 5, 6, 7)

        def ask(*loads, since=0):
            pending.extend([(since,) + load for load in loads])

        def ask_halo(load, half, order, tiles, since=0):
            for n, (u, vs) in enumerate(order):
                ask((load, half, u, vs), since=since)
                if n == len(order) // 2 - 1:
                    ask((share_rows, tiles, half, True), since=since)
            ask((share_rows, tiles, half, False), since=since)

        own_rows = (4, 5, 2, 3)
        ask_halo(load_k, 0, [(u, vs) for r in (4, 2) for vs in (own, beside) for u in (r, r + 1)], k_tiles)
        ask_halo(load_v, 0, [(u, v0) for u in own_rows for v0 in (0, PART)], v_tiles)
        ask_halo(load_k, 1, [(u, vs) for u in own_rows for vs in (left, right)], k_tiles, since=5)
        ask_halo(load_v, 1, [(u, v0) for u in own_rows for v0 in (0, PART)], v_tiles, since=first_tile[PATCH] + 2)

        pinned = {
            mybir.EngineType.PE,
            mybir.EngineType.Activation,
            mybir.EngineType.DVE,
            mybir.EngineType.Pool,
        }
        with tc.manual_schedule(engines=pinned):
            load_q(*unit_of[0])
            some_loads(GROUP, 0)
            some_loads(GROUP, 0)
            t = 0
            stored = 0
            while stored < UNITS:
                for n in range(1, UNITS):
                    if t == (1 if n == 1 else last_tile[n - 2] + 2):
                        load_q(*unit_of[n])
                some_loads(GROUP, t)
                ready = finished.get(stored, 0) == PATCH

                def units_at(steps):
                    return [n for n in range(UNITS) if last_tile[n] + steps == t]

                for n in units_at(4):
                    if n < DIRECT:
                        return_weights(n)
                        vector_queue.extend([(n, b) for b in range(PATCH) if SHARES[n][b] == "V"])
                for n in units_at(3):
                    share_out(n)

                def subtract():
                    for n in units_at(2):
                        subtract_top(n)

                if t < TILES:
                    product_blocks[t] = products(t, subtract)
                    if t < TILES - 1:
                        fold_products(product_blocks[t])
                else:
                    subtract()
                vector_copies()
                if ready:
                    store(stored)
                    stored += 1
                scalar_rows(1, t)
                for n in units_at(2):
                    exponential(n)
                    sum_weights(n)
                    normalise(n, nc.vector if n == UNITS - 1 else nc.gpsimd)
                vector_pixel(t)
                copies = []
                if 1 <= t < TILES + 1:
                    copies.append(sum_scores(t - 1, lambda: some_loads(GROUP, t, True)))
                else:
                    some_loads(GROUP, t, True)
                for n in units_at(3):
                    if n < DIRECT:
                        copies.append(turn_weights(n))
                if t < TILES:
                    scalar_rows(1, t)
                for copy in copies:
                    copy()
                if t >= TILES:
                    for n in units_at(1):
                        return_scores(n)
                for turn in range(2):
                    pixel_sum(t, stored)
                    scalar_rows(2 if t >= TILES else 1 + turn % 2, t)
                gpsimd_pixel(t)
                if t < TILES:
                    for n in units_at(1):
                        return_scores(n)
                t += 1
